import numpy as np
import ml_dtypes


def mxq(x, axis, fmt="e4m3"):
    dtype, down = {"e4m3": (ml_dtypes.float8_e4m3fn, 7), "e5m2": (ml_dtypes.float8_e5m2, 14)}[fmt]
    v = np.moveaxis(np.asarray(x, np.float32).astype(ml_dtypes.bfloat16).astype(np.float64), axis, -1)
    blocks = v.reshape(v.shape[:-1] + (-1, 32))
    amax = np.abs(blocks).max(-1, keepdims=True)
    byte = np.maximum(np.where(amax > 0, np.frexp(amax)[1] - 1 + 127, 0) - down, 1)
    scale = np.exp2(byte - 127.0)
    codes = (blocks / scale).astype(np.float32).astype(dtype).astype(np.float64)
    return np.moveaxis((codes * scale).reshape(v.shape), -1, axis)


WIDE = False


def mx_kscale(k):
    if not WIDE:
        return np.ones(k)
    levels = np.array([10, -10, 5, -5, 0])
    a = np.random.permutation(np.resize(levels, k // 512 * 4)).reshape(k // 512, 4)
    idx = np.arange(k)
    return np.exp2(a[idx // 512, idx % 128 // 32])


BF16 = ml_dtypes.bfloat16


def bf(x):
    return np.asarray(x, np.float32).astype(BF16)


def f64(x):
    return np.asarray(x).astype(np.float64)


B, L, C, D, H, Q = 2, 1024, 1024, 1024, 8, 256
EPS = 1e-5


def layer_norm(v, w, b):
    mu = v.mean(-1, keepdims=True)
    var = v.var(-1, keepdims=True)
    return (v - mu) * (1.0 / np.sqrt(var + EPS)) * w + b


def setup_inputs():
    s = mx_kscale(C)
    mag = 10.0 ** (-2.5 * np.random.uniform(size=(B, L, 1)))
    x = (np.random.standard_normal((B, L, C)) + 0.5 * np.random.standard_normal((B, L, 1))) * mag
    return {"x": bf(x),
            "ln_k_w": bf((1.0 + 0.1 * np.random.standard_normal(C)) * s),
            "ln_k_b": bf(0.1 * np.random.standard_normal(C) * s),
            "Wk": bf(np.random.standard_normal((D, C)) / np.sqrt(C) / s[None, :]),
            "Wv": bf(np.random.standard_normal((D, C)) / np.sqrt(C) / s[None, :]),
            "bk": bf(0.1 * np.random.standard_normal(D)),
            "bv": bf(0.1 * np.random.standard_normal(D))}


def reference(x, ln_k_w, ln_k_b, Wk, Wv, bk, bv):
    xk = mxq(layer_norm(f64(x), f64(ln_k_w), f64(ln_k_b)), 2, "e4m3")
    k = (xk @ mxq(f64(Wk).T, 0, "e4m3")) + f64(bk)
    v = (xk @ mxq(f64(Wv).T, 0, "e4m3")) + f64(bv)
    return k, v

@@ -1,0 +1,230 @@
+from contextlib import ExitStack
+
+import concourse.mybir as mybir
+from concourse.masks import make_identity
+
+F32 = mybir.dt.float32
+BF16 = mybir.dt.bfloat16
+U32 = mybir.dt.uint32
+U8 = mybir.dt.uint8
+FP8X4 = mybir.dt.float8_e4m3fn_x4
+ALU = mybir.AluOpType
+ACT = mybir.ActivationFunctionType
+
+P = 128
+C = 1024
+TG = 4
+NGRP = 4
+EPS = 1e-5
+FLOPS = 2 * 2048 * 1024 * 2048
+
+N_V_STATS = (4, 1, 1, 1)
+PASS1_ON_G = False
+F_ON_S = ()
+
+
+def tile_attentionalpoolerwmasking_pa_kernel(tc, x, ln_k_w, ln_k_b, Wk, Wv, bk, bv, out_0, out_1):
+    nc = tc.nc
+    xf = x.flatten_outer_dims()
+    outs = (out_0.flatten_outer_dims(), out_1.flatten_outer_dims())
+    with ExitStack() as ctx:
+        const = ctx.enter_context(tc.tile_pool(name="const", bufs=1))
+        small = ctx.enter_context(tc.tile_pool(name="small", bufs=2))
+        xhp = ctx.enter_context(tc.tile_pool(name="xhp", bufs=8))
+        work = ctx.enter_context(tc.tile_pool(name="work", bufs=2))
+        grpp = ctx.enter_context(tc.tile_pool(name="grpp", bufs=4))
+        ostp = ctx.enter_context(tc.tile_pool(name="ostp", bufs=6))
+        pst = ctx.enter_context(tc.psum_pool(name="pst", bufs=4))
+        pso = ctx.enter_context(tc.psum_pool(name="pso", bufs=4))
+
+        vecs = const.tile([P, 256], BF16, name="vecs")
+        nc.vector.memset(vecs[:], 0.0)
+        nc.sync.dma_start(out=vecs[0:4, :], in_=ln_k_w.rearrange("(v q) -> v q", v=4))
+        nc.sync.dma_start(out=vecs[4:8, :], in_=ln_k_b.rearrange("(v q) -> v q", v=4))
+        one_t = const.tile([P, 1], F32, name="one_t")
+        nc.vector.memset(one_t[:], 1.0)
+        warm = const.tile([P, 1], F32, name="warm")
+        nc.scalar.activation(out=warm[:], in_=one_t[:], func=ACT.Sqrt)
+        ident = const.tile([P, P], F32, name="ident")
+        make_identity(nc, ident[:])
+
+        xts = []
+        wts = []
+        for gi in range(NGRP):
+            xts.append(const.tile([P, TG, C], BF16, name="xt%d" % gi))
+            wts.append(const.tile([P, 4, C], BF16, name="wt%d" % gi))
+        bias_bc = const.tile([P, 2048], BF16, name="bias_bc")
+
+        def load_x(gi):
+            nc.sync.dma_start(out=xts[gi][:], in_=xf[512 * gi : 512 * gi + 512, :].rearrange("(n p) c -> p n c", p=P))
+
+        def load_w(c):
+            src = Wk if c < 2 else Wv
+            r0 = 512 * (c % 2)
+            nc.sync.dma_start(out=wts[c][:], in_=src[r0 : r0 + 512, :].rearrange("(n p) c -> p n c", p=P))
+
+        for h in range(2):
+            nc.sync.dma_start(
+                out=xts[0][:, 2 * h : 2 * h + 2, :],
+                in_=xf[256 * h : 256 * h + 256, :].rearrange("(n p) c -> p n c", p=P),
+            )
+        load_w(0)
+        load_w(1)
+        nc.sync.dma_start(out=bias_bc[:, 0:1024], in_=bk.partition_broadcast(P))
+        nc.sync.dma_start(out=bias_bc[:, 1024:2048], in_=bv.partition_broadcast(P))
+        load_w(2)
+        load_w(3)
+        load_x(1)
+        load_x(2)
+        load_x(3)
+
+        vb = pst.tile([P, 512], F32, tag="tp", name="vb")
+        nc.tensor.transpose(vb[:, 0:P], vecs[:].bitcast(F32), ident[:])
+        wb = const.tile([P, 16], F32, name="wb")
+        nc.vector.tensor_copy(out=wb[:], in_=vb[:, 0:8].bitcast(BF16))
+
+        wq = const.tile([P, 2, 2048], U32, name="wq", align_bytes=64)
+        ws = const.tile([P, 2, 2048], U8, name="ws", align_bytes=64)
+
+        def prep_w(c):
+            gw = work.tile([P, 2, 2048], BF16, tag="gw", name="gw", align_bytes=64)
+            gw32 = gw[:].bitcast(F32).rearrange("p g (d u) -> p g d u", u=2)
+            for n in range(4):
+                bank = pst.tile([P, 512], F32, tag="tp", name="wbank")
+                w32 = wts[c][:, n, :].bitcast(F32)
+                for v in range(4):
+                    nc.tensor.transpose(bank[:, P * v : P * v + P], w32[:, P * v : P * v + P], ident[:])
+                nc.scalar.copy(
+                    out=gw32[:, :, P * n : P * n + P, :],
+                    in_=bank[:].rearrange("p (g u d) -> p g d u", g=2, u=2),
+                )
+            for g in range(2):
+                nc.vector.quantize_mx(
+                    out=wq[:, g, 512 * c : 512 * c + 512].bitcast(FP8X4),
+                    scales=ws[:, g, 512 * c : 512 * c + 512],
+                    in_=gw[:, g, :],
+                )
+
+        state = {}
+
+        def prep_stats(gi):
+            xt = xts[gi]
+            nv = N_V_STATS[gi]
+            ve = small.tile([P, TG], F32, tag="ve", name="ve")
+            std = small.tile([P, TG], F32, tag="std", name="std")
+            rstd = small.tile([P, TG], F32, tag="rstd", name="rstd")
+            nms = []
+            if nv > 0:
+                mv = small.tile([P, TG, 2], F32, tag="mv", name="mv")
+                nmv = small.tile([P, TG], F32, tag="nmv", name="nmv")
+                for n in range(nv):
+                    st = small.tile([P, 2, 6], F32, tag="st", name="st", bufs=4)
+                    for h in range(2):
+                        nc.vector.bn_stats(out=st[:, h, :], in_=xt[:, n, 512 * h : 512 * h + 512])
+                    nc.vector.bn_aggr(out=mv[:, n, :], in_=st[:].rearrange("p a b -> p (a b)"))
+                nc.vector.tensor_scalar(out=nmv[:, 0:nv], in0=mv[:, 0:nv, 0], scalar1=-1.0, scalar2=None, op0=ALU.mult)
+                nc.vector.tensor_scalar(out=ve[:, 0:nv], in0=mv[:, 0:nv, 1], scalar1=EPS, scalar2=None, op0=ALU.add)
+                for n in range(nv):
+                    nms.append(nmv[:, n : n + 1])
+            if nv < TG:
+                sm = small.tile([P, TG], F32, tag="sm", name="sm")
+                nmS = small.tile([P, TG], F32, tag="nmS", name="nmS")
+                sq = small.tile([P, TG], F32, tag="sq", name="sq")
+                for n in range(nv, TG):
+                    junk = work.tile([P, C], BF16, tag="junk", name="junk")
+                    nc.scalar.activation(out=junk[:], in_=xt[:, n, :], func=ACT.Identity, accum_out=sm[:, n : n + 1])
+                nc.scalar.mul(out=nmS[:, nv:TG], in_=sm[:, nv:TG], mul=-1.0 / C)
+                for n in range(nv, TG):
+                    junk = work.tile([P, C], BF16, tag="junk", name="junk")
+                    nc.scalar.activation(
+                        out=junk[:], in_=xt[:, n, :], func=ACT.Square, bias=nmS[:, n : n + 1], scale=1.0,
+                        accum_out=sq[:, n : n + 1],
+                    )
+                nc.vector.tensor_scalar(out=ve[:, nv:TG], in0=sq[:, nv:TG], scalar1=1.0 / C, scalar2=EPS, op0=ALU.mult, op1=ALU.add)
+                for n in range(nv, TG):
+                    nms.append(nmS[:, n : n + 1])
+            nc.scalar.activation(out=std[:], in_=ve[:], func=ACT.Sqrt)
+            nc.vector.reciprocal(out=rstd[:], in_=std[:])
+            xhs = []
+            eng = nc.gpsimd if PASS1_ON_G else nc.vector
+            for n in range(TG):
+                xh = xhp.tile([P, 8, P], F32, tag="xh", name="xh")
+                eng.tensor_scalar(
+                    out=xh[:].rearrange("p (v e) q -> p v e q", e=2),
+                    in0=xt[:, n, :].rearrange("p (v q e) -> p v e q", v=4, e=2),
+                    scalar1=nms[n],
+                    scalar2=rstd[:, n : n + 1],
+                    op0=ALU.add,
+                    op1=ALU.mult,
+                )
+                xhs.append(xh)
+            state[gi] = {"xh": xhs}
+
+        def prep_t(gi, g):
+            s = state[gi]
+            if g == 0:
+                s["plan"] = work.tile([P, 8, 512], BF16, tag="plan", name="plan")
+                s["xq"] = work.tile([P, 2, 512], U32, tag="xq", name="xq", align_bytes=64)
+                s["xs"] = work.tile([P, 2, 512], U8, tag="xs", name="xs", align_bytes=64)
+            plan = s["plan"]
+            for t in range(4):
+                pl = 4 * g + t
+                bank = pst.tile([P, 512], F32, tag="tp", name="xbank")
+                for n in range(TG):
+                    nc.tensor.transpose(bank[:, P * n : P * n + P], s["xh"][n][:, pl, :], ident[:])
+                nc.scalar.activation(
+                    out=plan[:, pl, :], in_=bank[:], func=ACT.Identity,
+                    scale=wb[:, pl : pl + 1], bias=wb[:, 8 + pl : 9 + pl],
+                )
+            grp = grpp.tile([P, 512, 4], BF16, tag="grp", name="grp", align_bytes=64)
+            nc.vector.tensor_copy(out=grp[:], in_=plan[:, 4 * g : 4 * g + 4, :].rearrange("p t r -> p r t"))
+            nc.vector.quantize_mx(
+                out=s["xq"][:, g, :].bitcast(FP8X4),
+                scales=s["xs"][:, g, :],
+                in_=grp[:].rearrange("p r t -> p (r t)"),
+            )
+
+        def mx_half(gi, half):
+            s = state[gi]
+            for n in range(TG):
+                ost = ostp.tile([P, 1024], F32, tag="ost", name="ost")
+                for j in range(2):
+                    ch = 2 * half + j
+                    acc = pso.tile([P, 512], F32, tag="acc", name="acc")
+                    for g in range(2):
+                        nc.tensor.matmul_mx(
+                            out=acc[:],
+                            lhsT=s["xq"][:, g, P * n : P * n + P].bitcast(FP8X4),
+                            lhsT_scale=s["xs"][:, g, P * n : P * n + P],
+                            rhs=wq[:, g, 512 * ch : 512 * ch + 512].bitcast(FP8X4),
+                            rhs_scale=ws[:, g, 512 * ch : 512 * ch + 512],
+                            start=(g == 0),
+                            stop=(g == 1),
+                        )
+                    o = ost[:, 512 * j : 512 * j + 512]
+                    b = bias_bc[:, 512 * ch : 512 * ch + 512]
+                    if (8 * half + 2 * n + j) in F_ON_S:
+                        nc.scalar.copy(out=o, in_=acc[:])
+                        nc.gpsimd.tensor_tensor(out=o, in0=o, in1=b, op=ALU.add)
+                    else:
+                        nc.vector.tensor_tensor(out=o, in0=acc[:], in1=b, op=ALU.add)
+                r0 = 512 * gi + P * n
+                nc.sync.dma_start(out=outs[half][r0 : r0 + P, :], in_=ost[:])
+
+        prep_stats(0)
+        prep_w(0)
+        prep_w(1)
+        prep_t(0, 0)
+        prep_t(0, 1)
+        for gi in range(NGRP):
+            if gi + 1 < NGRP:
+                prep_stats(gi + 1)
+            mx_half(gi, 0)
+            if gi == 0:
+                prep_w(2)
+                prep_w(3)
+            if gi + 1 < NGRP:
+                prep_t(gi + 1, 0)
+            mx_half(gi, 1)
+            if gi + 1 < NGRP:
+                prep_t(gi + 1, 1)

@@ -13,13 +13,42 @@ ACT = mybir.ActivationFunctionType
 
 P = 128
 C = 1024
-TG = 4
-NGRP = 4
 EPS = 1e-5
 FLOPS = 2 * 2048 * 1024 * 2048
 
-N_V_STATS = (4, 1, 1, 1)
-PASS1_ON_G = False
+PINNED = True
+FLAT = (
+    ("sv", 0, 0), ("sv", 0, 1), ("ra", 0), ("rb", 0), ("p1", 0, 0), ("p1", 0, 1), ("xt", 0, 0), ("sv", 1, 0),
+    ("xt", 0, 1), ("wt", 0, 0), ("sv", 1, 1), ("rq", 0, 0), ("ra", 1), ("rq", 0, 1), ("wt", 0, 1), ("wt", 1, 0),
+    ("rb", 1), ("p1", 1, 1), ("wt", 1, 3), ("sa", 2, 1), ("p1", 1, 0), ("wt", 0, 2), ("sn", 2), ("sv", 2, 0),
+    ("wt", 0, 3), ("wq", 0), ("wt", 1, 2), ("xt", 1, 0), ("xt", 1, 1), ("rq", 1, 0), ("mb", 1, 0, 0),
+    ("mb", 0, 0, 0), ("rq", 1, 1), ("sb", 2, 1), ("wt", 2, 0), ("sa", 3, 1), ("wt", 1, 1), ("sn", 3), ("ra", 2),
+    ("wq", 1), ("wt", 2, 3), ("rb", 2), ("wt", 3, 0), ("mb", 3, 0, 0), ("wt", 2, 1), ("p1", 2, 1), ("wt", 3, 3),
+    ("sv", 3, 0), ("p1", 2, 0), ("sv", 4, 0), ("mb", 2, 0, 0), ("wt", 2, 2), ("mb", 3, 0, 1), ("wt", 3, 2),
+    ("mb", 0, 0, 1), ("sb", 3, 1), ("wq", 2), ("mb", 1, 0, 1), ("wt", 3, 1), ("mb", 2, 0, 1), ("xt", 2, 0),
+    ("wq", 3), ("ra", 3), ("xt", 2, 1), ("rq", 2, 0), ("rb", 3), ("rq", 2, 1), ("mb", 2, 1, 1), ("p1", 3, 0),
+    ("mb", 2, 1, 0), ("sa", 4, 1), ("sn", 4), ("mb", 0, 1, 1), ("mb", 0, 1, 0), ("sa", 5, 1), ("sb", 4, 1),
+    ("mb", 5, 1, 0), ("ra", 4), ("mb", 3, 1, 1), ("p1", 3, 1), ("mb", 4, 0, 0), ("sa", 5, 0), ("mb", 5, 1, 1),
+    ("rb", 4), ("mb", 1, 1, 0), ("p1", 4, 0), ("sn", 5), ("xt", 3, 0), ("mb", 1, 1, 1), ("rq", 3, 0), ("xt", 3, 1),
+    ("sb", 5, 1), ("sb", 5, 0), ("mb", 3, 1, 0), ("mb", 5, 0, 1), ("p1", 4, 1), ("mb", 5, 0, 0), ("rq", 3, 1),
+    ("mb", 4, 0, 1), ("ra", 5), ("sv", 6, 0), ("rb", 5), ("sa", 6, 1), ("p1", 5, 0), ("xt", 4, 0), ("sn", 6),
+    ("p1", 5, 1), ("sb", 6, 1), ("mb", 7, 0, 0), ("xt", 4, 1), ("mb", 6, 1, 0), ("ra", 6), ("mb", 4, 1, 0),
+    ("mb", 7, 0, 1), ("mb", 6, 0, 1), ("mb", 6, 1, 1), ("mb", 7, 1, 1), ("rq", 4, 0), ("xt", 5, 0), ("rq", 4, 1),
+    ("mb", 6, 0, 0), ("rb", 6), ("sa", 7, 1), ("rq", 5, 0), ("xt", 5, 1), ("sa", 7, 0), ("sn", 7), ("sb", 7, 1),
+    ("p1", 6, 1), ("mb", 8, 0, 1), ("p1", 6, 0), ("mb", 4, 1, 1), ("mb", 7, 1, 0), ("mb", 9, 0, 0), ("sb", 7, 0),
+    ("mb", 8, 0, 0), ("mb", 9, 1, 0), ("rq", 5, 1), ("mb", 9, 1, 1), ("ra", 7), ("rb", 7), ("mb", 8, 1, 1),
+    ("xt", 6, 0), ("mb", 8, 1, 0), ("mb", 11, 0, 1), ("p1", 7, 1), ("mb", 9, 0, 1), ("mb", 10, 0, 1),
+    ("mb", 11, 1, 1), ("p1", 7, 0), ("xt", 6, 1), ("rq", 6, 0), ("mb", 10, 0, 0), ("rq", 6, 1), ("mb", 11, 0, 0),
+    ("xt", 7, 0), ("mb", 11, 1, 0), ("mb", 10, 1, 1), ("mb", 10, 1, 0), ("mb", 12, 0, 0), ("mb", 12, 0, 1),
+    ("rq", 7, 0), ("mb", 13, 0, 1), ("mb", 12, 1, 0), ("xt", 7, 1), ("mb", 13, 0, 0), ("rq", 7, 1),
+    ("mb", 12, 1, 1), ("mb", 13, 1, 0), ("mb", 14, 0, 0), ("mb", 13, 1, 1), ("mb", 14, 0, 1), ("mb", 15, 0, 1),
+    ("mb", 14, 1, 0), ("mb", 15, 0, 0), ("mb", 14, 1, 1), ("mb", 15, 1, 1), ("mb", 15, 1, 0),
+)
+LOADS = (("x", 0), ("x", 1), ("w", 0), ("w", 1), ("w", 2), ("w", 3), ("x", 2), ("x", 3), ("x", 4), ("x", 5), ("x", 6), ("x", 7))
+PREP = ((0, 2), (2, 2), (4, 2), (6, 2), (8, 2), (10, 2), (12, 2), (14, 2))
+NV = (2, 2, 1, 1, 1, 0, 1, 0)
+P1_ON_G = (False, True, True, True, True, True, True, True)
+W_EVAC_V = ((2, 3), (1, 3), (), ())
 F_ON_S = ()
 
 
@@ -28,11 +57,13 @@ def tile_attentionalpoolerwmasking_pa_kernel(tc, x, ln_k_w, ln_k_b, Wk, Wv, bk, 
     xf = x.flatten_outer_dims()
     outs = (out_0.flatten_outer_dims(), out_1.flatten_outer_dims())
     with ExitStack() as ctx:
+        if PINNED:
+            ctx.enter_context(tc.manual_schedule())
         const = ctx.enter_context(tc.tile_pool(name="const", bufs=1))
-        small = ctx.enter_context(tc.tile_pool(name="small", bufs=2))
+        small = ctx.enter_context(tc.tile_pool(name="small", bufs=8))
         xhp = ctx.enter_context(tc.tile_pool(name="xhp", bufs=8))
         work = ctx.enter_context(tc.tile_pool(name="work", bufs=2))
-        grpp = ctx.enter_context(tc.tile_pool(name="grpp", bufs=4))
+        grpp = ctx.enter_context(tc.tile_pool(name="grpp", bufs=3))
         ostp = ctx.enter_context(tc.tile_pool(name="ostp", bufs=6))
         pst = ctx.enter_context(tc.psum_pool(name="pst", bufs=4))
         pso = ctx.enter_context(tc.psum_pool(name="pso", bufs=4))
@@ -41,190 +72,239 @@ def tile_attentionalpoolerwmasking_pa_kernel(tc, x, ln_k_w, ln_k_b, Wk, Wv, bk, 
         nc.vector.memset(vecs[:], 0.0)
         nc.sync.dma_start(out=vecs[0:4, :], in_=ln_k_w.rearrange("(v q) -> v q", v=4))
         nc.sync.dma_start(out=vecs[4:8, :], in_=ln_k_b.rearrange("(v q) -> v q", v=4))
-        one_t = const.tile([P, 1], F32, name="one_t")
-        nc.vector.memset(one_t[:], 1.0)
+        brow = const.tile([P, 2048], BF16, name="brow")
+        nc.vector.memset(brow[:], 0.0)
+        nc.sync.dma_start(out=brow[0:1, 0:1024], in_=bk.rearrange("(o d) -> o d", o=1))
+        nc.sync.dma_start(out=brow[0:1, 1024:2048], in_=bv.rearrange("(o d) -> o d", o=1))
+        ones = const.tile([P, P], BF16, name="ones")
+        nc.vector.memset(ones[:], 1.0)
+        zero_t = const.tile([P, 1], F32, name="zero_t")
+        nc.vector.memset(zero_t[:], 0.0)
+        eps_t = const.tile([P, 1], F32, name="eps_t")
+        nc.vector.tensor_scalar(out=eps_t[:], in0=zero_t[:], scalar1=EPS, scalar2=None, op0=ALU.add)
         warm = const.tile([P, 1], F32, name="warm")
-        nc.scalar.activation(out=warm[:], in_=one_t[:], func=ACT.Sqrt)
+        nc.scalar.activation(out=warm[:], in_=eps_t[:], func=ACT.Sqrt)
         ident = const.tile([P, P], F32, name="ident")
         make_identity(nc, ident[:])
 
-        xts = []
-        wts = []
-        for gi in range(NGRP):
-            xts.append(const.tile([P, TG, C], BF16, name="xt%d" % gi))
-            wts.append(const.tile([P, 4, C], BF16, name="wt%d" % gi))
+        xts = [const.tile([P, nt, C], BF16, name="xt%d" % gi) for gi, (t0, nt) in enumerate(PREP)]
+        wts = [const.tile([P, 4, C], BF16, name="wt%d" % c) for c in range(4)]
         bias_bc = const.tile([P, 2048], BF16, name="bias_bc")
 
         def load_x(gi):
-            nc.sync.dma_start(out=xts[gi][:], in_=xf[512 * gi : 512 * gi + 512, :].rearrange("(n p) c -> p n c", p=P))
+            t0, nt = PREP[gi]
+            nc.sync.dma_start(
+                out=xts[gi][:], in_=xf[P * t0 : P * (t0 + nt), :].rearrange("(n p) c -> p n c", p=P)
+            )
 
         def load_w(c):
             src = Wk if c < 2 else Wv
             r0 = 512 * (c % 2)
             nc.sync.dma_start(out=wts[c][:], in_=src[r0 : r0 + 512, :].rearrange("(n p) c -> p n c", p=P))
 
-        for h in range(2):
-            nc.sync.dma_start(
-                out=xts[0][:, 2 * h : 2 * h + 2, :],
-                in_=xf[256 * h : 256 * h + 256, :].rearrange("(n p) c -> p n c", p=P),
-            )
-        load_w(0)
-        load_w(1)
-        nc.sync.dma_start(out=bias_bc[:, 0:1024], in_=bk.partition_broadcast(P))
-        nc.sync.dma_start(out=bias_bc[:, 1024:2048], in_=bv.partition_broadcast(P))
-        load_w(2)
-        load_w(3)
-        load_x(1)
-        load_x(2)
-        load_x(3)
+        for kind, i in LOADS:
+            if kind == "x":
+                load_x(i)
+            else:
+                load_w(i)
 
         vb = pst.tile([P, 512], F32, tag="tp", name="vb")
         nc.tensor.transpose(vb[:, 0:P], vecs[:].bitcast(F32), ident[:])
         wb = const.tile([P, 16], F32, name="wb")
         nc.vector.tensor_copy(out=wb[:], in_=vb[:, 0:8].bitcast(BF16))
+        for c in range(4):
+            bb = pst.tile([P, 512], F32, tag="tp", name="bb")
+            nc.tensor.matmul(out=bb[:], lhsT=ones[:], rhs=brow[:, 512 * c : 512 * c + 512], start=True, stop=True)
+            nc.scalar.copy(out=bias_bc[:, 512 * c : 512 * c + 512], in_=bb[:])
 
         wq = const.tile([P, 2, 2048], U32, name="wq", align_bytes=64)
         ws = const.tile([P, 2, 2048], U8, name="ws", align_bytes=64)
+        gws = {}
 
-        def prep_w(c):
-            gw = work.tile([P, 2, 2048], BF16, tag="gw", name="gw", align_bytes=64)
-            gw32 = gw[:].bitcast(F32).rearrange("p g (d u) -> p g d u", u=2)
-            for n in range(4):
-                bank = pst.tile([P, 512], F32, tag="tp", name="wbank")
-                w32 = wts[c][:, n, :].bitcast(F32)
-                for v in range(4):
-                    nc.tensor.transpose(bank[:, P * v : P * v + P], w32[:, P * v : P * v + P], ident[:])
-                nc.scalar.copy(
-                    out=gw32[:, :, P * n : P * n + P, :],
-                    in_=bank[:].rearrange("p (g u d) -> p g d u", g=2, u=2),
-                )
+        def wt_tile(c, n):
+            if n == 0:
+                gws[c] = work.tile([P, 2, 2048], BF16, tag="gw", name="gw", align_bytes=64)
+            gw32 = gws[c][:].bitcast(F32).rearrange("p g (d u) -> p g d u", u=2)
+            bank = pst.tile([P, 512], F32, tag="tp", name="wbank")
+            w32 = wts[c][:, n, :].bitcast(F32)
+            for v in range(4):
+                nc.tensor.transpose(bank[:, P * v : P * v + P], w32[:, P * v : P * v + P], ident[:])
+            dst = gw32[:, :, P * n : P * n + P, :]
+            src = bank[:].rearrange("p (g u d) -> p g d u", g=2, u=2)
+            if n in W_EVAC_V[c]:
+                nc.vector.tensor_copy(out=dst, in_=src)
+            else:
+                nc.scalar.copy(out=dst, in_=src)
+
+        def wq_chunk(c):
             for g in range(2):
                 nc.vector.quantize_mx(
                     out=wq[:, g, 512 * c : 512 * c + 512].bitcast(FP8X4),
                     scales=ws[:, g, 512 * c : 512 * c + 512],
-                    in_=gw[:, g, :],
+                    in_=gws[c][:, g, :],
                 )
 
-        state = {}
+        st8 = [{} for gi in range(len(PREP))]
 
-        def prep_stats(gi):
-            xt = xts[gi]
-            nv = N_V_STATS[gi]
-            ve = small.tile([P, TG], F32, tag="ve", name="ve")
-            std = small.tile([P, TG], F32, tag="std", name="std")
-            rstd = small.tile([P, TG], F32, tag="rstd", name="rstd")
-            nms = []
+        def stats_open(gi):
+            nt = PREP[gi][1]
+            s = st8[gi]
+            if NV[gi] > 0:
+                s["mv"] = small.tile([P, 4, 2], F32, tag="mv", name="mv")
+                s["nmv"] = small.tile([P, 4], F32, tag="nmv", name="nmv")
+            if NV[gi] < nt:
+                s["sm"] = small.tile([P, 4], F32, tag="sm", name="sm")
+                s["nms"] = small.tile([P, 4], F32, tag="nms", name="nms")
+                s["sq"] = small.tile([P, 4], F32, tag="sq", name="sq")
+            s["std"] = small.tile([P, 4], F32, tag="std", name="std")
+            s["rstd"] = small.tile([P, 4], F32, tag="rstd", name="rstd")
+            s["xh"] = [None] * nt
+
+        def stats_v(gi, n):
+            st = small.tile([P, 2, 6], F32, tag="st", name="st", bufs=4)
+            for h in range(2):
+                nc.vector.bn_stats(out=st[:, h, :], in_=xts[gi][:, n, 512 * h : 512 * h + 512])
+            nc.vector.bn_aggr(out=st8[gi]["mv"][:, n, :], in_=st[:].rearrange("p a b -> p (a b)"))
+
+        def stats_s_a(gi, n):
+            junk = work.tile([P, C], BF16, tag="junk", name="junk")
+            nc.scalar.activation(
+                out=junk[:], in_=xts[gi][:, n, :], func=ACT.Identity, accum_out=st8[gi]["sm"][:, n : n + 1]
+            )
+
+        def stats_s_nm(gi):
+            nv, nt = NV[gi], PREP[gi][1]
+            nc.scalar.mul(out=st8[gi]["nms"][:, nv:nt], in_=st8[gi]["sm"][:, nv:nt], mul=-1.0 / C)
+
+        def stats_s_b(gi, n):
+            junk = work.tile([P, C], BF16, tag="junk", name="junk")
+            nc.scalar.activation(
+                out=junk[:], in_=xts[gi][:, n, :], func=ACT.Square, bias=st8[gi]["nms"][:, n : n + 1], scale=1.0,
+                accum_out=st8[gi]["sq"][:, n : n + 1],
+            )
+
+        def rstd_a(gi):
+            nv, nt = NV[gi], PREP[gi][1]
+            s = st8[gi]
             if nv > 0:
-                mv = small.tile([P, TG, 2], F32, tag="mv", name="mv")
-                nmv = small.tile([P, TG], F32, tag="nmv", name="nmv")
-                for n in range(nv):
-                    st = small.tile([P, 2, 6], F32, tag="st", name="st", bufs=4)
-                    for h in range(2):
-                        nc.vector.bn_stats(out=st[:, h, :], in_=xt[:, n, 512 * h : 512 * h + 512])
-                    nc.vector.bn_aggr(out=mv[:, n, :], in_=st[:].rearrange("p a b -> p (a b)"))
-                nc.vector.tensor_scalar(out=nmv[:, 0:nv], in0=mv[:, 0:nv, 0], scalar1=-1.0, scalar2=None, op0=ALU.mult)
-                nc.vector.tensor_scalar(out=ve[:, 0:nv], in0=mv[:, 0:nv, 1], scalar1=EPS, scalar2=None, op0=ALU.add)
-                for n in range(nv):
-                    nms.append(nmv[:, n : n + 1])
-            if nv < TG:
-                sm = small.tile([P, TG], F32, tag="sm", name="sm")
-                nmS = small.tile([P, TG], F32, tag="nmS", name="nmS")
-                sq = small.tile([P, TG], F32, tag="sq", name="sq")
-                for n in range(nv, TG):
-                    junk = work.tile([P, C], BF16, tag="junk", name="junk")
-                    nc.scalar.activation(out=junk[:], in_=xt[:, n, :], func=ACT.Identity, accum_out=sm[:, n : n + 1])
-                nc.scalar.mul(out=nmS[:, nv:TG], in_=sm[:, nv:TG], mul=-1.0 / C)
-                for n in range(nv, TG):
-                    junk = work.tile([P, C], BF16, tag="junk", name="junk")
-                    nc.scalar.activation(
-                        out=junk[:], in_=xt[:, n, :], func=ACT.Square, bias=nmS[:, n : n + 1], scale=1.0,
-                        accum_out=sq[:, n : n + 1],
-                    )
-                nc.vector.tensor_scalar(out=ve[:, nv:TG], in0=sq[:, nv:TG], scalar1=1.0 / C, scalar2=EPS, op0=ALU.mult, op1=ALU.add)
-                for n in range(nv, TG):
-                    nms.append(nmS[:, n : n + 1])
-            nc.scalar.activation(out=std[:], in_=ve[:], func=ACT.Sqrt)
-            nc.vector.reciprocal(out=rstd[:], in_=std[:])
-            xhs = []
-            eng = nc.gpsimd if PASS1_ON_G else nc.vector
-            for n in range(TG):
-                xh = xhp.tile([P, 8, P], F32, tag="xh", name="xh")
-                eng.tensor_scalar(
-                    out=xh[:].rearrange("p (v e) q -> p v e q", e=2),
-                    in0=xt[:, n, :].rearrange("p (v q e) -> p v e q", v=4, e=2),
-                    scalar1=nms[n],
-                    scalar2=rstd[:, n : n + 1],
-                    op0=ALU.add,
-                    op1=ALU.mult,
+                nc.vector.tensor_scalar(
+                    out=s["nmv"][:, 0:nv], in0=s["mv"][:, 0:nv, 0], scalar1=-1.0, scalar2=None, op0=ALU.mult
                 )
-                xhs.append(xh)
-            state[gi] = {"xh": xhs}
-
-        def prep_t(gi, g):
-            s = state[gi]
-            if g == 0:
-                s["plan"] = work.tile([P, 8, 512], BF16, tag="plan", name="plan")
-                s["xq"] = work.tile([P, 2, 512], U32, tag="xq", name="xq", align_bytes=64)
-                s["xs"] = work.tile([P, 2, 512], U8, tag="xs", name="xs", align_bytes=64)
-            plan = s["plan"]
-            for t in range(4):
-                pl = 4 * g + t
-                bank = pst.tile([P, 512], F32, tag="tp", name="xbank")
-                for n in range(TG):
-                    nc.tensor.transpose(bank[:, P * n : P * n + P], s["xh"][n][:, pl, :], ident[:])
                 nc.scalar.activation(
-                    out=plan[:, pl, :], in_=bank[:], func=ACT.Identity,
-                    scale=wb[:, pl : pl + 1], bias=wb[:, 8 + pl : 9 + pl],
+                    out=s["std"][:, 0:nv], in_=s["mv"][:, 0:nv, 1], func=ACT.Sqrt, bias=eps_t[:], scale=1.0
                 )
-            grp = grpp.tile([P, 512, 4], BF16, tag="grp", name="grp", align_bytes=64)
-            nc.vector.tensor_copy(out=grp[:], in_=plan[:, 4 * g : 4 * g + 4, :].rearrange("p t r -> p r t"))
+            if nv < nt:
+                nc.scalar.activation(
+                    out=s["std"][:, nv:nt], in_=s["sq"][:, nv:nt], func=ACT.Sqrt, bias=eps_t[:], scale=1.0 / C
+                )
+
+        def rstd_b(gi):
+            nt = PREP[gi][1]
+            nc.vector.reciprocal(out=st8[gi]["rstd"][:, 0:nt], in_=st8[gi]["std"][:, 0:nt])
+
+        def p1(gi, n):
+            s = st8[gi]
+            nm = s["nmv"] if n < NV[gi] else s["nms"]
+            xh = xhp.tile([P, 8, P], F32, tag="xh", name="xh")
+            eng = nc.gpsimd if P1_ON_G[gi] else nc.vector
+            eng.tensor_scalar(
+                out=xh[:].rearrange("p (v e) q -> p v e q", e=2),
+                in0=xts[gi][:, n, :].rearrange("p (v q e) -> p v e q", v=4, e=2),
+                scalar1=nm[:, n : n + 1],
+                scalar2=s["rstd"][:, n : n + 1],
+                op0=ALU.add,
+                op1=ALU.mult,
+            )
+            s["xh"][n] = xh
+
+        def xt_half(gi, g):
+            nt = PREP[gi][1]
+            ntok = P * nt
+            ppb = 512 // ntok
+            s = st8[gi]
+            if g == 0:
+                s["plan"] = work.tile([P, 8, ntok], BF16, tag="plan%d" % nt, name="plan")
+                s["xq"] = work.tile([P, 2, ntok], U32, tag="xq%d" % nt, name="xq", align_bytes=64, bufs=4)
+                s["xs"] = work.tile([P, 2, ntok], U8, tag="xs%d" % nt, name="xs", align_bytes=64, bufs=4)
+            for b in range(4 // ppb):
+                bank = pst.tile([P, 512], F32, tag="tp", name="xbank")
+                for a in range(ppb):
+                    pl = 4 * g + ppb * b + a
+                    for n in range(nt):
+                        o = ntok * a + P * n
+                        nc.tensor.transpose(bank[:, o : o + P], s["xh"][n][:, pl, :], ident[:])
+                for a in range(ppb):
+                    pl = 4 * g + ppb * b + a
+                    nc.scalar.activation(
+                        out=s["plan"][:, pl, :], in_=bank[:, ntok * a : ntok * a + ntok], func=ACT.Identity,
+                        scale=wb[:, pl : pl + 1], bias=wb[:, 8 + pl : 9 + pl],
+                    )
+
+        def rq(gi, g):
+            ntok = P * PREP[gi][1]
+            s = st8[gi]
+            grp = grpp.tile([P, ntok, 4], BF16, tag="grp%d" % ntok, name="grp", align_bytes=64)
+            nc.vector.tensor_copy(
+                out=grp[:].rearrange("p (c i) t -> p c t i", i=4),
+                in_=s["plan"][:, 4 * g : 4 * g + 4, :].rearrange("p t (c i) -> p c t i", i=4),
+            )
             nc.vector.quantize_mx(
                 out=s["xq"][:, g, :].bitcast(FP8X4),
                 scales=s["xs"][:, g, :],
                 in_=grp[:].rearrange("p r t -> p (r t)"),
             )
 
-        def mx_half(gi, half):
-            s = state[gi]
-            for n in range(TG):
-                ost = ostp.tile([P, 1024], F32, tag="ost", name="ost")
-                for j in range(2):
-                    ch = 2 * half + j
-                    acc = pso.tile([P, 512], F32, tag="acc", name="acc")
-                    for g in range(2):
-                        nc.tensor.matmul_mx(
-                            out=acc[:],
-                            lhsT=s["xq"][:, g, P * n : P * n + P].bitcast(FP8X4),
-                            lhsT_scale=s["xs"][:, g, P * n : P * n + P],
-                            rhs=wq[:, g, 512 * ch : 512 * ch + 512].bitcast(FP8X4),
-                            rhs_scale=ws[:, g, 512 * ch : 512 * ch + 512],
-                            start=(g == 0),
-                            stop=(g == 1),
-                        )
-                    o = ost[:, 512 * j : 512 * j + 512]
-                    b = bias_bc[:, 512 * ch : 512 * ch + 512]
-                    if (8 * half + 2 * n + j) in F_ON_S:
-                        nc.scalar.copy(out=o, in_=acc[:])
-                        nc.gpsimd.tensor_tensor(out=o, in0=o, in1=b, op=ALU.add)
-                    else:
-                        nc.vector.tensor_tensor(out=o, in0=acc[:], in1=b, op=ALU.add)
-                r0 = 512 * gi + P * n
-                nc.sync.dma_start(out=outs[half][r0 : r0 + P, :], in_=ost[:])
+        where = {}
+        for gi, (t0, nt) in enumerate(PREP):
+            for n in range(nt):
+                where[t0 + n] = (gi, n)
+        osts = {}
 
-        prep_stats(0)
-        prep_w(0)
-        prep_w(1)
-        prep_t(0, 0)
-        prep_t(0, 1)
-        for gi in range(NGRP):
-            if gi + 1 < NGRP:
-                prep_stats(gi + 1)
-            mx_half(gi, 0)
-            if gi == 0:
-                prep_w(2)
-                prep_w(3)
-            if gi + 1 < NGRP:
-                prep_t(gi + 1, 0)
-            mx_half(gi, 1)
-            if gi + 1 < NGRP:
-                prep_t(gi + 1, 1)
+        def mb(tile_i, half, j):
+            gi, n = where[tile_i]
+            s = st8[gi]
+            if (tile_i, half) not in osts:
+                osts[(tile_i, half)] = [ostp.tile([P, 1024], F32, tag="ost", name="ost"), 0]
+            ost = osts[(tile_i, half)][0]
+            osts[(tile_i, half)][1] += 1
+            ch = 2 * half + j
+            acc = pso.tile([P, 512], F32, tag="acc", name="acc")
+            for g in range(2):
+                nc.tensor.matmul_mx(
+                    out=acc[:],
+                    lhsT=s["xq"][:, g, P * n : P * n + P].bitcast(FP8X4),
+                    lhsT_scale=s["xs"][:, g, P * n : P * n + P],
+                    rhs=wq[:, g, 512 * ch : 512 * ch + 512].bitcast(FP8X4),
+                    rhs_scale=ws[:, g, 512 * ch : 512 * ch + 512],
+                    start=(g == 0),
+                    stop=(g == 1),
+                )
+            o = ost[:, 512 * j : 512 * j + 512]
+            b = bias_bc[:, 512 * ch : 512 * ch + 512]
+            if (tile_i, half, j) in F_ON_S:
+                nc.scalar.copy(out=o, in_=acc[:])
+                nc.gpsimd.tensor_tensor(out=o, in0=o, in1=b, op=ALU.add)
+            else:
+                nc.vector.tensor_tensor(out=o, in0=acc[:], in1=b, op=ALU.add)
+            if osts[(tile_i, half)][1] == 2:
+                nc.sync.dma_start(out=outs[half][P * tile_i : P * tile_i + P, :], in_=ost[:])
+
+        def run(tasks):
+            for t in tasks:
+                t[0](*t[1:])
+
+        def stats_s_tasks(gi):
+            nv, nt = NV[gi], PREP[gi][1]
+            return (
+                [(stats_s_a, gi, n) for n in range(nv, nt)]
+                + ([(stats_s_nm, gi)] if nv < nt else [])
+                + [(stats_s_b, gi, n) for n in range(nv, nt)]
+            )
+
+        NG = len(PREP)
+        fn = {"sv": stats_v, "ra": rstd_a, "rb": rstd_b, "p1": p1, "wt": wt_tile, "wq": wq_chunk, "xt": xt_half,
+              "rq": rq, "sa": stats_s_a, "sn": stats_s_nm, "sb": stats_s_b, "mb": mb}
+        for gi in range(NG):
+            stats_open(gi)
+        for t in FLAT:
+            fn[t[0]](*t[1:])

@@ -15,41 +15,28 @@ P = 128
 C = 1024
 EPS = 1e-5
 FLOPS = 2 * 2048 * 1024 * 2048
+NG = 8
 
-PINNED = True
-FLAT = (
-    ("sv", 0, 0), ("sv", 0, 1), ("ra", 0), ("rb", 0), ("p1", 0, 0), ("p1", 0, 1), ("xt", 0, 0), ("sv", 1, 0),
-    ("xt", 0, 1), ("wt", 0, 0), ("sv", 1, 1), ("rq", 0, 0), ("ra", 1), ("rq", 0, 1), ("wt", 0, 1), ("wt", 1, 0),
-    ("rb", 1), ("p1", 1, 1), ("wt", 1, 3), ("sa", 2, 1), ("p1", 1, 0), ("wt", 0, 2), ("sn", 2), ("sv", 2, 0),
-    ("wt", 0, 3), ("wq", 0), ("wt", 1, 2), ("xt", 1, 0), ("xt", 1, 1), ("rq", 1, 0), ("mb", 1, 0, 0),
-    ("mb", 0, 0, 0), ("rq", 1, 1), ("sb", 2, 1), ("wt", 2, 0), ("sa", 3, 1), ("wt", 1, 1), ("sn", 3), ("ra", 2),
-    ("wq", 1), ("wt", 2, 3), ("rb", 2), ("wt", 3, 0), ("mb", 3, 0, 0), ("wt", 2, 1), ("p1", 2, 1), ("wt", 3, 3),
-    ("sv", 3, 0), ("p1", 2, 0), ("sv", 4, 0), ("mb", 2, 0, 0), ("wt", 2, 2), ("mb", 3, 0, 1), ("wt", 3, 2),
-    ("mb", 0, 0, 1), ("sb", 3, 1), ("wq", 2), ("mb", 1, 0, 1), ("wt", 3, 1), ("mb", 2, 0, 1), ("xt", 2, 0),
-    ("wq", 3), ("ra", 3), ("xt", 2, 1), ("rq", 2, 0), ("rb", 3), ("rq", 2, 1), ("mb", 2, 1, 1), ("p1", 3, 0),
-    ("mb", 2, 1, 0), ("sa", 4, 1), ("sn", 4), ("mb", 0, 1, 1), ("mb", 0, 1, 0), ("sa", 5, 1), ("sb", 4, 1),
-    ("mb", 5, 1, 0), ("ra", 4), ("mb", 3, 1, 1), ("p1", 3, 1), ("mb", 4, 0, 0), ("sa", 5, 0), ("mb", 5, 1, 1),
-    ("rb", 4), ("mb", 1, 1, 0), ("p1", 4, 0), ("sn", 5), ("xt", 3, 0), ("mb", 1, 1, 1), ("rq", 3, 0), ("xt", 3, 1),
-    ("sb", 5, 1), ("sb", 5, 0), ("mb", 3, 1, 0), ("mb", 5, 0, 1), ("p1", 4, 1), ("mb", 5, 0, 0), ("rq", 3, 1),
-    ("mb", 4, 0, 1), ("ra", 5), ("sv", 6, 0), ("rb", 5), ("sa", 6, 1), ("p1", 5, 0), ("xt", 4, 0), ("sn", 6),
-    ("p1", 5, 1), ("sb", 6, 1), ("mb", 7, 0, 0), ("xt", 4, 1), ("mb", 6, 1, 0), ("ra", 6), ("mb", 4, 1, 0),
-    ("mb", 7, 0, 1), ("mb", 6, 0, 1), ("mb", 6, 1, 1), ("mb", 7, 1, 1), ("rq", 4, 0), ("xt", 5, 0), ("rq", 4, 1),
-    ("mb", 6, 0, 0), ("rb", 6), ("sa", 7, 1), ("rq", 5, 0), ("xt", 5, 1), ("sa", 7, 0), ("sn", 7), ("sb", 7, 1),
-    ("p1", 6, 1), ("mb", 8, 0, 1), ("p1", 6, 0), ("mb", 4, 1, 1), ("mb", 7, 1, 0), ("mb", 9, 0, 0), ("sb", 7, 0),
-    ("mb", 8, 0, 0), ("mb", 9, 1, 0), ("rq", 5, 1), ("mb", 9, 1, 1), ("ra", 7), ("rb", 7), ("mb", 8, 1, 1),
-    ("xt", 6, 0), ("mb", 8, 1, 0), ("mb", 11, 0, 1), ("p1", 7, 1), ("mb", 9, 0, 1), ("mb", 10, 0, 1),
-    ("mb", 11, 1, 1), ("p1", 7, 0), ("xt", 6, 1), ("rq", 6, 0), ("mb", 10, 0, 0), ("rq", 6, 1), ("mb", 11, 0, 0),
-    ("xt", 7, 0), ("mb", 11, 1, 0), ("mb", 10, 1, 1), ("mb", 10, 1, 0), ("mb", 12, 0, 0), ("mb", 12, 0, 1),
-    ("rq", 7, 0), ("mb", 13, 0, 1), ("mb", 12, 1, 0), ("xt", 7, 1), ("mb", 13, 0, 0), ("rq", 7, 1),
-    ("mb", 12, 1, 1), ("mb", 13, 1, 0), ("mb", 14, 0, 0), ("mb", 13, 1, 1), ("mb", 14, 0, 1), ("mb", 15, 0, 1),
-    ("mb", 14, 1, 0), ("mb", 15, 0, 0), ("mb", 14, 1, 1), ("mb", 15, 1, 1), ("mb", 15, 1, 0),
-)
-LOADS = (("x", 0), ("x", 1), ("w", 0), ("w", 1), ("w", 2), ("w", 3), ("x", 2), ("x", 3), ("x", 4), ("x", 5), ("x", 6), ("x", 7))
-PREP = ((0, 2), (2, 2), (4, 2), (6, 2), (8, 2), (10, 2), (12, 2), (14, 2))
-NV = (2, 2, 1, 1, 1, 0, 1, 0)
-P1_ON_G = (False, True, True, True, True, True, True, True)
-W_EVAC_V = ((2, 3), (1, 3), (), ())
+XH_BUFS = 6
+PLAN_BUFS = 3
+OSTV_BUFS = 6
+OSTS_BUFS = 2
+SMALL_ON_S = True
+STAT_V = (0, 1, 2, 4, 5, 7, 10, 15)
 F_ON_S = ()
+ON_V = (('P1', 0), ('P1', 1), ('WE', 0, 2), ('WE', 0, 3), ('C', 1, 0, 0), ('C', 1, 1, 0))
+ON_G = (('RG', 2, 0), ('RG', 3, 0), ('RG', 5, 0), ('RG', 7, 0), ('RG', 7, 1), ('RG', 2, 1), ('RG', 6, 0))
+QUEUES = {
+    'PE': (('WT', 0, 0), ('WT', 0, 1), ('VB',), ('WT', 0, 2), ('WT', 0, 3), ('T', 0, 0, 0), ('T', 0, 0, 1), ('T', 0, 1, 0), ('T', 0, 1, 1), ('BB', 0), ('WT', 1, 0), ('WT', 1, 1), ('WT', 1, 2), ('WT', 1, 3), ('WT', 2, 0), ('WT', 2, 1), ('WT', 2, 2), ('WT', 2, 3), ('M', 0, 0), ('M', 1, 0), ('M', 0, 1), ('M', 1, 1), ('T', 1, 0, 0), ('T', 1, 0, 1), ('T', 1, 1, 0), ('T', 1, 1, 1), ('WT', 3, 0), ('WT', 3, 1), ('WT', 3, 2), ('WT', 3, 3), ('BB', 1), ('M', 0, 2), ('M', 1, 2), ('M', 0, 3), ('M', 1, 3), ('T', 2, 0, 0), ('T', 2, 0, 1), ('T', 2, 1, 0), ('T', 2, 1, 1), ('M', 2, 0), ('M', 2, 1), ('M', 2, 2), ('M', 2, 3), ('M', 3, 0), ('M', 3, 1), ('M', 3, 2), ('M', 3, 3), ('T', 3, 0, 0), ('T', 3, 0, 1), ('T', 3, 1, 0), ('T', 3, 1, 1), ('M', 4, 0), ('M', 4, 1), ('M', 4, 2), ('M', 4, 3), ('M', 5, 0), ('M', 5, 1), ('M', 5, 2), ('M', 5, 3), ('T', 4, 0, 0), ('T', 4, 0, 1), ('T', 4, 1, 0), ('T', 4, 1, 1), ('M', 6, 0), ('M', 6, 1), ('M', 6, 2), ('M', 6, 3), ('M', 7, 0), ('M', 7, 1), ('M', 7, 2), ('M', 7, 3), ('T', 5, 0, 0), ('T', 5, 0, 1), ('T', 5, 1, 0), ('T', 5, 1, 1), ('M', 8, 0), ('M', 8, 1), ('M', 8, 2), ('M', 8, 3), ('M', 9, 0), ('M', 9, 1), ('M', 9, 2), ('M', 9, 3), ('T', 6, 0, 0), ('T', 6, 0, 1), ('T', 6, 1, 0), ('T', 6, 1, 1), ('M', 10, 0), ('M', 10, 1), ('M', 10, 2), ('M', 10, 3), ('M', 11, 0), ('M', 11, 1), ('M', 11, 2), ('M', 11, 3), ('T', 7, 0, 0), ('T', 7, 0, 1), ('T', 7, 1, 0), ('T', 7, 1, 1), ('M', 12, 0), ('M', 12, 1), ('M', 12, 2), ('M', 12, 3), ('M', 13, 0), ('M', 13, 1), ('M', 13, 2), ('M', 13, 3), ('M', 14, 0), ('M', 14, 1), ('M', 14, 2), ('M', 14, 3), ('M', 15, 0), ('M', 15, 1), ('M', 15, 2), ('M', 15, 3)),
+    'S': (('IS',), ('LDV',), ('LDB',), ('SA', 3), ('RA', 0), ('RA', 1), ('SN', 3), ('WE', 0, 0), ('WE', 0, 1), ('SB', 3), ('C', 0, 0, 0), ('C', 0, 0, 1), ('C', 0, 1, 0), ('C', 0, 1, 1), ('RA', 2), ('RA', 3), ('BC', 0), ('WE', 1, 0), ('WE', 1, 1), ('WE', 1, 2), ('WE', 1, 3), ('WE', 2, 0), ('WE', 2, 1), ('WE', 2, 2), ('WE', 2, 3), ('RA', 5), ('RA', 4), ('SA', 6), ('SN', 6), ('SB', 6), ('C', 1, 0, 1), ('C', 1, 1, 1), ('WE', 3, 0), ('WE', 3, 2), ('WE', 3, 1), ('WE', 3, 3), ('BC', 1), ('RA', 7), ('RA', 6), ('SA', 8), ('SA', 9), ('C', 2, 0, 0), ('C', 2, 0, 1), ('C', 2, 1, 1), ('C', 2, 1, 0), ('SN', 9), ('SN', 8), ('SB', 9), ('SB', 8), ('RA', 9), ('RA', 8), ('C', 3, 0, 0), ('C', 3, 0, 1), ('SA', 11), ('C', 3, 1, 1), ('C', 3, 1, 0), ('SN', 11), ('SB', 11), ('RA', 10), ('RA', 11), ('SA', 13), ('SA', 12), ('C', 4, 0, 1), ('C', 4, 0, 0), ('C', 4, 1, 0), ('C', 4, 1, 1), ('SN', 12), ('SN', 13), ('SB', 12), ('SB', 13), ('RA', 12), ('RA', 13), ('C', 5, 0, 1), ('C', 5, 0, 0), ('SA', 14), ('C', 5, 1, 0), ('C', 5, 1, 1), ('SN', 14), ('SB', 14), ('RA', 15), ('RA', 14), ('C', 6, 0, 0), ('C', 6, 0, 1), ('C', 6, 1, 1), ('C', 6, 1, 0), ('C', 7, 0, 0), ('C', 7, 0, 1), ('C', 7, 1, 0), ('C', 7, 1, 1)),
+    'V': (('IV',), ('SU', 0), ('SU', 1), ('SV', 0), ('SV', 1), ('SU', 2), ('RB', 0), ('P1', 0), ('P1', 1), ('WBC',), ('WE', 0, 2), ('WE', 0, 3), ('SV', 2), ('WQ', 0, 1), ('WQ', 0, 0), ('RG', 0, 0), ('QZ', 0, 0), ('RB', 1), ('RG', 0, 1), ('SU', 5), ('QZ', 0, 1), ('SU', 4), ('WQ', 1, 1), ('WQ', 1, 0), ('SV', 4), ('SV', 5), ('SU', 7), ('RB', 2), ('WQ', 2, 0), ('F', 0, 0), ('F', 1, 0), ('WQ', 2, 1), ('C', 1, 0, 0), ('C', 1, 1, 0), ('F', 0, 1), ('RG', 1, 0), ('F', 1, 1), ('RG', 1, 1), ('SV', 7), ('WQ', 3, 0), ('WQ', 3, 1), ('F', 0, 2), ('QZ', 1, 0), ('QZ', 1, 1), ('F', 1, 2), ('RB', 3), ('F', 0, 3), ('F', 1, 3), ('SU', 10), ('F', 2, 0), ('F', 2, 1), ('F', 2, 2), ('F', 2, 3), ('F', 3, 0), ('F', 3, 1), ('F', 3, 2), ('QZ', 2, 0), ('QZ', 2, 1), ('RB', 4), ('F', 3, 3), ('SV', 10), ('SU', 15), ('F', 4, 0), ('F', 4, 1), ('F', 4, 2), ('F', 4, 3), ('RG', 3, 1), ('F', 5, 0), ('QZ', 3, 1), ('QZ', 3, 0), ('F', 5, 1), ('RB', 5), ('F', 5, 2), ('F', 5, 3), ('F', 6, 0), ('F', 6, 1), ('F', 6, 2), ('RG', 4, 0), ('F', 6, 3), ('RG', 4, 1), ('F', 7, 0), ('QZ', 4, 1), ('QZ', 4, 0), ('F', 7, 1), ('RB', 6), ('F', 7, 2), ('F', 7, 3), ('F', 8, 0), ('F', 8, 1), ('F', 8, 2), ('F', 8, 3), ('SV', 15), ('F', 9, 0), ('F', 9, 1), ('RG', 5, 1), ('QZ', 5, 0), ('QZ', 5, 1), ('RB', 7), ('F', 9, 2), ('F', 9, 3), ('F', 10, 0), ('F', 10, 1), ('F', 10, 2), ('F', 10, 3), ('F', 11, 0), ('RG', 6, 1), ('QZ', 6, 0), ('QZ', 6, 1), ('F', 11, 1), ('F', 11, 2), ('F', 11, 3), ('F', 12, 0), ('F', 12, 1), ('F', 12, 2), ('F', 12, 3), ('F', 13, 0), ('QZ', 7, 0), ('QZ', 7, 1), ('F', 13, 1), ('F', 13, 2), ('F', 13, 3), ('F', 14, 0), ('F', 14, 1), ('F', 14, 2), ('F', 14, 3), ('F', 15, 0), ('F', 15, 1), ('F', 15, 2), ('F', 15, 3)),
+    'G': (('IG',), ('P1', 2), ('P1', 3), ('P1', 4), ('P1', 5), ('P1', 6), ('RG', 2, 0), ('P1', 7), ('RG', 2, 1), ('P1', 8), ('RG', 3, 0), ('P1', 9), ('P1', 10), ('P1', 11), ('P1', 12), ('RG', 5, 0), ('P1', 13), ('P1', 14), ('RG', 6, 0), ('P1', 15), ('RG', 7, 0), ('RG', 7, 1)),
+    'SP': (('LDX', 0, 0, 1), ('LDX', 0, 1, 1), ('LDX', 1, 0, 2), ('LDW', 0, 0, 2), ('LDW', 0, 2, 2), ('LDW', 1, 0, 4), ('LDX', 2, 0, 2), ('LDW', 2, 0, 4), ('LDX', 3, 0, 2), ('LDW', 3, 0, 4), ('LDX', 4, 0, 2), ('LDX', 5, 0, 2), ('LDX', 6, 0, 2), ('LDX', 7, 0, 2), ('ST', 0, 0), ('ST', 1, 0), ('ST', 0, 1), ('ST', 1, 1), ('ST', 2, 0), ('ST', 2, 1), ('ST', 3, 0), ('ST', 3, 1), ('ST', 4, 0), ('ST', 4, 1), ('ST', 5, 0), ('ST', 5, 1), ('ST', 6, 0), ('ST', 6, 1), ('ST', 7, 0), ('ST', 7, 1), ('ST', 8, 0), ('ST', 8, 1), ('ST', 9, 0), ('ST', 9, 1), ('ST', 10, 0), ('ST', 10, 1), ('ST', 11, 0), ('ST', 11, 1), ('ST', 12, 0), ('ST', 12, 1), ('ST', 13, 0), ('ST', 13, 1), ('ST', 14, 0), ('ST', 14, 1), ('ST', 15, 0), ('ST', 15, 1)),
+}
+
+
+def build_queues():
+    return QUEUES
 
 
 def tile_attentionalpoolerwmasking_pa_kernel(tc, x, ln_k_w, ln_k_b, Wk, Wv, bk, bv, out_0, out_1):
@@ -57,254 +44,363 @@ def tile_attentionalpoolerwmasking_pa_kernel(tc, x, ln_k_w, ln_k_b, Wk, Wv, bk, 
     xf = x.flatten_outer_dims()
     outs = (out_0.flatten_outer_dims(), out_1.flatten_outer_dims())
     with ExitStack() as ctx:
-        if PINNED:
-            ctx.enter_context(tc.manual_schedule())
+        ctx.enter_context(tc.manual_schedule())
         const = ctx.enter_context(tc.tile_pool(name="const", bufs=1))
-        small = ctx.enter_context(tc.tile_pool(name="small", bufs=8))
-        xhp = ctx.enter_context(tc.tile_pool(name="xhp", bufs=8))
+        xhp = ctx.enter_context(tc.tile_pool(name="xhp", bufs=XH_BUFS))
         work = ctx.enter_context(tc.tile_pool(name="work", bufs=2))
-        grpp = ctx.enter_context(tc.tile_pool(name="grpp", bufs=3))
-        ostp = ctx.enter_context(tc.tile_pool(name="ostp", bufs=6))
+        planp = ctx.enter_context(tc.tile_pool(name="planp", bufs=PLAN_BUFS))
+        grpp = ctx.enter_context(tc.tile_pool(name="grpp", bufs=4))
+        ostv = ctx.enter_context(tc.tile_pool(name="ostv", bufs=OSTV_BUFS))
+        osts = ctx.enter_context(tc.tile_pool(name="osts", bufs=OSTS_BUFS))
         pst = ctx.enter_context(tc.psum_pool(name="pst", bufs=4))
         pso = ctx.enter_context(tc.psum_pool(name="pso", bufs=4))
 
         vecs = const.tile([P, 256], BF16, name="vecs")
-        nc.vector.memset(vecs[:], 0.0)
-        nc.sync.dma_start(out=vecs[0:4, :], in_=ln_k_w.rearrange("(v q) -> v q", v=4))
-        nc.sync.dma_start(out=vecs[4:8, :], in_=ln_k_b.rearrange("(v q) -> v q", v=4))
         brow = const.tile([P, 2048], BF16, name="brow")
-        nc.vector.memset(brow[:], 0.0)
-        nc.sync.dma_start(out=brow[0:1, 0:1024], in_=bk.rearrange("(o d) -> o d", o=1))
-        nc.sync.dma_start(out=brow[0:1, 1024:2048], in_=bv.rearrange("(o d) -> o d", o=1))
         ones = const.tile([P, P], BF16, name="ones")
-        nc.vector.memset(ones[:], 1.0)
         zero_t = const.tile([P, 1], F32, name="zero_t")
-        nc.vector.memset(zero_t[:], 0.0)
         eps_t = const.tile([P, 1], F32, name="eps_t")
-        nc.vector.tensor_scalar(out=eps_t[:], in0=zero_t[:], scalar1=EPS, scalar2=None, op0=ALU.add)
         warm = const.tile([P, 1], F32, name="warm")
-        nc.scalar.activation(out=warm[:], in_=eps_t[:], func=ACT.Sqrt)
         ident = const.tile([P, P], F32, name="ident")
-        make_identity(nc, ident[:])
-
-        xts = [const.tile([P, nt, C], BF16, name="xt%d" % gi) for gi, (t0, nt) in enumerate(PREP)]
-        wts = [const.tile([P, 4, C], BF16, name="wt%d" % c) for c in range(4)]
-        bias_bc = const.tile([P, 2048], BF16, name="bias_bc")
-
-        def load_x(gi):
-            t0, nt = PREP[gi]
-            nc.sync.dma_start(
-                out=xts[gi][:], in_=xf[P * t0 : P * (t0 + nt), :].rearrange("(n p) c -> p n c", p=P)
-            )
-
-        def load_w(c):
-            src = Wk if c < 2 else Wv
-            r0 = 512 * (c % 2)
-            nc.sync.dma_start(out=wts[c][:], in_=src[r0 : r0 + 512, :].rearrange("(n p) c -> p n c", p=P))
-
-        for kind, i in LOADS:
-            if kind == "x":
-                load_x(i)
-            else:
-                load_w(i)
-
-        vb = pst.tile([P, 512], F32, tag="tp", name="vb")
-        nc.tensor.transpose(vb[:, 0:P], vecs[:].bitcast(F32), ident[:])
         wb = const.tile([P, 16], F32, name="wb")
-        nc.vector.tensor_copy(out=wb[:], in_=vb[:, 0:8].bitcast(BF16))
-        for c in range(4):
-            bb = pst.tile([P, 512], F32, tag="tp", name="bb")
-            nc.tensor.matmul(out=bb[:], lhsT=ones[:], rhs=brow[:, 512 * c : 512 * c + 512], start=True, stop=True)
-            nc.scalar.copy(out=bias_bc[:, 512 * c : 512 * c + 512], in_=bb[:])
-
+        bias_bc = const.tile([P, 2048], BF16, name="bias_bc")
+        xts = [const.tile([P, 2, C], BF16, name="xt%d" % j) for j in range(NG)]
+        wts = [const.tile([P, 4, C], BF16, name="wt%d" % c) for c in range(4)]
         wq = const.tile([P, 2, 2048], U32, name="wq", align_bytes=64)
         ws = const.tile([P, 2, 2048], U8, name="ws", align_bytes=64)
-        gws = {}
+        xq = [const.tile([P, 2, 256], U32, name="xq%d" % j, align_bytes=64) for j in range(NG)]
+        xs = [const.tile([P, 2, 256], U8, name="xs%d" % j, align_bytes=64) for j in range(NG)]
+        mv = [const.tile([P, 2], F32, name="mv%d" % i) for i in range(16)]
+        st6 = [const.tile([P, 2, 6], F32, name="st%d" % i) for i in range(16)]
+        nm = [const.tile([P, 1], F32, name="nm%d" % i) for i in range(16)]
+        sm = [const.tile([P, 1], F32, name="sm%d" % i) for i in range(16)]
+        sq = [const.tile([P, 1], F32, name="sq%d" % i) for i in range(16)]
+        std = [const.tile([P, 2], F32, name="std%d" % j) for j in range(NG)]
+        rstd = [const.tile([P, 2], F32, name="rstd%d" % j) for j in range(NG)]
+        live = {}
 
-        def wt_tile(c, n):
-            if n == 0:
-                gws[c] = work.tile([P, 2, 2048], BF16, tag="gw", name="gw", align_bytes=64)
-            gw32 = gws[c][:].bitcast(F32).rearrange("p g (d u) -> p g d u", u=2)
+        def t_init_v():
+            nc.vector.memset(vecs[:], 0.0)
+            nc.vector.memset(zero_t[:], 0.0)
+            nc.vector.tensor_scalar(out=eps_t[:], in0=zero_t[:], scalar1=EPS, scalar2=None, op0=ALU.add)
+            nc.vector.memset(brow[:], 0.0)
+            nc.vector.memset(ones[:], 1.0)
+
+        def t_init_s():
+            nc.scalar.activation(out=warm[:], in_=eps_t[:], func=ACT.Sqrt)
+
+        def t_init_g():
+            make_identity(nc, ident[:])
+
+        def t_ldv():
+            q = nc.scalar if SMALL_ON_S else nc.sync
+            q.dma_start(out=vecs[0:4, :], in_=ln_k_w.rearrange("(v q) -> v q", v=4))
+            q.dma_start(out=vecs[4:8, :], in_=ln_k_b.rearrange("(v q) -> v q", v=4))
+
+        def t_ldb():
+            q = nc.scalar if SMALL_ON_S else nc.sync
+            q.dma_start(out=brow[0:1, 0:1024], in_=bk.rearrange("(o d) -> o d", o=1))
+            q.dma_start(out=brow[0:1, 1024:2048], in_=bv.rearrange("(o d) -> o d", o=1))
+
+        def t_ldx(j, n0, nn):
+            r0 = P * (2 * j + n0)
+            nc.sync.dma_start(
+                out=xts[j][:, n0 : n0 + nn, :], in_=xf[r0 : r0 + P * nn, :].rearrange("(n p) c -> p n c", p=P)
+            )
+
+        def t_ldw(c, n0, nn):
+            src = Wk if c < 2 else Wv
+            r0 = 512 * (c % 2) + P * n0
+            nc.sync.dma_start(
+                out=wts[c][:, n0 : n0 + nn, :], in_=src[r0 : r0 + P * nn, :].rearrange("(n p) c -> p n c", p=P)
+            )
+
+        def t_vb():
+            bank = pst.tile([P, 512], F32, tag="tp", name="vb")
+            live[("vb",)] = bank
+            nc.tensor.transpose(bank[:, 0:P], vecs[:].bitcast(F32), ident[:])
+
+        def t_wbc():
+            nc.vector.tensor_copy(out=wb[:], in_=live[("vb",)][:, 0:8].bitcast(BF16))
+
+        def t_bb(h):
+            bank = pst.tile([P, 1024], BF16, tag="tp", name="bb")
+            live[("bb", h)] = bank
+            for c in range(2):
+                o = 1024 * h + 512 * c
+                nc.tensor.matmul(
+                    out=bank[:, 512 * c : 512 * c + 512], lhsT=ones[:], rhs=brow[:, o : o + 512], start=True, stop=True
+                )
+
+        def t_bc(h):
+            dst = bias_bc[:, 1024 * h : 1024 * h + 1024]
+            if ("BC", h) in ON_V:
+                nc.vector.tensor_copy(out=dst, in_=live[("bb", h)][:])
+            else:
+                nc.scalar.copy(out=dst, in_=live[("bb", h)][:])
+
+        def t_wt(c, n):
             bank = pst.tile([P, 512], F32, tag="tp", name="wbank")
+            live[("wt", c, n)] = bank
             w32 = wts[c][:, n, :].bitcast(F32)
             for v in range(4):
                 nc.tensor.transpose(bank[:, P * v : P * v + P], w32[:, P * v : P * v + P], ident[:])
+
+        def t_we(c, n):
+            if ("gw", c) not in live:
+                live[("gw", c)] = work.tile([P, 2, 2048], BF16, tag="gw", name="gw", align_bytes=64)
+            gw32 = live[("gw", c)][:].bitcast(F32).rearrange("p g (d u) -> p g d u", u=2)
             dst = gw32[:, :, P * n : P * n + P, :]
-            src = bank[:].rearrange("p (g u d) -> p g d u", g=2, u=2)
-            if n in W_EVAC_V[c]:
+            src = live[("wt", c, n)][:].rearrange("p (g u d) -> p g d u", g=2, u=2)
+            if ("WE", c, n) in ON_V:
                 nc.vector.tensor_copy(out=dst, in_=src)
             else:
                 nc.scalar.copy(out=dst, in_=src)
 
-        def wq_chunk(c):
-            for g in range(2):
-                nc.vector.quantize_mx(
-                    out=wq[:, g, 512 * c : 512 * c + 512].bitcast(FP8X4),
-                    scales=ws[:, g, 512 * c : 512 * c + 512],
-                    in_=gws[c][:, g, :],
-                )
+        def t_wq(c, g):
+            nc.vector.quantize_mx(
+                out=wq[:, g, 512 * c : 512 * c + 512].bitcast(FP8X4),
+                scales=ws[:, g, 512 * c : 512 * c + 512],
+                in_=live[("gw", c)][:, g, :],
+            )
 
-        st8 = [{} for gi in range(len(PREP))]
-
-        def stats_open(gi):
-            nt = PREP[gi][1]
-            s = st8[gi]
-            if NV[gi] > 0:
-                s["mv"] = small.tile([P, 4, 2], F32, tag="mv", name="mv")
-                s["nmv"] = small.tile([P, 4], F32, tag="nmv", name="nmv")
-            if NV[gi] < nt:
-                s["sm"] = small.tile([P, 4], F32, tag="sm", name="sm")
-                s["nms"] = small.tile([P, 4], F32, tag="nms", name="nms")
-                s["sq"] = small.tile([P, 4], F32, tag="sq", name="sq")
-            s["std"] = small.tile([P, 4], F32, tag="std", name="std")
-            s["rstd"] = small.tile([P, 4], F32, tag="rstd", name="rstd")
-            s["xh"] = [None] * nt
-
-        def stats_v(gi, n):
-            st = small.tile([P, 2, 6], F32, tag="st", name="st", bufs=4)
+        def t_su(i):
             for h in range(2):
-                nc.vector.bn_stats(out=st[:, h, :], in_=xts[gi][:, n, 512 * h : 512 * h + 512])
-            nc.vector.bn_aggr(out=st8[gi]["mv"][:, n, :], in_=st[:].rearrange("p a b -> p (a b)"))
+                nc.vector.bn_stats(out=st6[i][:, h, :], in_=xts[i // 2][:, i % 2, 512 * h : 512 * h + 512])
 
-        def stats_s_a(gi, n):
+        def t_sv(i):
+            nc.vector.bn_aggr(out=mv[i][:], in_=st6[i][:].rearrange("p a b -> p (a b)"))
+
+        def t_sa(i):
+            junk = work.tile([P, C], BF16, tag="junk", name="junk")
+            nc.scalar.activation(out=junk[:], in_=xts[i // 2][:, i % 2, :], func=ACT.Identity, accum_out=sm[i][:])
+
+        def t_sn(i):
+            nc.scalar.mul(out=nm[i][:], in_=sm[i][:], mul=-1.0 / C)
+
+        def t_sb(i):
             junk = work.tile([P, C], BF16, tag="junk", name="junk")
             nc.scalar.activation(
-                out=junk[:], in_=xts[gi][:, n, :], func=ACT.Identity, accum_out=st8[gi]["sm"][:, n : n + 1]
+                out=junk[:], in_=xts[i // 2][:, i % 2, :], func=ACT.Square, bias=nm[i][:], scale=1.0,
+                accum_out=sq[i][:],
             )
 
-        def stats_s_nm(gi):
-            nv, nt = NV[gi], PREP[gi][1]
-            nc.scalar.mul(out=st8[gi]["nms"][:, nv:nt], in_=st8[gi]["sm"][:, nv:nt], mul=-1.0 / C)
+        def t_ra(i):
+            dst = std[i // 2][:, i % 2 : i % 2 + 1]
+            if i in STAT_V:
+                nc.scalar.activation(out=dst, in_=mv[i][:, 1:2], func=ACT.Sqrt, bias=eps_t[:], scale=1.0)
+            else:
+                nc.scalar.activation(out=dst, in_=sq[i][:], func=ACT.Sqrt, bias=eps_t[:], scale=1.0 / C)
 
-        def stats_s_b(gi, n):
-            junk = work.tile([P, C], BF16, tag="junk", name="junk")
-            nc.scalar.activation(
-                out=junk[:], in_=xts[gi][:, n, :], func=ACT.Square, bias=st8[gi]["nms"][:, n : n + 1], scale=1.0,
-                accum_out=st8[gi]["sq"][:, n : n + 1],
-            )
+        def t_rb(j):
+            nc.vector.reciprocal(out=rstd[j][:], in_=std[j][:])
 
-        def rstd_a(gi):
-            nv, nt = NV[gi], PREP[gi][1]
-            s = st8[gi]
-            if nv > 0:
-                nc.vector.tensor_scalar(
-                    out=s["nmv"][:, 0:nv], in0=s["mv"][:, 0:nv, 0], scalar1=-1.0, scalar2=None, op0=ALU.mult
-                )
-                nc.scalar.activation(
-                    out=s["std"][:, 0:nv], in_=s["mv"][:, 0:nv, 1], func=ACT.Sqrt, bias=eps_t[:], scale=1.0
-                )
-            if nv < nt:
-                nc.scalar.activation(
-                    out=s["std"][:, nv:nt], in_=s["sq"][:, nv:nt], func=ACT.Sqrt, bias=eps_t[:], scale=1.0 / C
-                )
-
-        def rstd_b(gi):
-            nt = PREP[gi][1]
-            nc.vector.reciprocal(out=st8[gi]["rstd"][:, 0:nt], in_=st8[gi]["std"][:, 0:nt])
-
-        def p1(gi, n):
-            s = st8[gi]
-            nm = s["nmv"] if n < NV[gi] else s["nms"]
+        def t_p1(i):
             xh = xhp.tile([P, 8, P], F32, tag="xh", name="xh")
-            eng = nc.gpsimd if P1_ON_G[gi] else nc.vector
+            live[("xh", i)] = xh
+            eng = nc.vector if ("P1", i) in ON_V else nc.gpsimd
             eng.tensor_scalar(
                 out=xh[:].rearrange("p (v e) q -> p v e q", e=2),
-                in0=xts[gi][:, n, :].rearrange("p (v q e) -> p v e q", v=4, e=2),
-                scalar1=nm[:, n : n + 1],
-                scalar2=s["rstd"][:, n : n + 1],
-                op0=ALU.add,
+                in0=xts[i // 2][:, i % 2, :].rearrange("p (v q e) -> p v e q", v=4, e=2),
+                scalar1=mv[i][:, 0:1] if i in STAT_V else nm[i][:],
+                scalar2=rstd[i // 2][:, i % 2 : i % 2 + 1],
+                op0=ALU.subtract if i in STAT_V else ALU.add,
                 op1=ALU.mult,
             )
-            s["xh"][n] = xh
 
-        def xt_half(gi, g):
-            nt = PREP[gi][1]
-            ntok = P * nt
-            ppb = 512 // ntok
-            s = st8[gi]
-            if g == 0:
-                s["plan"] = work.tile([P, 8, ntok], BF16, tag="plan%d" % nt, name="plan")
-                s["xq"] = work.tile([P, 2, ntok], U32, tag="xq%d" % nt, name="xq", align_bytes=64, bufs=4)
-                s["xs"] = work.tile([P, 2, ntok], U8, tag="xs%d" % nt, name="xs", align_bytes=64, bufs=4)
-            for b in range(4 // ppb):
-                bank = pst.tile([P, 512], F32, tag="tp", name="xbank")
-                for a in range(ppb):
-                    pl = 4 * g + ppb * b + a
-                    for n in range(nt):
-                        o = ntok * a + P * n
-                        nc.tensor.transpose(bank[:, o : o + P], s["xh"][n][:, pl, :], ident[:])
-                for a in range(ppb):
-                    pl = 4 * g + ppb * b + a
+        def t_t(j, g, b):
+            bank = pst.tile([P, 512], F32, tag="tp", name="xbank")
+            live[("xb", j, g, b)] = bank
+            for a in range(2):
+                pl = 4 * g + 2 * b + a
+                for n in range(2):
+                    o = 256 * a + P * n
+                    nc.tensor.transpose(bank[:, o : o + P], live[("xh", 2 * j + n)][:, pl, :], ident[:])
+
+        def t_c(j, g, b):
+            if ("plan", j) not in live:
+                live[("plan", j)] = planp.tile([P, 8, 256], BF16, tag="plan", name="plan")
+            bank = live[("xb", j, g, b)]
+            for a in range(2):
+                pl = 4 * g + 2 * b + a
+                dst = live[("plan", j)][:, pl, :]
+                src = bank[:, 256 * a : 256 * a + 256]
+                if ("C", j, g, b) in ON_V:
+                    nc.vector.tensor_scalar(
+                        out=dst, in0=src, scalar1=wb[:, pl : pl + 1], scalar2=wb[:, 8 + pl : 9 + pl],
+                        op0=ALU.mult, op1=ALU.add,
+                    )
+                else:
                     nc.scalar.activation(
-                        out=s["plan"][:, pl, :], in_=bank[:, ntok * a : ntok * a + ntok], func=ACT.Identity,
-                        scale=wb[:, pl : pl + 1], bias=wb[:, 8 + pl : 9 + pl],
+                        out=dst, in_=src, func=ACT.Identity, scale=wb[:, pl : pl + 1], bias=wb[:, 8 + pl : 9 + pl]
                     )
 
-        def rq(gi, g):
-            ntok = P * PREP[gi][1]
-            s = st8[gi]
-            grp = grpp.tile([P, ntok, 4], BF16, tag="grp%d" % ntok, name="grp", align_bytes=64)
-            nc.vector.tensor_copy(
-                out=grp[:].rearrange("p (c i) t -> p c t i", i=4),
-                in_=s["plan"][:, 4 * g : 4 * g + 4, :].rearrange("p t (c i) -> p c t i", i=4),
-            )
+        def t_rg(j, g):
+            grp = grpp.tile([P, 256, 4], BF16, tag="grp", name="grp", align_bytes=64)
+            live[("grp", j, g)] = grp
+            if ("RG", j, g) in ON_G:
+                nc.gpsimd.tensor_scalar(
+                    out=grp[:],
+                    in0=live[("plan", j)][:, 4 * g : 4 * g + 4, :].rearrange("p t r -> p r t"),
+                    scalar1=1.0, scalar2=0.0, op0=ALU.mult, op1=ALU.add,
+                )
+            else:
+                nc.vector.tensor_copy(
+                    out=grp[:].rearrange("p (c i) t -> p c t i", i=4),
+                    in_=live[("plan", j)][:, 4 * g : 4 * g + 4, :].rearrange("p t (c i) -> p c t i", i=4),
+                )
+
+        def t_qz(j, g):
             nc.vector.quantize_mx(
-                out=s["xq"][:, g, :].bitcast(FP8X4),
-                scales=s["xs"][:, g, :],
-                in_=grp[:].rearrange("p r t -> p (r t)"),
+                out=xq[j][:, g, :].bitcast(FP8X4),
+                scales=xs[j][:, g, :],
+                in_=live[("grp", j, g)][:].rearrange("p r t -> p (r t)"),
             )
 
-        where = {}
-        for gi, (t0, nt) in enumerate(PREP):
-            for n in range(nt):
-                where[t0 + n] = (gi, n)
-        osts = {}
-
-        def mb(tile_i, half, j):
-            gi, n = where[tile_i]
-            s = st8[gi]
-            if (tile_i, half) not in osts:
-                osts[(tile_i, half)] = [ostp.tile([P, 1024], F32, tag="ost", name="ost"), 0]
-            ost = osts[(tile_i, half)][0]
-            osts[(tile_i, half)][1] += 1
-            ch = 2 * half + j
+        def t_m(i, ch):
             acc = pso.tile([P, 512], F32, tag="acc", name="acc")
+            live[("acc", i, ch)] = acc
+            j, n = i // 2, i % 2
             for g in range(2):
                 nc.tensor.matmul_mx(
                     out=acc[:],
-                    lhsT=s["xq"][:, g, P * n : P * n + P].bitcast(FP8X4),
-                    lhsT_scale=s["xs"][:, g, P * n : P * n + P],
+                    lhsT=xq[j][:, g, P * n : P * n + P].bitcast(FP8X4),
+                    lhsT_scale=xs[j][:, g, P * n : P * n + P],
                     rhs=wq[:, g, 512 * ch : 512 * ch + 512].bitcast(FP8X4),
                     rhs_scale=ws[:, g, 512 * ch : 512 * ch + 512],
                     start=(g == 0),
                     stop=(g == 1),
                 )
-            o = ost[:, 512 * j : 512 * j + 512]
-            b = bias_bc[:, 512 * ch : 512 * ch + 512]
-            if (tile_i, half, j) in F_ON_S:
-                nc.scalar.copy(out=o, in_=acc[:])
-                nc.gpsimd.tensor_tensor(out=o, in0=o, in1=b, op=ALU.add)
+
+        def t_f(i, ch):
+            half = ch // 2
+            on_s = (i, half) in F_ON_S
+            if ("ost", i, half) not in live:
+                pool = osts if on_s else ostv
+                live[("ost", i, half)] = pool.tile([P, 1024], F32, tag="ost", name="ost")
+            o = live[("ost", i, half)][:, 512 * (ch % 2) : 512 * (ch % 2) + 512]
+            if on_s:
+                nc.scalar.copy(out=o, in_=live[("acc", i, ch)][:])
             else:
-                nc.vector.tensor_tensor(out=o, in0=acc[:], in1=b, op=ALU.add)
-            if osts[(tile_i, half)][1] == 2:
-                nc.sync.dma_start(out=outs[half][P * tile_i : P * tile_i + P, :], in_=ost[:])
+                nc.vector.tensor_tensor(
+                    out=o, in0=live[("acc", i, ch)][:], in1=bias_bc[:, 512 * ch : 512 * ch + 512], op=ALU.add
+                )
 
-        def run(tasks):
-            for t in tasks:
-                t[0](*t[1:])
+        def t_a(i, half):
+            o = live[("ost", i, half)]
+            nc.gpsimd.tensor_tensor(out=o[:], in0=o[:], in1=bias_bc[:, 1024 * half : 1024 * half + 1024], op=ALU.add)
 
-        def stats_s_tasks(gi):
-            nv, nt = NV[gi], PREP[gi][1]
-            return (
-                [(stats_s_a, gi, n) for n in range(nv, nt)]
-                + ([(stats_s_nm, gi)] if nv < nt else [])
-                + [(stats_s_b, gi, n) for n in range(nv, nt)]
-            )
+        def t_st(i, half):
+            nc.sync.dma_start(out=outs[half][P * i : P * i + P, :], in_=live[("ost", i, half)][:])
 
-        NG = len(PREP)
-        fn = {"sv": stats_v, "ra": rstd_a, "rb": rstd_b, "p1": p1, "wt": wt_tile, "wq": wq_chunk, "xt": xt_half,
-              "rq": rq, "sa": stats_s_a, "sn": stats_s_nm, "sb": stats_s_b, "mb": mb}
-        for gi in range(NG):
-            stats_open(gi)
-        for t in FLAT:
-            fn[t[0]](*t[1:])
+        fn = {"IV": t_init_v, "IS": t_init_s, "IG": t_init_g, "LDV": t_ldv, "LDB": t_ldb, "LDX": t_ldx, "LDW": t_ldw,
+              "VB": t_vb, "WBC": t_wbc, "BB": t_bb, "BC": t_bc, "WT": t_wt, "WE": t_we, "WQ": t_wq, "SU": t_su, "SV": t_sv,
+              "SA": t_sa, "SN": t_sn, "SB": t_sb, "RA": t_ra, "RB": t_rb, "P1": t_p1, "T": t_t, "C": t_c, "RG": t_rg,
+              "QZ": t_qz, "M": t_m, "F": t_f, "A": t_a, "ST": t_st}
+
+        queues = build_queues()
+
+        need = {}
+
+        def after(key, *others):
+            need[key] = need.get(key, []) + [o for o in others]
+
+        ldx_of = {}
+        ldw_of = {}
+        for k in queues["SP"]:
+            if k[0] == "LDX":
+                for n in range(k[2], k[2] + k[3]):
+                    ldx_of[2 * k[1] + n] = k
+            if k[0] == "LDW":
+                for n in range(k[2], k[2] + k[3]):
+                    ldw_of[(k[1], n)] = k
+        after(("IS",), ("IV",))
+        after(("LDV",), ("IV",))
+        after(("LDB",), ("IV",))
+        after(("VB",), ("LDV",), ("IG",))
+        after(("WBC",), ("VB",))
+        for h in range(2):
+            after(("BB", h), ("LDB",))
+            after(("BC", h), ("BB", h))
+        for c in range(4):
+            for n in range(4):
+                after(("WT", c, n), ldw_of[(c, n)], ("IG",))
+                after(("WE", c, n), ("WT", c, n))
+                if c >= 2:
+                    after(("WE", c, n), ("WQ", c - 2, 0), ("WQ", c - 2, 1))
+                if c >= 1:
+                    after(("WE", c, n), ("WE", c - 1, 0))
+            for g in range(2):
+                after(("WQ", c, g), *[("WE", c, n) for n in range(4)])
+        for i in range(16):
+            j = i // 2
+            after(("SU", i), ldx_of[i])
+            after(("SV", i), ("SU", i))
+            after(("SA", i), ldx_of[i], ("IS",))
+            after(("SN", i), ("SA", i))
+            after(("SB", i), ("SN", i))
+            after(("RA", i), ("SV", i) if i in STAT_V else ("SB", i), ("IS",))
+            after(("RB", j), ("RA", i))
+            after(("P1", i), ("RB", j))
+            if i >= 1:
+                after(("P1", i), ("P1", i - 1))
+            if i >= XH_BUFS:
+                after(("P1", i), *[("T", (i - XH_BUFS) // 2, g, b) for g in range(2) for b in range(2)])
+            for ch in range(4):
+                after(("M", i, ch), ("QZ", j, 0), ("QZ", j, 1), ("WQ", ch, 0), ("WQ", ch, 1))
+                after(("F", i, ch), ("M", i, ch), ("BC", ch // 2))
+            for half in range(2):
+                fs = [("F", i, 2 * half), ("F", i, 2 * half + 1)]
+                if (i, half) in F_ON_S:
+                    after(("A", i, half), ("BC", half), *fs)
+                    after(("ST", i, half), ("A", i, half))
+                else:
+                    after(("ST", i, half), *fs)
+        for j in range(NG):
+            for g in range(2):
+                for b in range(2):
+                    after(("T", j, g, b), ("P1", 2 * j), ("P1", 2 * j + 1))
+                    after(("C", j, g, b), ("T", j, g, b), ("WBC",))
+                    if j >= 1:
+                        after(("C", j, g, b), ("C", j - 1, 0, 0))
+                    if j >= PLAN_BUFS:
+                        after(("C", j, g, b), ("RG", j - PLAN_BUFS, 0), ("RG", j - PLAN_BUFS, 1))
+                    after(("RG", j, g), ("C", j, g, b))
+                after(("QZ", j, g), ("RG", j, g))
+                prev = (j, 0) if g == 1 else (j - 1, 1)
+                if prev[0] >= 0:
+                    after(("RG", j, g), ("RG", prev[0], prev[1]))
+                if j >= 2:
+                    after(("RG", j, g), ("QZ", j - 2, g))
+        evac = {"VB": "WBC", "BB": "BC", "WT": "WE", "T": "C", "M": "F"}
+        ring = {"tp": [], "acc": []}
+        for k in queues["PE"]:
+            r = ring["acc" if k[0] == "M" else "tp"]
+            if len(r) >= 4:
+                after(k, r[len(r) - 4])
+            r.append((evac[k[0]],) + k[1:])
+        for eng, bufs in (("V", OSTV_BUFS), ("S", OSTS_BUFS)):
+            r = []
+            for k in queues[eng]:
+                if k[0] == "F" and ("ST", k[1], k[2] // 2) not in r:
+                    if len(r) >= bufs:
+                        after(k, r[len(r) - bufs])
+                    r.append(("ST", k[1], k[2] // 2))
+
+        order = ("SP", "PE", "S", "V", "G")
+        pos = {e: 0 for e in order}
+        done = set()
+        total = sum(len(queues[e]) for e in order)
+        while len(done) < total:
+            moved = False
+            for e in order:
+                while pos[e] < len(queues[e]):
+                    k = queues[e][pos[e]]
+                    if not all(o in done for o in need.get(k, [])):
+                        break
+                    fn[k[0]](*k[1:])
+                    done.add(k)
+                    pos[e] += 1
+                    moved = True
+            if not moved:
+                raise ValueError("queues wait for each other: %s" % str([queues[e][pos[e]] for e in order if pos[e] < len(queues[e])]))

@@ -19,18 +19,19 @@ NG = 8
 
 XH_BUFS = 6
 PLAN_BUFS = 3
-OSTV_BUFS = 6
-OSTS_BUFS = 2
+OSTV_BUFS = 5
+OSTS_BUFS = 3
 SMALL_ON_S = True
-STAT_V = (0, 1, 2, 4, 5, 7, 10, 15)
+STAT_V = (0, 1, 2, 3, 4, 5, 7, 8, 9, 10)
 F_ON_S = ()
-ON_V = (('P1', 0), ('P1', 1), ('WE', 0, 2), ('WE', 0, 3), ('C', 1, 0, 0), ('C', 1, 1, 0))
-ON_G = (('RG', 2, 0), ('RG', 3, 0), ('RG', 5, 0), ('RG', 7, 0), ('RG', 7, 1), ('RG', 2, 1), ('RG', 6, 0))
+ON_V = (('P1', 0), ('P1', 1), ('P1', 2), ('C', 1, 1, 0))
+ON_G = ()
+ON_S = (('RG', 6, 1), ('RG', 3, 1), ('RG', 6, 0), ('RG', 7, 0), ('RG', 2, 0), ('RG', 7, 1))
 QUEUES = {
-    'PE': (('WT', 0, 0), ('WT', 0, 1), ('VB',), ('WT', 0, 2), ('WT', 0, 3), ('T', 0, 0, 0), ('T', 0, 0, 1), ('T', 0, 1, 0), ('T', 0, 1, 1), ('BB', 0), ('WT', 1, 0), ('WT', 1, 1), ('WT', 1, 2), ('WT', 1, 3), ('WT', 2, 0), ('WT', 2, 1), ('WT', 2, 2), ('WT', 2, 3), ('M', 0, 0), ('M', 1, 0), ('M', 0, 1), ('M', 1, 1), ('T', 1, 0, 0), ('T', 1, 0, 1), ('T', 1, 1, 0), ('T', 1, 1, 1), ('WT', 3, 0), ('WT', 3, 1), ('WT', 3, 2), ('WT', 3, 3), ('BB', 1), ('M', 0, 2), ('M', 1, 2), ('M', 0, 3), ('M', 1, 3), ('T', 2, 0, 0), ('T', 2, 0, 1), ('T', 2, 1, 0), ('T', 2, 1, 1), ('M', 2, 0), ('M', 2, 1), ('M', 2, 2), ('M', 2, 3), ('M', 3, 0), ('M', 3, 1), ('M', 3, 2), ('M', 3, 3), ('T', 3, 0, 0), ('T', 3, 0, 1), ('T', 3, 1, 0), ('T', 3, 1, 1), ('M', 4, 0), ('M', 4, 1), ('M', 4, 2), ('M', 4, 3), ('M', 5, 0), ('M', 5, 1), ('M', 5, 2), ('M', 5, 3), ('T', 4, 0, 0), ('T', 4, 0, 1), ('T', 4, 1, 0), ('T', 4, 1, 1), ('M', 6, 0), ('M', 6, 1), ('M', 6, 2), ('M', 6, 3), ('M', 7, 0), ('M', 7, 1), ('M', 7, 2), ('M', 7, 3), ('T', 5, 0, 0), ('T', 5, 0, 1), ('T', 5, 1, 0), ('T', 5, 1, 1), ('M', 8, 0), ('M', 8, 1), ('M', 8, 2), ('M', 8, 3), ('M', 9, 0), ('M', 9, 1), ('M', 9, 2), ('M', 9, 3), ('T', 6, 0, 0), ('T', 6, 0, 1), ('T', 6, 1, 0), ('T', 6, 1, 1), ('M', 10, 0), ('M', 10, 1), ('M', 10, 2), ('M', 10, 3), ('M', 11, 0), ('M', 11, 1), ('M', 11, 2), ('M', 11, 3), ('T', 7, 0, 0), ('T', 7, 0, 1), ('T', 7, 1, 0), ('T', 7, 1, 1), ('M', 12, 0), ('M', 12, 1), ('M', 12, 2), ('M', 12, 3), ('M', 13, 0), ('M', 13, 1), ('M', 13, 2), ('M', 13, 3), ('M', 14, 0), ('M', 14, 1), ('M', 14, 2), ('M', 14, 3), ('M', 15, 0), ('M', 15, 1), ('M', 15, 2), ('M', 15, 3)),
-    'S': (('IS',), ('LDV',), ('LDB',), ('SA', 3), ('RA', 0), ('RA', 1), ('SN', 3), ('WE', 0, 0), ('WE', 0, 1), ('SB', 3), ('C', 0, 0, 0), ('C', 0, 0, 1), ('C', 0, 1, 0), ('C', 0, 1, 1), ('RA', 2), ('RA', 3), ('BC', 0), ('WE', 1, 0), ('WE', 1, 1), ('WE', 1, 2), ('WE', 1, 3), ('WE', 2, 0), ('WE', 2, 1), ('WE', 2, 2), ('WE', 2, 3), ('RA', 5), ('RA', 4), ('SA', 6), ('SN', 6), ('SB', 6), ('C', 1, 0, 1), ('C', 1, 1, 1), ('WE', 3, 0), ('WE', 3, 2), ('WE', 3, 1), ('WE', 3, 3), ('BC', 1), ('RA', 7), ('RA', 6), ('SA', 8), ('SA', 9), ('C', 2, 0, 0), ('C', 2, 0, 1), ('C', 2, 1, 1), ('C', 2, 1, 0), ('SN', 9), ('SN', 8), ('SB', 9), ('SB', 8), ('RA', 9), ('RA', 8), ('C', 3, 0, 0), ('C', 3, 0, 1), ('SA', 11), ('C', 3, 1, 1), ('C', 3, 1, 0), ('SN', 11), ('SB', 11), ('RA', 10), ('RA', 11), ('SA', 13), ('SA', 12), ('C', 4, 0, 1), ('C', 4, 0, 0), ('C', 4, 1, 0), ('C', 4, 1, 1), ('SN', 12), ('SN', 13), ('SB', 12), ('SB', 13), ('RA', 12), ('RA', 13), ('C', 5, 0, 1), ('C', 5, 0, 0), ('SA', 14), ('C', 5, 1, 0), ('C', 5, 1, 1), ('SN', 14), ('SB', 14), ('RA', 15), ('RA', 14), ('C', 6, 0, 0), ('C', 6, 0, 1), ('C', 6, 1, 1), ('C', 6, 1, 0), ('C', 7, 0, 0), ('C', 7, 0, 1), ('C', 7, 1, 0), ('C', 7, 1, 1)),
-    'V': (('IV',), ('SU', 0), ('SU', 1), ('SV', 0), ('SV', 1), ('SU', 2), ('RB', 0), ('P1', 0), ('P1', 1), ('WBC',), ('WE', 0, 2), ('WE', 0, 3), ('SV', 2), ('WQ', 0, 1), ('WQ', 0, 0), ('RG', 0, 0), ('QZ', 0, 0), ('RB', 1), ('RG', 0, 1), ('SU', 5), ('QZ', 0, 1), ('SU', 4), ('WQ', 1, 1), ('WQ', 1, 0), ('SV', 4), ('SV', 5), ('SU', 7), ('RB', 2), ('WQ', 2, 0), ('F', 0, 0), ('F', 1, 0), ('WQ', 2, 1), ('C', 1, 0, 0), ('C', 1, 1, 0), ('F', 0, 1), ('RG', 1, 0), ('F', 1, 1), ('RG', 1, 1), ('SV', 7), ('WQ', 3, 0), ('WQ', 3, 1), ('F', 0, 2), ('QZ', 1, 0), ('QZ', 1, 1), ('F', 1, 2), ('RB', 3), ('F', 0, 3), ('F', 1, 3), ('SU', 10), ('F', 2, 0), ('F', 2, 1), ('F', 2, 2), ('F', 2, 3), ('F', 3, 0), ('F', 3, 1), ('F', 3, 2), ('QZ', 2, 0), ('QZ', 2, 1), ('RB', 4), ('F', 3, 3), ('SV', 10), ('SU', 15), ('F', 4, 0), ('F', 4, 1), ('F', 4, 2), ('F', 4, 3), ('RG', 3, 1), ('F', 5, 0), ('QZ', 3, 1), ('QZ', 3, 0), ('F', 5, 1), ('RB', 5), ('F', 5, 2), ('F', 5, 3), ('F', 6, 0), ('F', 6, 1), ('F', 6, 2), ('RG', 4, 0), ('F', 6, 3), ('RG', 4, 1), ('F', 7, 0), ('QZ', 4, 1), ('QZ', 4, 0), ('F', 7, 1), ('RB', 6), ('F', 7, 2), ('F', 7, 3), ('F', 8, 0), ('F', 8, 1), ('F', 8, 2), ('F', 8, 3), ('SV', 15), ('F', 9, 0), ('F', 9, 1), ('RG', 5, 1), ('QZ', 5, 0), ('QZ', 5, 1), ('RB', 7), ('F', 9, 2), ('F', 9, 3), ('F', 10, 0), ('F', 10, 1), ('F', 10, 2), ('F', 10, 3), ('F', 11, 0), ('RG', 6, 1), ('QZ', 6, 0), ('QZ', 6, 1), ('F', 11, 1), ('F', 11, 2), ('F', 11, 3), ('F', 12, 0), ('F', 12, 1), ('F', 12, 2), ('F', 12, 3), ('F', 13, 0), ('QZ', 7, 0), ('QZ', 7, 1), ('F', 13, 1), ('F', 13, 2), ('F', 13, 3), ('F', 14, 0), ('F', 14, 1), ('F', 14, 2), ('F', 14, 3), ('F', 15, 0), ('F', 15, 1), ('F', 15, 2), ('F', 15, 3)),
-    'G': (('IG',), ('P1', 2), ('P1', 3), ('P1', 4), ('P1', 5), ('P1', 6), ('RG', 2, 0), ('P1', 7), ('RG', 2, 1), ('P1', 8), ('RG', 3, 0), ('P1', 9), ('P1', 10), ('P1', 11), ('P1', 12), ('RG', 5, 0), ('P1', 13), ('P1', 14), ('RG', 6, 0), ('P1', 15), ('RG', 7, 0), ('RG', 7, 1)),
+    'PE': (('WT', 0, 0), ('WT', 0, 1), ('VB',), ('WT', 0, 2), ('WT', 0, 3), ('BB', 0), ('T', 0, 0, 0), ('T', 0, 0, 1), ('T', 0, 1, 0), ('T', 0, 1, 1), ('WT', 1, 0), ('WT', 1, 1), ('WT', 1, 2), ('WT', 1, 3), ('M', 0, 0), ('M', 1, 0), ('WT', 2, 0), ('WT', 2, 1), ('WT', 2, 2), ('WT', 2, 3), ('M', 0, 1), ('M', 1, 1), ('T', 1, 0, 0), ('T', 1, 0, 1), ('T', 1, 1, 0), ('T', 1, 1, 1), ('WT', 3, 0), ('WT', 3, 1), ('WT', 3, 2), ('WT', 3, 3), ('BB', 1), ('M', 0, 2), ('M', 1, 2), ('M', 0, 3), ('M', 1, 3), ('T', 2, 0, 0), ('T', 2, 0, 1), ('T', 2, 1, 0), ('T', 2, 1, 1), ('M', 2, 0), ('M', 2, 1), ('M', 2, 2), ('M', 2, 3), ('M', 3, 0), ('M', 3, 1), ('M', 3, 2), ('M', 3, 3), ('T', 3, 0, 0), ('T', 3, 0, 1), ('T', 3, 1, 0), ('T', 3, 1, 1), ('M', 4, 0), ('M', 4, 1), ('M', 4, 2), ('M', 4, 3), ('M', 5, 0), ('M', 5, 1), ('M', 5, 2), ('M', 5, 3), ('T', 4, 0, 0), ('T', 4, 0, 1), ('T', 4, 1, 0), ('T', 4, 1, 1), ('M', 6, 0), ('M', 6, 1), ('M', 6, 2), ('M', 6, 3), ('M', 7, 0), ('M', 7, 1), ('M', 7, 2), ('M', 7, 3), ('T', 5, 0, 0), ('T', 5, 0, 1), ('T', 5, 1, 0), ('T', 5, 1, 1), ('M', 8, 0), ('M', 8, 1), ('M', 8, 2), ('M', 8, 3), ('M', 9, 0), ('M', 9, 1), ('M', 9, 2), ('M', 9, 3), ('T', 6, 0, 0), ('T', 6, 0, 1), ('T', 6, 1, 0), ('T', 6, 1, 1), ('M', 10, 0), ('M', 10, 1), ('M', 10, 2), ('M', 10, 3), ('M', 11, 0), ('M', 11, 1), ('M', 11, 2), ('M', 11, 3), ('T', 7, 0, 0), ('T', 7, 0, 1), ('T', 7, 1, 0), ('T', 7, 1, 1), ('M', 12, 0), ('M', 12, 1), ('M', 12, 2), ('M', 12, 3), ('M', 13, 0), ('M', 13, 1), ('M', 13, 2), ('M', 13, 3), ('M', 14, 0), ('M', 14, 1), ('M', 14, 2), ('M', 14, 3), ('M', 15, 0), ('M', 15, 1), ('M', 15, 2), ('M', 15, 3)),
+    'S': (('IS',), ('LDV',), ('LDB',), ('RA', 0), ('RA', 1), ('WE', 0, 0), ('WE', 0, 1), ('RA', 2), ('RA', 3), ('WE', 0, 2), ('WE', 0, 3), ('BC', 0), ('C', 0, 0, 0), ('C', 0, 0, 1), ('C', 0, 1, 0), ('C', 0, 1, 1), ('WE', 1, 0), ('SA', 6), ('WE', 1, 1), ('WE', 1, 3), ('WE', 1, 2), ('RA', 4), ('RA', 5), ('SN', 6), ('RA', 7), ('SB', 6), ('WE', 2, 0), ('WE', 2, 1), ('WE', 2, 2), ('WE', 2, 3), ('C', 1, 0, 0), ('C', 1, 0, 1), ('C', 1, 1, 1), ('WE', 3, 0), ('WE', 3, 2), ('WE', 3, 3), ('WE', 3, 1), ('BC', 1), ('RA', 6), ('SA', 11), ('SA', 13), ('SN', 11), ('SA', 12), ('C', 2, 0, 0), ('C', 2, 0, 1), ('C', 2, 1, 0), ('RG', 2, 0), ('C', 2, 1, 1), ('RA', 9), ('RA', 8), ('SB', 11), ('SN', 13), ('SN', 12), ('SA', 14), ('C', 3, 0, 1), ('C', 3, 0, 0), ('C', 3, 1, 1), ('C', 3, 1, 0), ('RA', 11), ('SB', 12), ('RG', 3, 1), ('RA', 10), ('SB', 13), ('C', 4, 0, 0), ('C', 4, 0, 1), ('C', 4, 1, 0), ('C', 4, 1, 1), ('RA', 13), ('RA', 12), ('SA', 15), ('SN', 14), ('SN', 15), ('SB', 14), ('C', 5, 0, 0), ('C', 5, 0, 1), ('C', 5, 1, 1), ('C', 5, 1, 0), ('SB', 15), ('RA', 14), ('RA', 15), ('C', 6, 0, 0), ('C', 6, 0, 1), ('C', 6, 1, 0), ('RG', 6, 0), ('C', 6, 1, 1), ('RG', 6, 1), ('C', 7, 0, 0), ('C', 7, 0, 1), ('C', 7, 1, 0), ('RG', 7, 0), ('C', 7, 1, 1), ('RG', 7, 1)),
+    'V': (('IV',), ('SU', 0), ('SU', 1), ('SV', 0), ('SU', 2), ('SV', 1), ('SU', 3), ('RB', 0), ('SV', 2), ('WBC',), ('SV', 3), ('P1', 0), ('RB', 1), ('P1', 1), ('P1', 2), ('WQ', 0, 1), ('SU', 4), ('SU', 5), ('RG', 0, 0), ('WQ', 0, 0), ('RG', 0, 1), ('QZ', 0, 0), ('QZ', 0, 1), ('SV', 5), ('SV', 4), ('SU', 7), ('SV', 7), ('WQ', 1, 1), ('WQ', 1, 0), ('RB', 2), ('F', 0, 0), ('F', 1, 0), ('SU', 9), ('F', 0, 1), ('F', 1, 1), ('C', 1, 1, 0), ('WQ', 2, 0), ('WQ', 2, 1), ('RG', 1, 0), ('SU', 8), ('RG', 1, 1), ('WQ', 3, 1), ('WQ', 3, 0), ('F', 0, 2), ('QZ', 1, 1), ('QZ', 1, 0), ('F', 1, 2), ('RB', 3), ('F', 0, 3), ('F', 1, 3), ('SV', 9), ('SV', 8), ('SU', 10), ('F', 2, 0), ('F', 2, 1), ('F', 2, 2), ('F', 2, 3), ('RG', 2, 1), ('F', 3, 0), ('QZ', 2, 0), ('QZ', 2, 1), ('F', 3, 1), ('RB', 4), ('F', 3, 2), ('F', 3, 3), ('F', 4, 0), ('F', 4, 1), ('F', 4, 2), ('F', 4, 3), ('RG', 3, 0), ('SV', 10), ('F', 5, 0), ('QZ', 3, 0), ('F', 5, 1), ('QZ', 3, 1), ('RB', 5), ('F', 5, 2), ('F', 5, 3), ('F', 6, 0), ('F', 6, 1), ('F', 6, 2), ('F', 6, 3), ('RG', 4, 0), ('F', 7, 0), ('RG', 4, 1), ('QZ', 4, 0), ('QZ', 4, 1), ('F', 7, 1), ('RB', 6), ('F', 7, 2), ('F', 7, 3), ('F', 8, 0), ('F', 8, 1), ('F', 8, 2), ('F', 8, 3), ('RG', 5, 0), ('F', 9, 0), ('RG', 5, 1), ('QZ', 5, 0), ('QZ', 5, 1), ('F', 9, 1), ('RB', 7), ('F', 9, 2), ('F', 9, 3), ('F', 10, 0), ('F', 10, 1), ('F', 10, 2), ('F', 10, 3), ('F', 11, 0), ('QZ', 6, 0), ('QZ', 6, 1), ('F', 11, 1), ('F', 11, 2), ('F', 11, 3), ('F', 12, 0), ('F', 12, 1), ('F', 12, 2), ('F', 12, 3), ('F', 13, 0), ('QZ', 7, 0), ('F', 13, 1), ('QZ', 7, 1), ('F', 13, 2), ('F', 13, 3), ('F', 14, 0), ('F', 14, 1), ('F', 14, 2), ('F', 14, 3), ('F', 15, 0), ('F', 15, 1), ('F', 15, 2), ('F', 15, 3)),
+    'G': (('IG',), ('P1', 3), ('P1', 4), ('P1', 5), ('P1', 6), ('P1', 7), ('P1', 8), ('P1', 9), ('P1', 10), ('P1', 11), ('P1', 12), ('P1', 13), ('P1', 14), ('P1', 15)),
     'SP': (('LDX', 0, 0, 1), ('LDX', 0, 1, 1), ('LDX', 1, 0, 2), ('LDW', 0, 0, 2), ('LDW', 0, 2, 2), ('LDW', 1, 0, 4), ('LDX', 2, 0, 2), ('LDW', 2, 0, 4), ('LDX', 3, 0, 2), ('LDW', 3, 0, 4), ('LDX', 4, 0, 2), ('LDX', 5, 0, 2), ('LDX', 6, 0, 2), ('LDX', 7, 0, 2), ('ST', 0, 0), ('ST', 1, 0), ('ST', 0, 1), ('ST', 1, 1), ('ST', 2, 0), ('ST', 2, 1), ('ST', 3, 0), ('ST', 3, 1), ('ST', 4, 0), ('ST', 4, 1), ('ST', 5, 0), ('ST', 5, 1), ('ST', 6, 0), ('ST', 6, 1), ('ST', 7, 0), ('ST', 7, 1), ('ST', 8, 0), ('ST', 8, 1), ('ST', 9, 0), ('ST', 9, 1), ('ST', 10, 0), ('ST', 10, 1), ('ST', 11, 0), ('ST', 11, 1), ('ST', 12, 0), ('ST', 12, 1), ('ST', 13, 0), ('ST', 13, 1), ('ST', 14, 0), ('ST', 14, 1), ('ST', 15, 0), ('ST', 15, 1)),
 }
 
@@ -243,6 +244,11 @@ def tile_attentionalpoolerwmasking_pa_kernel(tc, x, ln_k_w, ln_k_b, Wk, Wv, bk, 
                     out=grp[:],
                     in0=live[("plan", j)][:, 4 * g : 4 * g + 4, :].rearrange("p t r -> p r t"),
                     scalar1=1.0, scalar2=0.0, op0=ALU.mult, op1=ALU.add,
+                )
+            elif ("RG", j, g) in ON_S:
+                nc.scalar.copy(
+                    out=grp[:].rearrange("p (c i) t -> p c t i", i=4),
+                    in_=live[("plan", j)][:, 4 * g : 4 * g + 4, :].rearrange("p t (c i) -> p c t i", i=4),
                 )
             else:
                 nc.vector.tensor_copy(

@@ -22,17 +22,17 @@ PLAN_BUFS = 3
 OSTV_BUFS = 5
 OSTS_BUFS = 3
 SMALL_ON_S = True
-STAT_V = (0, 1, 2, 3, 4, 5, 7, 8, 9, 10)
+STAT_V = (0, 1, 2, 3, 4, 5, 6, 7, 8, 9, 15)
 F_ON_S = ()
-ON_V = (('P1', 0), ('P1', 1), ('P1', 2), ('C', 1, 1, 0))
-ON_G = ()
-ON_S = (('RG', 6, 1), ('RG', 3, 1), ('RG', 6, 0), ('RG', 7, 0), ('RG', 2, 0), ('RG', 7, 1))
+ON_V = (('P1', 0), ('P1', 1), ('P1', 2), ('P1', 3))
+ON_G = (('RG', 2, 0), ('RG', 3, 0), ('RG', 5, 0), ('RG', 7, 0), ('RG', 1, 0), ('RG', 4, 0))
+ON_S = (('RG', 6, 1), ('RG', 6, 0), ('RG', 7, 1), ('RG', 4, 1), ('RG', 0, 1), ('RG', 2, 1), ('RG', 3, 1), ('RG', 3, 0), ('RG', 7, 0))
 QUEUES = {
     'PE': (('WT', 0, 0), ('WT', 0, 1), ('VB',), ('WT', 0, 2), ('WT', 0, 3), ('BB', 0), ('T', 0, 0, 0), ('T', 0, 0, 1), ('T', 0, 1, 0), ('T', 0, 1, 1), ('WT', 1, 0), ('WT', 1, 1), ('WT', 1, 2), ('WT', 1, 3), ('M', 0, 0), ('M', 1, 0), ('WT', 2, 0), ('WT', 2, 1), ('WT', 2, 2), ('WT', 2, 3), ('M', 0, 1), ('M', 1, 1), ('T', 1, 0, 0), ('T', 1, 0, 1), ('T', 1, 1, 0), ('T', 1, 1, 1), ('WT', 3, 0), ('WT', 3, 1), ('WT', 3, 2), ('WT', 3, 3), ('BB', 1), ('M', 0, 2), ('M', 1, 2), ('M', 0, 3), ('M', 1, 3), ('T', 2, 0, 0), ('T', 2, 0, 1), ('T', 2, 1, 0), ('T', 2, 1, 1), ('M', 2, 0), ('M', 2, 1), ('M', 2, 2), ('M', 2, 3), ('M', 3, 0), ('M', 3, 1), ('M', 3, 2), ('M', 3, 3), ('T', 3, 0, 0), ('T', 3, 0, 1), ('T', 3, 1, 0), ('T', 3, 1, 1), ('M', 4, 0), ('M', 4, 1), ('M', 4, 2), ('M', 4, 3), ('M', 5, 0), ('M', 5, 1), ('M', 5, 2), ('M', 5, 3), ('T', 4, 0, 0), ('T', 4, 0, 1), ('T', 4, 1, 0), ('T', 4, 1, 1), ('M', 6, 0), ('M', 6, 1), ('M', 6, 2), ('M', 6, 3), ('M', 7, 0), ('M', 7, 1), ('M', 7, 2), ('M', 7, 3), ('T', 5, 0, 0), ('T', 5, 0, 1), ('T', 5, 1, 0), ('T', 5, 1, 1), ('M', 8, 0), ('M', 8, 1), ('M', 8, 2), ('M', 8, 3), ('M', 9, 0), ('M', 9, 1), ('M', 9, 2), ('M', 9, 3), ('T', 6, 0, 0), ('T', 6, 0, 1), ('T', 6, 1, 0), ('T', 6, 1, 1), ('M', 10, 0), ('M', 10, 1), ('M', 10, 2), ('M', 10, 3), ('M', 11, 0), ('M', 11, 1), ('M', 11, 2), ('M', 11, 3), ('T', 7, 0, 0), ('T', 7, 0, 1), ('T', 7, 1, 0), ('T', 7, 1, 1), ('M', 12, 0), ('M', 12, 1), ('M', 12, 2), ('M', 12, 3), ('M', 13, 0), ('M', 13, 1), ('M', 13, 2), ('M', 13, 3), ('M', 14, 0), ('M', 14, 1), ('M', 14, 2), ('M', 14, 3), ('M', 15, 0), ('M', 15, 1), ('M', 15, 2), ('M', 15, 3)),
-    'S': (('IS',), ('LDV',), ('LDB',), ('RA', 0), ('RA', 1), ('WE', 0, 0), ('WE', 0, 1), ('RA', 2), ('RA', 3), ('WE', 0, 2), ('WE', 0, 3), ('BC', 0), ('C', 0, 0, 0), ('C', 0, 0, 1), ('C', 0, 1, 0), ('C', 0, 1, 1), ('WE', 1, 0), ('SA', 6), ('WE', 1, 1), ('WE', 1, 3), ('WE', 1, 2), ('RA', 4), ('RA', 5), ('SN', 6), ('RA', 7), ('SB', 6), ('WE', 2, 0), ('WE', 2, 1), ('WE', 2, 2), ('WE', 2, 3), ('C', 1, 0, 0), ('C', 1, 0, 1), ('C', 1, 1, 1), ('WE', 3, 0), ('WE', 3, 2), ('WE', 3, 3), ('WE', 3, 1), ('BC', 1), ('RA', 6), ('SA', 11), ('SA', 13), ('SN', 11), ('SA', 12), ('C', 2, 0, 0), ('C', 2, 0, 1), ('C', 2, 1, 0), ('RG', 2, 0), ('C', 2, 1, 1), ('RA', 9), ('RA', 8), ('SB', 11), ('SN', 13), ('SN', 12), ('SA', 14), ('C', 3, 0, 1), ('C', 3, 0, 0), ('C', 3, 1, 1), ('C', 3, 1, 0), ('RA', 11), ('SB', 12), ('RG', 3, 1), ('RA', 10), ('SB', 13), ('C', 4, 0, 0), ('C', 4, 0, 1), ('C', 4, 1, 0), ('C', 4, 1, 1), ('RA', 13), ('RA', 12), ('SA', 15), ('SN', 14), ('SN', 15), ('SB', 14), ('C', 5, 0, 0), ('C', 5, 0, 1), ('C', 5, 1, 1), ('C', 5, 1, 0), ('SB', 15), ('RA', 14), ('RA', 15), ('C', 6, 0, 0), ('C', 6, 0, 1), ('C', 6, 1, 0), ('RG', 6, 0), ('C', 6, 1, 1), ('RG', 6, 1), ('C', 7, 0, 0), ('C', 7, 0, 1), ('C', 7, 1, 0), ('RG', 7, 0), ('C', 7, 1, 1), ('RG', 7, 1)),
-    'V': (('IV',), ('SU', 0), ('SU', 1), ('SV', 0), ('SU', 2), ('SV', 1), ('SU', 3), ('RB', 0), ('SV', 2), ('WBC',), ('SV', 3), ('P1', 0), ('RB', 1), ('P1', 1), ('P1', 2), ('WQ', 0, 1), ('SU', 4), ('SU', 5), ('RG', 0, 0), ('WQ', 0, 0), ('RG', 0, 1), ('QZ', 0, 0), ('QZ', 0, 1), ('SV', 5), ('SV', 4), ('SU', 7), ('SV', 7), ('WQ', 1, 1), ('WQ', 1, 0), ('RB', 2), ('F', 0, 0), ('F', 1, 0), ('SU', 9), ('F', 0, 1), ('F', 1, 1), ('C', 1, 1, 0), ('WQ', 2, 0), ('WQ', 2, 1), ('RG', 1, 0), ('SU', 8), ('RG', 1, 1), ('WQ', 3, 1), ('WQ', 3, 0), ('F', 0, 2), ('QZ', 1, 1), ('QZ', 1, 0), ('F', 1, 2), ('RB', 3), ('F', 0, 3), ('F', 1, 3), ('SV', 9), ('SV', 8), ('SU', 10), ('F', 2, 0), ('F', 2, 1), ('F', 2, 2), ('F', 2, 3), ('RG', 2, 1), ('F', 3, 0), ('QZ', 2, 0), ('QZ', 2, 1), ('F', 3, 1), ('RB', 4), ('F', 3, 2), ('F', 3, 3), ('F', 4, 0), ('F', 4, 1), ('F', 4, 2), ('F', 4, 3), ('RG', 3, 0), ('SV', 10), ('F', 5, 0), ('QZ', 3, 0), ('F', 5, 1), ('QZ', 3, 1), ('RB', 5), ('F', 5, 2), ('F', 5, 3), ('F', 6, 0), ('F', 6, 1), ('F', 6, 2), ('F', 6, 3), ('RG', 4, 0), ('F', 7, 0), ('RG', 4, 1), ('QZ', 4, 0), ('QZ', 4, 1), ('F', 7, 1), ('RB', 6), ('F', 7, 2), ('F', 7, 3), ('F', 8, 0), ('F', 8, 1), ('F', 8, 2), ('F', 8, 3), ('RG', 5, 0), ('F', 9, 0), ('RG', 5, 1), ('QZ', 5, 0), ('QZ', 5, 1), ('F', 9, 1), ('RB', 7), ('F', 9, 2), ('F', 9, 3), ('F', 10, 0), ('F', 10, 1), ('F', 10, 2), ('F', 10, 3), ('F', 11, 0), ('QZ', 6, 0), ('QZ', 6, 1), ('F', 11, 1), ('F', 11, 2), ('F', 11, 3), ('F', 12, 0), ('F', 12, 1), ('F', 12, 2), ('F', 12, 3), ('F', 13, 0), ('QZ', 7, 0), ('F', 13, 1), ('QZ', 7, 1), ('F', 13, 2), ('F', 13, 3), ('F', 14, 0), ('F', 14, 1), ('F', 14, 2), ('F', 14, 3), ('F', 15, 0), ('F', 15, 1), ('F', 15, 2), ('F', 15, 3)),
-    'G': (('IG',), ('P1', 3), ('P1', 4), ('P1', 5), ('P1', 6), ('P1', 7), ('P1', 8), ('P1', 9), ('P1', 10), ('P1', 11), ('P1', 12), ('P1', 13), ('P1', 14), ('P1', 15)),
-    'SP': (('LDX', 0, 0, 1), ('LDX', 0, 1, 1), ('LDX', 1, 0, 2), ('LDW', 0, 0, 2), ('LDW', 0, 2, 2), ('LDW', 1, 0, 4), ('LDX', 2, 0, 2), ('LDW', 2, 0, 4), ('LDX', 3, 0, 2), ('LDW', 3, 0, 4), ('LDX', 4, 0, 2), ('LDX', 5, 0, 2), ('LDX', 6, 0, 2), ('LDX', 7, 0, 2), ('ST', 0, 0), ('ST', 1, 0), ('ST', 0, 1), ('ST', 1, 1), ('ST', 2, 0), ('ST', 2, 1), ('ST', 3, 0), ('ST', 3, 1), ('ST', 4, 0), ('ST', 4, 1), ('ST', 5, 0), ('ST', 5, 1), ('ST', 6, 0), ('ST', 6, 1), ('ST', 7, 0), ('ST', 7, 1), ('ST', 8, 0), ('ST', 8, 1), ('ST', 9, 0), ('ST', 9, 1), ('ST', 10, 0), ('ST', 10, 1), ('ST', 11, 0), ('ST', 11, 1), ('ST', 12, 0), ('ST', 12, 1), ('ST', 13, 0), ('ST', 13, 1), ('ST', 14, 0), ('ST', 14, 1), ('ST', 15, 0), ('ST', 15, 1)),
+    'S': (('IS',), ('LDV',), ('LDB',), ('RA', 0), ('RA', 1), ('WE', 0, 0), ('WE', 0, 1), ('WE', 0, 2), ('WE', 0, 3), ('BC', 0), ('C', 0, 0, 0), ('C', 0, 0, 1), ('C', 0, 1, 0), ('C', 0, 1, 1), ('RG', 0, 1), ('RA', 3), ('RA', 2), ('WE', 1, 0), ('WE', 1, 2), ('WE', 1, 1), ('WE', 1, 3), ('WE', 2, 0), ('WE', 2, 1), ('WE', 2, 2), ('WE', 2, 3), ('C', 1, 0, 0), ('RA', 4), ('RA', 5), ('C', 1, 0, 1), ('C', 1, 1, 0), ('C', 1, 1, 1), ('WE', 3, 0), ('WE', 3, 2), ('WE', 3, 1), ('WE', 3, 3), ('BC', 1), ('RA', 6), ('RA', 7), ('SA', 11), ('SA', 10), ('SN', 11), ('SN', 10), ('SB', 11), ('C', 2, 0, 0), ('C', 2, 0, 1), ('C', 2, 1, 0), ('C', 2, 1, 1), ('SB', 10), ('RG', 2, 1), ('RA', 8), ('RA', 9), ('RA', 10), ('RA', 11), ('SA', 13), ('C', 3, 0, 1), ('C', 3, 0, 0), ('C', 3, 1, 1), ('C', 3, 1, 0), ('SA', 12), ('RG', 3, 1), ('SN', 13), ('SN', 12), ('SB', 13), ('C', 4, 0, 1), ('C', 4, 0, 0), ('C', 4, 1, 0), ('C', 4, 1, 1), ('SB', 12), ('RG', 4, 1), ('RA', 13), ('RA', 12), ('C', 5, 0, 0), ('C', 5, 0, 1), ('SA', 14), ('C', 5, 1, 1), ('C', 5, 1, 0), ('SN', 14), ('SB', 14), ('RA', 15), ('RA', 14), ('C', 6, 0, 0), ('C', 6, 0, 1), ('RG', 6, 0), ('C', 6, 1, 1), ('C', 6, 1, 0), ('RG', 6, 1), ('C', 7, 0, 0), ('C', 7, 0, 1), ('C', 7, 1, 0), ('C', 7, 1, 1), ('RG', 7, 1)),
+    'V': (('IV',), ('SU', 0), ('SU', 1), ('SV', 0), ('SV', 1), ('NM', 0), ('RB', 0), ('P1', 0), ('WBC',), ('NM', 1), ('P1', 1), ('SU', 2), ('SU', 3), ('WQ', 0, 1), ('WQ', 0, 0), ('RG', 0, 0), ('QZ', 0, 0), ('SV', 3), ('SV', 2), ('NM', 2), ('SU', 5), ('QZ', 0, 1), ('RB', 1), ('P1', 2), ('SU', 4), ('WQ', 1, 0), ('WQ', 1, 1), ('NM', 3), ('P1', 3), ('SV', 4), ('SV', 5), ('F', 0, 0), ('F', 1, 0), ('WQ', 2, 1), ('WQ', 2, 0), ('RB', 2), ('F', 0, 1), ('SU', 7), ('SU', 6), ('F', 1, 1), ('SV', 6), ('SV', 7), ('SU', 9), ('WQ', 3, 1), ('WQ', 3, 0), ('RG', 1, 1), ('F', 0, 2), ('QZ', 1, 1), ('QZ', 1, 0), ('F', 1, 2), ('RB', 3), ('F', 0, 3), ('F', 1, 3), ('F', 2, 0), ('F', 2, 1), ('F', 2, 2), ('SU', 8), ('F', 2, 3), ('SV', 9), ('SV', 8), ('F', 3, 0), ('QZ', 2, 0), ('QZ', 2, 1), ('F', 3, 1), ('RB', 4), ('F', 3, 2), ('F', 3, 3), ('F', 4, 0), ('F', 4, 1), ('F', 4, 2), ('F', 4, 3), ('F', 5, 0), ('F', 5, 1), ('QZ', 3, 0), ('QZ', 3, 1), ('RB', 5), ('F', 5, 2), ('F', 5, 3), ('SU', 15), ('F', 6, 0), ('F', 6, 1), ('F', 6, 2), ('F', 6, 3), ('F', 7, 0), ('QZ', 4, 0), ('F', 7, 1), ('QZ', 4, 1), ('RB', 6), ('F', 7, 2), ('F', 7, 3), ('F', 8, 0), ('F', 8, 1), ('F', 8, 2), ('F', 8, 3), ('SV', 15), ('F', 9, 0), ('F', 9, 1), ('RG', 5, 1), ('QZ', 5, 0), ('QZ', 5, 1), ('RB', 7), ('F', 9, 2), ('F', 9, 3), ('F', 10, 0), ('F', 10, 1), ('F', 10, 2), ('F', 10, 3), ('F', 11, 0), ('QZ', 6, 0), ('F', 11, 1), ('QZ', 6, 1), ('F', 11, 2), ('F', 11, 3), ('F', 12, 0), ('F', 12, 1), ('F', 12, 2), ('F', 12, 3), ('F', 13, 0), ('QZ', 7, 1), ('QZ', 7, 0), ('F', 13, 1), ('F', 13, 2), ('F', 13, 3), ('F', 14, 0), ('F', 14, 1), ('F', 14, 2), ('F', 14, 3), ('F', 15, 0), ('F', 15, 1), ('F', 15, 2), ('F', 15, 3)),
+    'G': (('IG',), ('NM', 4), ('NM', 5), ('P1', 4), ('RG', 1, 0), ('P1', 5), ('NM', 6), ('NM', 7), ('P1', 6), ('RG', 2, 0), ('P1', 7), ('NM', 8), ('NM', 9), ('P1', 8), ('RG', 3, 0), ('P1', 9), ('P1', 10), ('P1', 11), ('RG', 4, 0), ('P1', 12), ('RG', 5, 0), ('P1', 13), ('NM', 15), ('P1', 14), ('P1', 15), ('RG', 7, 0)),
+    'SP': (('LDX', 0, 0, 1), ('LDX', 0, 1, 1), ('LDW', 0, 0, 2), ('LDW', 0, 2, 2), ('LDX', 1, 0, 2), ('LDW', 1, 0, 4), ('LDX', 2, 0, 2), ('LDW', 2, 0, 4), ('LDW', 3, 0, 4), ('LDX', 3, 0, 2), ('LDX', 4, 0, 2), ('LDX', 5, 0, 2), ('LDX', 6, 0, 2), ('LDX', 7, 0, 2), ('ST', 0, 0), ('ST', 1, 0), ('ST', 0, 1), ('ST', 1, 1), ('ST', 2, 0), ('ST', 2, 1), ('ST', 3, 0), ('ST', 3, 1), ('ST', 4, 0), ('ST', 4, 1), ('ST', 5, 0), ('ST', 5, 1), ('ST', 6, 0), ('ST', 6, 1), ('ST', 7, 0), ('ST', 7, 1), ('ST', 8, 0), ('ST', 8, 1), ('ST', 9, 0), ('ST', 9, 1), ('ST', 10, 0), ('ST', 10, 1), ('ST', 11, 0), ('ST', 11, 1), ('ST', 12, 0), ('ST', 12, 1), ('ST', 13, 0), ('ST', 13, 1), ('ST', 14, 0), ('ST', 14, 1), ('ST', 15, 0), ('ST', 15, 1)),
 }
 
 
@@ -196,6 +196,10 @@ def tile_attentionalpoolerwmasking_pa_kernel(tc, x, ln_k_w, ln_k_b, Wk, Wv, bk, 
         def t_rb(j):
             nc.vector.reciprocal(out=rstd[j][:], in_=std[j][:])
 
+        def t_nm(i):
+            eng = nc.vector if ("P1", i) in ON_V else nc.gpsimd
+            eng.tensor_scalar(out=nm[i][:], in0=mv[i][:, 0:1], scalar1=-1.0, scalar2=0.0, op0=ALU.mult, op1=ALU.add)
+
         def t_p1(i):
             xh = xhp.tile([P, 8, P], F32, tag="xh", name="xh")
             live[("xh", i)] = xh
@@ -203,9 +207,9 @@ def tile_attentionalpoolerwmasking_pa_kernel(tc, x, ln_k_w, ln_k_b, Wk, Wv, bk, 
             eng.tensor_scalar(
                 out=xh[:].rearrange("p (v e) q -> p v e q", e=2),
                 in0=xts[i // 2][:, i % 2, :].rearrange("p (v q e) -> p v e q", v=4, e=2),
-                scalar1=mv[i][:, 0:1] if i in STAT_V else nm[i][:],
+                scalar1=nm[i][:],
                 scalar2=rstd[i // 2][:, i % 2 : i % 2 + 1],
-                op0=ALU.subtract if i in STAT_V else ALU.add,
+                op0=ALU.add,
                 op1=ALU.mult,
             )
 
@@ -301,7 +305,7 @@ def tile_attentionalpoolerwmasking_pa_kernel(tc, x, ln_k_w, ln_k_b, Wk, Wv, bk, 
 
         fn = {"IV": t_init_v, "IS": t_init_s, "IG": t_init_g, "LDV": t_ldv, "LDB": t_ldb, "LDX": t_ldx, "LDW": t_ldw,
               "VB": t_vb, "WBC": t_wbc, "BB": t_bb, "BC": t_bc, "WT": t_wt, "WE": t_we, "WQ": t_wq, "SU": t_su, "SV": t_sv,
-              "SA": t_sa, "SN": t_sn, "SB": t_sb, "RA": t_ra, "RB": t_rb, "P1": t_p1, "T": t_t, "C": t_c, "RG": t_rg,
+              "SA": t_sa, "SN": t_sn, "SB": t_sb, "RA": t_ra, "RB": t_rb, "NM": t_nm, "P1": t_p1, "T": t_t, "C": t_c, "RG": t_rg,
               "QZ": t_qz, "M": t_m, "F": t_f, "A": t_a, "ST": t_st}
 
         queues = build_queues()
@@ -348,6 +352,9 @@ def tile_attentionalpoolerwmasking_pa_kernel(tc, x, ln_k_w, ln_k_b, Wk, Wv, bk, 
             after(("RA", i), ("SV", i) if i in STAT_V else ("SB", i), ("IS",))
             after(("RB", j), ("RA", i))
             after(("P1", i), ("RB", j))
+            if i in STAT_V:
+                after(("NM", i), ("SV", i))
+                after(("P1", i), ("NM", i))
             if i >= 1:
                 after(("P1", i), ("P1", i - 1))
             if i >= XH_BUFS:

@@ -24,20 +24,54 @@ OSTS_BUFS = 3
 SMALL_ON_S = True
 STAT_V = (0, 1, 2, 3, 4, 5, 6, 7, 8, 9, 15)
 F_ON_S = ()
-ON_V = (('P1', 0), ('P1', 1), ('P1', 2), ('P1', 3))
-ON_G = (('RG', 2, 0), ('RG', 3, 0), ('RG', 5, 0), ('RG', 7, 0), ('RG', 1, 0), ('RG', 4, 0))
-ON_S = (('RG', 6, 1), ('RG', 6, 0), ('RG', 7, 1), ('RG', 4, 1), ('RG', 0, 1), ('RG', 2, 1), ('RG', 3, 1), ('RG', 3, 0), ('RG', 7, 0))
-QUEUES = {
-    'PE': (('WT', 0, 0), ('WT', 0, 1), ('VB',), ('WT', 0, 2), ('WT', 0, 3), ('BB', 0), ('T', 0, 0, 0), ('T', 0, 0, 1), ('T', 0, 1, 0), ('T', 0, 1, 1), ('WT', 1, 0), ('WT', 1, 1), ('WT', 1, 2), ('WT', 1, 3), ('M', 0, 0), ('M', 1, 0), ('WT', 2, 0), ('WT', 2, 1), ('WT', 2, 2), ('WT', 2, 3), ('M', 0, 1), ('M', 1, 1), ('T', 1, 0, 0), ('T', 1, 0, 1), ('T', 1, 1, 0), ('T', 1, 1, 1), ('WT', 3, 0), ('WT', 3, 1), ('WT', 3, 2), ('WT', 3, 3), ('BB', 1), ('M', 0, 2), ('M', 1, 2), ('M', 0, 3), ('M', 1, 3), ('T', 2, 0, 0), ('T', 2, 0, 1), ('T', 2, 1, 0), ('T', 2, 1, 1), ('M', 2, 0), ('M', 2, 1), ('M', 2, 2), ('M', 2, 3), ('M', 3, 0), ('M', 3, 1), ('M', 3, 2), ('M', 3, 3), ('T', 3, 0, 0), ('T', 3, 0, 1), ('T', 3, 1, 0), ('T', 3, 1, 1), ('M', 4, 0), ('M', 4, 1), ('M', 4, 2), ('M', 4, 3), ('M', 5, 0), ('M', 5, 1), ('M', 5, 2), ('M', 5, 3), ('T', 4, 0, 0), ('T', 4, 0, 1), ('T', 4, 1, 0), ('T', 4, 1, 1), ('M', 6, 0), ('M', 6, 1), ('M', 6, 2), ('M', 6, 3), ('M', 7, 0), ('M', 7, 1), ('M', 7, 2), ('M', 7, 3), ('T', 5, 0, 0), ('T', 5, 0, 1), ('T', 5, 1, 0), ('T', 5, 1, 1), ('M', 8, 0), ('M', 8, 1), ('M', 8, 2), ('M', 8, 3), ('M', 9, 0), ('M', 9, 1), ('M', 9, 2), ('M', 9, 3), ('T', 6, 0, 0), ('T', 6, 0, 1), ('T', 6, 1, 0), ('T', 6, 1, 1), ('M', 10, 0), ('M', 10, 1), ('M', 10, 2), ('M', 10, 3), ('M', 11, 0), ('M', 11, 1), ('M', 11, 2), ('M', 11, 3), ('T', 7, 0, 0), ('T', 7, 0, 1), ('T', 7, 1, 0), ('T', 7, 1, 1), ('M', 12, 0), ('M', 12, 1), ('M', 12, 2), ('M', 12, 3), ('M', 13, 0), ('M', 13, 1), ('M', 13, 2), ('M', 13, 3), ('M', 14, 0), ('M', 14, 1), ('M', 14, 2), ('M', 14, 3), ('M', 15, 0), ('M', 15, 1), ('M', 15, 2), ('M', 15, 3)),
-    'S': (('IS',), ('LDV',), ('LDB',), ('RA', 0), ('RA', 1), ('WE', 0, 0), ('WE', 0, 1), ('WE', 0, 2), ('WE', 0, 3), ('BC', 0), ('C', 0, 0, 0), ('C', 0, 0, 1), ('C', 0, 1, 0), ('C', 0, 1, 1), ('RG', 0, 1), ('RA', 3), ('RA', 2), ('WE', 1, 0), ('WE', 1, 2), ('WE', 1, 1), ('WE', 1, 3), ('WE', 2, 0), ('WE', 2, 1), ('WE', 2, 2), ('WE', 2, 3), ('C', 1, 0, 0), ('RA', 4), ('RA', 5), ('C', 1, 0, 1), ('C', 1, 1, 0), ('C', 1, 1, 1), ('WE', 3, 0), ('WE', 3, 2), ('WE', 3, 1), ('WE', 3, 3), ('BC', 1), ('RA', 6), ('RA', 7), ('SA', 11), ('SA', 10), ('SN', 11), ('SN', 10), ('SB', 11), ('C', 2, 0, 0), ('C', 2, 0, 1), ('C', 2, 1, 0), ('C', 2, 1, 1), ('SB', 10), ('RG', 2, 1), ('RA', 8), ('RA', 9), ('RA', 10), ('RA', 11), ('SA', 13), ('C', 3, 0, 1), ('C', 3, 0, 0), ('C', 3, 1, 1), ('C', 3, 1, 0), ('SA', 12), ('RG', 3, 1), ('SN', 13), ('SN', 12), ('SB', 13), ('C', 4, 0, 1), ('C', 4, 0, 0), ('C', 4, 1, 0), ('C', 4, 1, 1), ('SB', 12), ('RG', 4, 1), ('RA', 13), ('RA', 12), ('C', 5, 0, 0), ('C', 5, 0, 1), ('SA', 14), ('C', 5, 1, 1), ('C', 5, 1, 0), ('SN', 14), ('SB', 14), ('RA', 15), ('RA', 14), ('C', 6, 0, 0), ('C', 6, 0, 1), ('RG', 6, 0), ('C', 6, 1, 1), ('C', 6, 1, 0), ('RG', 6, 1), ('C', 7, 0, 0), ('C', 7, 0, 1), ('C', 7, 1, 0), ('C', 7, 1, 1), ('RG', 7, 1)),
-    'V': (('IV',), ('SU', 0), ('SU', 1), ('SV', 0), ('SV', 1), ('NM', 0), ('RB', 0), ('P1', 0), ('WBC',), ('NM', 1), ('P1', 1), ('SU', 2), ('SU', 3), ('WQ', 0, 1), ('WQ', 0, 0), ('RG', 0, 0), ('QZ', 0, 0), ('SV', 3), ('SV', 2), ('NM', 2), ('SU', 5), ('QZ', 0, 1), ('RB', 1), ('P1', 2), ('SU', 4), ('WQ', 1, 0), ('WQ', 1, 1), ('NM', 3), ('P1', 3), ('SV', 4), ('SV', 5), ('F', 0, 0), ('F', 1, 0), ('WQ', 2, 1), ('WQ', 2, 0), ('RB', 2), ('F', 0, 1), ('SU', 7), ('SU', 6), ('F', 1, 1), ('SV', 6), ('SV', 7), ('SU', 9), ('WQ', 3, 1), ('WQ', 3, 0), ('RG', 1, 1), ('F', 0, 2), ('QZ', 1, 1), ('QZ', 1, 0), ('F', 1, 2), ('RB', 3), ('F', 0, 3), ('F', 1, 3), ('F', 2, 0), ('F', 2, 1), ('F', 2, 2), ('SU', 8), ('F', 2, 3), ('SV', 9), ('SV', 8), ('F', 3, 0), ('QZ', 2, 0), ('QZ', 2, 1), ('F', 3, 1), ('RB', 4), ('F', 3, 2), ('F', 3, 3), ('F', 4, 0), ('F', 4, 1), ('F', 4, 2), ('F', 4, 3), ('F', 5, 0), ('F', 5, 1), ('QZ', 3, 0), ('QZ', 3, 1), ('RB', 5), ('F', 5, 2), ('F', 5, 3), ('SU', 15), ('F', 6, 0), ('F', 6, 1), ('F', 6, 2), ('F', 6, 3), ('F', 7, 0), ('QZ', 4, 0), ('F', 7, 1), ('QZ', 4, 1), ('RB', 6), ('F', 7, 2), ('F', 7, 3), ('F', 8, 0), ('F', 8, 1), ('F', 8, 2), ('F', 8, 3), ('SV', 15), ('F', 9, 0), ('F', 9, 1), ('RG', 5, 1), ('QZ', 5, 0), ('QZ', 5, 1), ('RB', 7), ('F', 9, 2), ('F', 9, 3), ('F', 10, 0), ('F', 10, 1), ('F', 10, 2), ('F', 10, 3), ('F', 11, 0), ('QZ', 6, 0), ('F', 11, 1), ('QZ', 6, 1), ('F', 11, 2), ('F', 11, 3), ('F', 12, 0), ('F', 12, 1), ('F', 12, 2), ('F', 12, 3), ('F', 13, 0), ('QZ', 7, 1), ('QZ', 7, 0), ('F', 13, 1), ('F', 13, 2), ('F', 13, 3), ('F', 14, 0), ('F', 14, 1), ('F', 14, 2), ('F', 14, 3), ('F', 15, 0), ('F', 15, 1), ('F', 15, 2), ('F', 15, 3)),
-    'G': (('IG',), ('NM', 4), ('NM', 5), ('P1', 4), ('RG', 1, 0), ('P1', 5), ('NM', 6), ('NM', 7), ('P1', 6), ('RG', 2, 0), ('P1', 7), ('NM', 8), ('NM', 9), ('P1', 8), ('RG', 3, 0), ('P1', 9), ('P1', 10), ('P1', 11), ('RG', 4, 0), ('P1', 12), ('RG', 5, 0), ('P1', 13), ('NM', 15), ('P1', 14), ('P1', 15), ('RG', 7, 0)),
-    'SP': (('LDX', 0, 0, 1), ('LDX', 0, 1, 1), ('LDW', 0, 0, 2), ('LDW', 0, 2, 2), ('LDX', 1, 0, 2), ('LDW', 1, 0, 4), ('LDX', 2, 0, 2), ('LDW', 2, 0, 4), ('LDW', 3, 0, 4), ('LDX', 3, 0, 2), ('LDX', 4, 0, 2), ('LDX', 5, 0, 2), ('LDX', 6, 0, 2), ('LDX', 7, 0, 2), ('ST', 0, 0), ('ST', 1, 0), ('ST', 0, 1), ('ST', 1, 1), ('ST', 2, 0), ('ST', 2, 1), ('ST', 3, 0), ('ST', 3, 1), ('ST', 4, 0), ('ST', 4, 1), ('ST', 5, 0), ('ST', 5, 1), ('ST', 6, 0), ('ST', 6, 1), ('ST', 7, 0), ('ST', 7, 1), ('ST', 8, 0), ('ST', 8, 1), ('ST', 9, 0), ('ST', 9, 1), ('ST', 10, 0), ('ST', 10, 1), ('ST', 11, 0), ('ST', 11, 1), ('ST', 12, 0), ('ST', 12, 1), ('ST', 13, 0), ('ST', 13, 1), ('ST', 14, 0), ('ST', 14, 1), ('ST', 15, 0), ('ST', 15, 1)),
-}
+ON_V = (("P1", 0), ("P1", 1), ("P1", 2), ("P1", 3))
+ON_G = tuple(("RG", j, 0) for j in range(1, NG))
+ON_S = tuple(("RG", j, 1) for j in (0, 2, 6, 7))
 
 
 def build_queues():
-    return QUEUES
+    t4 = lambda j: [("T", j, g, b) for g in range(2) for b in range(2)] if j < NG else []
+    c4 = lambda j: [("C", j, g, b) for g in range(2) for b in range(2)] if j < NG else []
+    ra = lambda j: [("RA", 2 * j), ("RA", 2 * j + 1)] if j < NG else []
+    rb = lambda j: [("RB", j)] if j < NG else []
+    w4 = lambda k, c: [(k, c, n) for n in range(4)]
+    wq = lambda c: [("WQ", c, 0), ("WQ", c, 1)]
+    qz = lambda j: [("QZ", j, 0), ("QZ", j, 1)] if j < NG else []
+    two = lambda k, j: [(k, 2 * j), (k, 2 * j + 1)] if j < NG else []
+    ss = lambda j: two("SA", j) + two("SN", j) + two("SB", j) + ra(j) if j < NG else []
+    f = lambda i, chs: [("F", i, ch) for ch in chs]
+    pe = [("WT", 0, 0), ("WT", 0, 1), ("VB",), ("WT", 0, 2), ("WT", 0, 3), ("BB", 0)] + t4(0) + w4("WT", 1)
+    pe += [("M", 0, 0), ("M", 1, 0)] + w4("WT", 2) + [("M", 0, 1), ("M", 1, 1)] + t4(1) + w4("WT", 3) + [("BB", 1)]
+    pe += [("M", 0, 2), ("M", 1, 2), ("M", 0, 3), ("M", 1, 3)]
+    for j in range(1, NG):
+        pe += t4(j + 1) + [("M", 2 * j + n, ch) for n in range(2) for ch in range(4)]
+    sp = [("LDX", 0, 0, 1), ("LDX", 0, 1, 1), ("LDW", 0, 0, 2), ("LDW", 0, 2, 2), ("LDX", 1, 0, 2), ("LDW", 1, 0, 4),
+          ("LDX", 2, 0, 2), ("LDW", 2, 0, 4), ("LDW", 3, 0, 4)] + [("LDX", j, 0, 2) for j in range(3, NG)]
+    sp += [("ST", 0, 0), ("ST", 1, 0), ("ST", 0, 1), ("ST", 1, 1)]
+    sp += [("ST", i, h) for i in range(2, 16) for h in range(2)]
+    s = [("LDV",), ("IS",), ("LDB",)] + ra(0) + w4("WE", 0) + [("BC", 0)] + c4(0) + ra(1) + [("RG", 0, 1)]
+    s += w4("WE", 1) + w4("WE", 2) + ra(2) + c4(1) + w4("WE", 3) + [("BC", 1)] + ra(3)
+    s += [("SA", 10), ("SA", 11), ("SN", 10), ("SB", 10)]
+    v = [("IV",)] + two("SU", 0) + two("SV", 0) + two("NM", 0) + rb(0) + [("P1", 0), ("WBC",), ("P1", 1)] + two("SU", 1)
+    v += wq(0) + [("RG", 0, 0)] + two("SV", 1) + [("NM", 2), ("QZ", 0, 0), ("SU", 5), ("QZ", 0, 1), ("SU", 4)] + rb(1)
+    v += [("P1", 2), ("WQ", 1, 0), ("NM", 3), ("WQ", 1, 1), ("P1", 3)] + two("SV", 2) + [("F", 0, 0), ("F", 1, 0)] + wq(2)[0:1] + rb(2) + wq(2)[1:]
+    v += two("SU", 3) + [("F", 0, 1), ("F", 1, 1), ("SV", 6), ("SU", 9), ("SV", 7)] + wq(3) + [("RG", 1, 1), ("F", 0, 2)] + qz(1) + rb(3)
+    v += [("F", 1, 2), ("F", 0, 3), ("F", 1, 3), ("SU", 8)]
+    g = [("IG",)] + two("NM", 2) + two("P1", 2) + [("RG", 1, 0)] + two("NM", 3)
+    for j in range(1, NG):
+        a, b = 2 * j, 2 * j + 1
+        i = 10 + j
+        s += c4(j + 1) + ([("SN", i), ("SB", i)] if i < 15 else []) + ([("RG", j + 1, 1)] if ("RG", j + 1, 1) in ON_S else [])
+        s += (ra(4) + [("RA", 10)] if j == 1 else []) + ([("RA", i)] if i < 15 else []) + ([("RA", 15)] if j == 4 else [])
+        s += [("SA", i + 1)] if i + 1 < 15 else []
+        v += f(a, range(4)) + (two("SV", 4) if j == 1 else []) + f(b, VCUT[0]) + ([("RG", j + 1, 1)] if j + 1 < NG and ("RG", j + 1, 1) not in ON_S else []) + qz(j + 1) + rb(j + 3) + f(b, VCUT[1])
+        v += [("SU", 15), ("SV", 15)] if j == 2 else []
+        g += two("P1", j + 2) + ([("RG", j + 1, 0)] if j + 1 < NG else [])
+        g += (two("NM", 4) if j == 1 else []) + ([("NM", 15)] if j == 3 else [])
+    return {"PE": pe, "S": s, "V": v, "G": g, "SP": sp}
+
+
+VCUT = ((0, 1), (2, 3))
 
 
 def tile_attentionalpoolerwmasking_pa_kernel(tc, x, ln_k_w, ln_k_b, Wk, Wv, bk, bv, out_0, out_1):

@@ -12,442 +12,459 @@ ALU = mybir.AluOpType
 ACT = mybir.ActivationFunctionType
 
 P = 128
-C = 1024
+FEATURES = 1024
 EPS = 1e-5
+TILES = 16
+GROUPS = 8
+CHUNK = 512
 FLOPS = 2 * 2048 * 1024 * 2048
-NG = 8
 
-XH_BUFS = 6
-PLAN_BUFS = 3
-OSTV_BUFS = 5
-OSTS_BUFS = 3
-SMALL_ON_S = True
-STAT_V = (0, 1, 2, 3, 4, 5, 6, 7, 8, 9, 15)
-F_ON_S = ()
-ON_V = (("P1", 0), ("P1", 1), ("P1", 2), ("P1", 3))
-ON_G = tuple(("RG", j, 0) for j in range(1, NG))
-ON_S = tuple(("RG", j, 1) for j in (0, 2, 6, 7))
+PSUM_RING = 4
+NORMALISED_BUFS = 6
+PLANES_BUFS = 3
+GROUPED_BUFS = 4
+RESULT_BUFS = 5
+
+STATS_ON_VECTOR = tuple(range(10))
+NORMALISE_ON_VECTOR = tuple(range(4))
+REGROUP_1_ON_SCALAR = (0, 2, 6, 7)
 
 
-def build_queues():
-    t4 = lambda j: [("T", j, g, b) for g in range(2) for b in range(2)] if j < NG else []
-    c4 = lambda j: [("C", j, g, b) for g in range(2) for b in range(2)] if j < NG else []
-    ra = lambda j: [("RA", 2 * j), ("RA", 2 * j + 1)] if j < NG else []
-    rb = lambda j: [("RB", j)] if j < NG else []
-    w4 = lambda k, c: [(k, c, n) for n in range(4)]
-    wq = lambda c: [("WQ", c, 0), ("WQ", c, 1)]
-    qz = lambda j: [("QZ", j, 0), ("QZ", j, 1)] if j < NG else []
-    two = lambda k, j: [(k, 2 * j), (k, 2 * j + 1)] if j < NG else []
-    ss = lambda j: two("SA", j) + two("SN", j) + two("SB", j) + ra(j) if j < NG else []
-    f = lambda i, chs: [("F", i, ch) for ch in chs]
-    pe = [("WT", 0, 0), ("WT", 0, 1), ("VB",), ("WT", 0, 2), ("WT", 0, 3), ("BB", 0)] + t4(0) + w4("WT", 1)
-    pe += [("M", 0, 0), ("M", 1, 0)] + w4("WT", 2) + [("M", 0, 1), ("M", 1, 1)] + t4(1) + w4("WT", 3) + [("BB", 1)]
-    pe += [("M", 0, 2), ("M", 1, 2), ("M", 0, 3), ("M", 1, 3)]
-    for j in range(1, NG):
-        pe += t4(j + 1) + [("M", 2 * j + n, ch) for n in range(2) for ch in range(4)]
-    sp = [("LDX", 0, 0, 1), ("LDX", 0, 1, 1), ("LDW", 0, 0, 2), ("LDW", 0, 2, 2), ("LDX", 1, 0, 2), ("LDW", 1, 0, 4),
-          ("LDX", 2, 0, 2), ("LDW", 2, 0, 4), ("LDW", 3, 0, 4)] + [("LDX", j, 0, 2) for j in range(3, NG)]
-    sp += [("ST", 0, 0), ("ST", 1, 0), ("ST", 0, 1), ("ST", 1, 1)]
-    sp += [("ST", i, h) for i in range(2, 16) for h in range(2)]
-    s = [("LDV",), ("IS",), ("LDB",)] + ra(0) + w4("WE", 0) + [("BC", 0)] + c4(0) + ra(1) + [("RG", 0, 1)]
-    s += w4("WE", 1) + w4("WE", 2) + ra(2) + c4(1) + w4("WE", 3) + [("BC", 1)] + ra(3)
-    s += [("SA", 10), ("SA", 11), ("SN", 10), ("SB", 10)]
-    v = [("IV",)] + two("SU", 0) + two("SV", 0) + two("NM", 0) + rb(0) + [("P1", 0), ("WBC",), ("P1", 1)] + two("SU", 1)
-    v += wq(0) + [("RG", 0, 0)] + two("SV", 1) + [("NM", 2), ("QZ", 0, 0), ("SU", 5), ("QZ", 0, 1), ("SU", 4)] + rb(1)
-    v += [("P1", 2), ("WQ", 1, 0), ("NM", 3), ("WQ", 1, 1), ("P1", 3)] + two("SV", 2) + [("F", 0, 0), ("F", 1, 0)] + wq(2)[0:1] + rb(2) + wq(2)[1:]
-    v += two("SU", 3) + [("F", 0, 1), ("F", 1, 1), ("SV", 6), ("SU", 9), ("SV", 7)] + wq(3) + [("RG", 1, 1), ("F", 0, 2)] + qz(1) + rb(3)
-    v += [("F", 1, 2), ("F", 0, 3), ("F", 1, 3), ("SU", 8)]
-    g = [("IG",)] + two("NM", 2) + two("P1", 2) + [("RG", 1, 0)] + two("NM", 3)
-    for j in range(1, NG):
+def regroup_engine(j, g):
+    if g == 0:
+        return "V" if j == 0 else "G"
+    return "S" if j in REGROUP_1_ON_SCALAR else "V"
+
+
+def engine_queues():
+    def banks(name, j):
+        return [(name, j, g, b) for g in range(2) for b in range(2)] if j < GROUPS else []
+
+    def pair(name, j):
+        return [(name, 2 * j), (name, 2 * j + 1)] if j < GROUPS else []
+
+    def rows(name, c):
+        return [(name, c, n) for n in range(4)]
+
+    def both(name, j):
+        return [(name, j, 0), (name, j, 1)] if j < GROUPS else []
+
+    def recip(j):
+        return [("RB", j)] if j < GROUPS else []
+
+    def regroup(j, g, engine):
+        return [("RG", j, g)] if j < GROUPS and regroup_engine(j, g) == engine else []
+
+    def results(name, i, chunks):
+        return [(name, i, c) for c in chunks]
+
+    sync = [("LDX", 0, 0, 1), ("LDX", 0, 1, 1), ("LDW", 0, 0, 2), ("LDW", 0, 2, 2), ("LDX", 1, 0, 2), ("LDW", 1, 0, 4)]
+    sync += [("LDX", 2, 0, 2), ("LDW", 2, 0, 4), ("LDW", 3, 0, 4)] + [("LDX", j, 0, 2) for j in range(3, GROUPS)]
+    sync += [("ST", 0, 0), ("ST", 1, 0), ("ST", 0, 1), ("ST", 1, 1)]
+    tensor = [("WT", 0, 0), ("WT", 0, 1), ("VB",), ("WT", 0, 2), ("WT", 0, 3), ("BB", 0)] + banks("T", 0) + rows("WT", 1)
+    tensor += [("M", 0, 0), ("M", 1, 0)] + rows("WT", 2) + [("M", 0, 1), ("M", 1, 1)] + banks("T", 1) + rows("WT", 3)
+    tensor += [("BB", 1), ("M", 0, 2), ("M", 1, 2), ("M", 0, 3), ("M", 1, 3)]
+    scalar = [("LDV",), ("IS",), ("LDB",)] + pair("RA", 0) + rows("WE", 0) + [("BC", 0)] + banks("C", 0) + pair("RA", 1)
+    scalar += regroup(0, 1, "S") + rows("WE", 1) + rows("WE", 2) + pair("RA", 2) + banks("C", 1) + rows("WE", 3)
+    scalar += [("BC", 1)] + pair("RA", 3) + [("SA", 10), ("SA", 11), ("SN", 10), ("SB", 10)]
+    vector = [("IV",)] + pair("SU", 0) + pair("SV", 0) + pair("NM", 0) + recip(0) + [("P1", 0), ("WBC",), ("P1", 1)]
+    vector += pair("SU", 1) + both("WQ", 0) + regroup(0, 0, "V") + pair("SV", 1)
+    vector += [("NM", 2), ("QZ", 0, 0), ("SU", 5), ("QZ", 0, 1), ("SU", 4)] + recip(1)
+    vector += [("P1", 2), ("WQ", 1, 0), ("NM", 3), ("WQ", 1, 1), ("P1", 3)] + pair("SV", 2)
+    vector += [("F", 0, 0), ("F", 1, 0), ("WQ", 2, 0)] + recip(2) + [("WQ", 2, 1)] + pair("SU", 3)
+    vector += [("F", 0, 1), ("F", 1, 1), ("SV", 6), ("SU", 9), ("SV", 7)] + both("WQ", 3) + regroup(1, 1, "V")
+    vector += [("F", 0, 2)] + both("QZ", 1) + recip(3) + [("F", 1, 2), ("F", 0, 3), ("F", 1, 3), ("SU", 8)]
+    gpsimd = [("IG",)] + pair("NM", 2) + pair("P1", 2) + regroup(1, 0, "G") + pair("NM", 3)
+
+    for j in range(1, GROUPS):
         a, b = 2 * j, 2 * j + 1
-        i = 10 + j
-        s += c4(j + 1) + ([("SN", i), ("SB", i)] if i < 15 else []) + ([("RG", j + 1, 1)] if ("RG", j + 1, 1) in ON_S else [])
-        s += (ra(4) + [("RA", 10)] if j == 1 else []) + ([("RA", i)] if i < 15 else []) + ([("RA", 15)] if j == 4 else [])
-        s += [("SA", i + 1)] if i + 1 < 15 else []
-        v += f(a, range(4)) + (two("SV", 4) if j == 1 else []) + f(b, VCUT[0]) + ([("RG", j + 1, 1)] if j + 1 < NG and ("RG", j + 1, 1) not in ON_S else []) + qz(j + 1) + rb(j + 3) + f(b, VCUT[1])
-        v += [("SU", 15), ("SV", 15)] if j == 2 else []
-        g += two("P1", j + 2) + ([("RG", j + 1, 0)] if j + 1 < NG else [])
-        g += (two("NM", 4) if j == 1 else []) + ([("NM", 15)] if j == 3 else [])
-    return {"PE": pe, "S": s, "V": v, "G": g, "SP": sp}
+        tensor += banks("T", j + 1) + results("M", a, range(4)) + results("M", b, range(4))
+        second = {1: (11,), 2: (12,), 3: (13,), 4: (14, 15)}.get(j, ())
+        first = {1: (12,), 2: (13,), 3: (14, 15)}.get(j, ())
+        roots = (pair("RA", 4) + [("RA", 10)] if j == 1 else []) + [("RA", i) for i in second]
+        emptied = banks("C", j + 1)
+        scalar += emptied[0:1] + [("SN", i) for i in second] + emptied[1:] + [("SB", i) for i in second]
+        if regroup(j + 1, 1, "S"):
+            scalar += regroup(j + 1, 1, "S") + roots + [("SA", i) for i in first]
+        else:
+            scalar += [("SA", i) for i in first] + roots
+        vector += results("F", a, range(4)) + (pair("SV", 4) if j == 1 else []) + results("F", b, (0, 1))
+        vector += regroup(j + 1, 1, "V") + both("QZ", j + 1) + recip(j + 3) + results("F", b, (2, 3))
+        gpsimd += pair("P1", j + 2) + regroup(j + 1, 0, "G") + (pair("NM", 4) if j == 1 else [])
+        if b < TILES - 1:
+            sync += [("ST", a, 0), ("ST", a, 1), ("ST", b, 0), ("ST", b, 1)]
+        else:
+            sync += [("ST", a, 0), ("ST", a, 1), ("ST", b, 0), ("SH", b, 2), ("SH", b, 3)]
+    return {"SP": sync, "PE": tensor, "S": scalar, "V": vector, "G": gpsimd}
 
 
-VCUT = ((0, 1), (2, 3))
+def text_rules(queues):
+    earlier = {}
+
+    def after(unit, *others):
+        earlier[unit] = earlier.get(unit, []) + [o for o in others]
+
+    load_of_tile = {}
+    load_of_rows = {}
+    for u in queues["SP"]:
+        for n in range(u[2], u[2] + u[3]) if u[0] in ("LDX", "LDW") else ():
+            if u[0] == "LDX":
+                load_of_tile[2 * u[1] + n] = u
+            else:
+                load_of_rows[(u[1], n)] = u
+    after(("IS",), ("IV",))
+    after(("LDV",), ("IV",))
+    after(("LDB",), ("IV",))
+    after(("VB",), ("LDV",), ("IG",))
+    after(("WBC",), ("VB",))
+    for h in range(2):
+        after(("BB", h), ("LDB",))
+        after(("BC", h), ("BB", h))
+    for c in range(4):
+        for n in range(4):
+            after(("WT", c, n), load_of_rows[(c, n)], ("IG",))
+            after(("WE", c, n), ("WT", c, n))
+            if c >= 1:
+                after(("WE", c, n), ("WE", c - 1, 0))
+            if c >= 2:
+                after(("WE", c, n), ("WQ", c - 2, 0), ("WQ", c - 2, 1))
+        for g in range(2):
+            after(("WQ", c, g), *[("WE", c, n) for n in range(4)])
+    for i in range(TILES):
+        j = i // 2
+        if i in STATS_ON_VECTOR:
+            after(("SU", i), load_of_tile[i])
+            after(("SV", i), ("SU", i))
+            after(("NM", i), ("SV", i))
+            after(("RA", i), ("SV", i), ("IS",))
+            after(("P1", i), ("NM", i))
+        else:
+            after(("SA", i), load_of_tile[i], ("IS",))
+            after(("SN", i), ("SA", i))
+            after(("SB", i), ("SN", i))
+            after(("RA", i), ("SB", i))
+        after(("RB", j), ("RA", i))
+        after(("P1", i), ("RB", j))
+        if i >= 1:
+            after(("P1", i), ("P1", i - 1))
+        if i >= NORMALISED_BUFS:
+            after(("P1", i), *[("T", (i - NORMALISED_BUFS) // 2, g, b) for g in range(2) for b in range(2)])
+        for c in range(4):
+            after(("M", i, c), ("QZ", j, 0), ("QZ", j, 1), ("WQ", c, 0), ("WQ", c, 1))
+            after(("F", i, c), ("M", i, c), ("BC", c // 2))
+            after(("SH", i, c), ("F", i, c))
+        for h in range(2):
+            after(("ST", i, h), ("F", i, 2 * h), ("F", i, 2 * h + 1))
+    for j in range(GROUPS):
+        for g in range(2):
+            for b in range(2):
+                after(("T", j, g, b), ("P1", 2 * j), ("P1", 2 * j + 1))
+                after(("C", j, g, b), ("T", j, g, b), ("WBC",))
+                if j >= 1:
+                    after(("C", j, g, b), ("C", j - 1, 0, 0))
+                if j >= PLANES_BUFS:
+                    after(("C", j, g, b), ("RG", j - PLANES_BUFS, 0), ("RG", j - PLANES_BUFS, 1))
+                after(("RG", j, g), ("C", j, g, b))
+            after(("QZ", j, g), ("RG", j, g))
+            if (j, g) != (0, 0):
+                after(("RG", j, g), ("RG", j, 0) if g == 1 else ("RG", j - 1, 1))
+            if j >= GROUPED_BUFS // 2:
+                after(("RG", j, g), ("QZ", j - GROUPED_BUFS // 2, g))
+    empties = {"VB": "WBC", "BB": "BC", "WT": "WE", "T": "C", "M": "F"}
+    rings = {"transposes": [], "sums": []}
+    for u in queues["PE"]:
+        ring = rings["sums" if u[0] == "M" else "transposes"]
+        if len(ring) >= PSUM_RING:
+            after(u, ring[len(ring) - PSUM_RING])
+        ring.append((empties[u[0]],) + u[1:])
+    stores = []
+    for u in queues["V"]:
+        if u[0] == "F" and ("ST", u[1], u[2] // 2) not in stores:
+            if len(stores) >= RESULT_BUFS:
+                after(u, stores[len(stores) - RESULT_BUFS])
+            stores.append(("ST", u[1], u[2] // 2))
+    return earlier
+
+
+def merge_queues(queues, earlier, emit):
+    names = ("SP", "PE", "S", "V", "G")
+    position = {e: 0 for e in names}
+    written = set()
+    total = sum(len(queues[e]) for e in names)
+    while len(written) < total:
+        moved = False
+        for e in names:
+            while position[e] < len(queues[e]):
+                u = queues[e][position[e]]
+                if not all(o in written for o in earlier.get(u, [])):
+                    break
+                emit(u)
+                written.add(u)
+                position[e] += 1
+                moved = True
+        if not moved:
+            raise ValueError("the queues wait for each other")
 
 
 def tile_attentionalpoolerwmasking_pa_kernel(tc, x, ln_k_w, ln_k_b, Wk, Wv, bk, bv, out_0, out_1):
     nc = tc.nc
-    xf = x.flatten_outer_dims()
+    tokens = x.flatten_outer_dims()
     outs = (out_0.flatten_outer_dims(), out_1.flatten_outer_dims())
     with ExitStack() as ctx:
         ctx.enter_context(tc.manual_schedule())
-        const = ctx.enter_context(tc.tile_pool(name="const", bufs=1))
-        xhp = ctx.enter_context(tc.tile_pool(name="xhp", bufs=XH_BUFS))
-        work = ctx.enter_context(tc.tile_pool(name="work", bufs=2))
-        planp = ctx.enter_context(tc.tile_pool(name="planp", bufs=PLAN_BUFS))
-        grpp = ctx.enter_context(tc.tile_pool(name="grpp", bufs=4))
-        ostv = ctx.enter_context(tc.tile_pool(name="ostv", bufs=OSTV_BUFS))
-        osts = ctx.enter_context(tc.tile_pool(name="osts", bufs=OSTS_BUFS))
-        pst = ctx.enter_context(tc.psum_pool(name="pst", bufs=4))
-        pso = ctx.enter_context(tc.psum_pool(name="pso", bufs=4))
+        keep = ctx.enter_context(tc.tile_pool(name="keep", bufs=1))
+        normalised_pool = ctx.enter_context(tc.tile_pool(name="normalised", bufs=NORMALISED_BUFS))
+        alternating = ctx.enter_context(tc.tile_pool(name="alternating", bufs=2))
+        planes_pool = ctx.enter_context(tc.tile_pool(name="planes", bufs=PLANES_BUFS))
+        grouped_pool = ctx.enter_context(tc.tile_pool(name="grouped", bufs=GROUPED_BUFS))
+        result_pool = ctx.enter_context(tc.tile_pool(name="result", bufs=RESULT_BUFS))
+        transposes_psum = ctx.enter_context(tc.psum_pool(name="transposes", bufs=PSUM_RING))
+        sums_psum = ctx.enter_context(tc.psum_pool(name="sums", bufs=PSUM_RING))
 
-        vecs = const.tile([P, 256], BF16, name="vecs")
-        brow = const.tile([P, 2048], BF16, name="brow")
-        ones = const.tile([P, P], BF16, name="ones")
-        zero_t = const.tile([P, 1], F32, name="zero_t")
-        eps_t = const.tile([P, 1], F32, name="eps_t")
-        warm = const.tile([P, 1], F32, name="warm")
-        ident = const.tile([P, P], F32, name="ident")
-        wb = const.tile([P, 16], F32, name="wb")
-        bias_bc = const.tile([P, 2048], BF16, name="bias_bc")
-        xts = [const.tile([P, 2, C], BF16, name="xt%d" % j) for j in range(NG)]
-        wts = [const.tile([P, 4, C], BF16, name="wt%d" % c) for c in range(4)]
-        wq = const.tile([P, 2, 2048], U32, name="wq", align_bytes=64)
-        ws = const.tile([P, 2, 2048], U8, name="ws", align_bytes=64)
-        xq = [const.tile([P, 2, 256], U32, name="xq%d" % j, align_bytes=64) for j in range(NG)]
-        xs = [const.tile([P, 2, 256], U8, name="xs%d" % j, align_bytes=64) for j in range(NG)]
-        mv = [const.tile([P, 2], F32, name="mv%d" % i) for i in range(16)]
-        st6 = [const.tile([P, 2, 6], F32, name="st%d" % i) for i in range(16)]
-        nm = [const.tile([P, 1], F32, name="nm%d" % i) for i in range(16)]
-        sm = [const.tile([P, 1], F32, name="sm%d" % i) for i in range(16)]
-        sq = [const.tile([P, 1], F32, name="sq%d" % i) for i in range(16)]
-        std = [const.tile([P, 2], F32, name="std%d" % j) for j in range(NG)]
-        rstd = [const.tile([P, 2], F32, name="rstd%d" % j) for j in range(NG)]
+        vector_rows = keep.tile([P, 256], BF16, name="vector_rows")
+        bias_rows = keep.tile([P, 2048], BF16, name="bias_rows")
+        ones = keep.tile([P, P], BF16, name="ones")
+        zero = keep.tile([P, 1], F32, name="zero")
+        eps = keep.tile([P, 1], F32, name="eps")
+        warm = keep.tile([P, 1], F32, name="warm")
+        identity = keep.tile([P, P], F32, name="identity")
+        gain_shift = keep.tile([P, 16], F32, name="gain_shift")
+        bias = keep.tile([P, 2048], BF16, name="bias")
+        x_in = [keep.tile([P, 2, FEATURES], BF16, name="x_in%d" % j) for j in range(GROUPS)]
+        w_in = [keep.tile([P, 4, FEATURES], BF16, name="w_in%d" % c) for c in range(4)]
+        w_codes = keep.tile([P, 2, 2048], U32, name="w_codes", align_bytes=64)
+        w_scales = keep.tile([P, 2, 2048], U8, name="w_scales", align_bytes=64)
+        x_codes = [keep.tile([P, 2, 256], U32, name="x_codes%d" % j, align_bytes=64) for j in range(GROUPS)]
+        x_scales = [keep.tile([P, 2, 256], U8, name="x_scales%d" % j, align_bytes=64) for j in range(GROUPS)]
+        chunk_stats = {i: keep.tile([P, 2, 6], F32, name="chunk_stats%d" % i) for i in STATS_ON_VECTOR}
+        mean_var = {i: keep.tile([P, 2], F32, name="mean_var%d" % i) for i in STATS_ON_VECTOR}
+        x_sum = {i: keep.tile([P, 1], F32, name="x_sum%d" % i) for i in range(TILES) if i not in STATS_ON_VECTOR}
+        sq_sum = {i: keep.tile([P, 1], F32, name="sq_sum%d" % i) for i in range(TILES) if i not in STATS_ON_VECTOR}
+        minus_mean = [keep.tile([P, 1], F32, name="minus_mean%d" % i) for i in range(TILES)]
+        std = [keep.tile([P, 2], F32, name="std%d" % j) for j in range(GROUPS)]
+        rstd = [keep.tile([P, 2], F32, name="rstd%d" % j) for j in range(GROUPS)]
         live = {}
 
-        def t_init_v():
-            nc.vector.memset(vecs[:], 0.0)
-            nc.vector.memset(zero_t[:], 0.0)
-            nc.vector.tensor_scalar(out=eps_t[:], in0=zero_t[:], scalar1=EPS, scalar2=None, op0=ALU.add)
-            nc.vector.memset(brow[:], 0.0)
+        def x_tile(i):
+            return x_in[i // 2][:, i % 2, :]
+
+        def constants_vector():
+            nc.vector.memset(vector_rows[:], 0.0)
+            nc.vector.memset(zero[:], 0.0)
+            nc.vector.tensor_scalar(out=eps[:], in0=zero[:], scalar1=EPS, scalar2=None, op0=ALU.add)
+            nc.vector.memset(bias_rows[:], 0.0)
             nc.vector.memset(ones[:], 1.0)
 
-        def t_init_s():
-            nc.scalar.activation(out=warm[:], in_=eps_t[:], func=ACT.Sqrt)
+        def constants_scalar():
+            nc.scalar.activation(out=warm[:], in_=eps[:], func=ACT.Sqrt)
 
-        def t_init_g():
-            make_identity(nc, ident[:])
+        def constants_gpsimd():
+            make_identity(nc, identity[:])
 
-        def t_ldv():
-            q = nc.scalar if SMALL_ON_S else nc.sync
-            q.dma_start(out=vecs[0:4, :], in_=ln_k_w.rearrange("(v q) -> v q", v=4))
-            q.dma_start(out=vecs[4:8, :], in_=ln_k_b.rearrange("(v q) -> v q", v=4))
+        def load_gain_shift():
+            nc.scalar.dma_start(out=vector_rows[0:4, :], in_=ln_k_w.rearrange("(v q) -> v q", v=4))
+            nc.scalar.dma_start(out=vector_rows[4:8, :], in_=ln_k_b.rearrange("(v q) -> v q", v=4))
 
-        def t_ldb():
-            q = nc.scalar if SMALL_ON_S else nc.sync
-            q.dma_start(out=brow[0:1, 0:1024], in_=bk.rearrange("(o d) -> o d", o=1))
-            q.dma_start(out=brow[0:1, 1024:2048], in_=bv.rearrange("(o d) -> o d", o=1))
+        def load_bias():
+            nc.scalar.dma_start(out=bias_rows[0:1, 0:1024], in_=bk.rearrange("(o d) -> o d", o=1))
+            nc.scalar.dma_start(out=bias_rows[0:1, 1024:2048], in_=bv.rearrange("(o d) -> o d", o=1))
 
-        def t_ldx(j, n0, nn):
+        def load_tokens(j, n0, count):
             r0 = P * (2 * j + n0)
             nc.sync.dma_start(
-                out=xts[j][:, n0 : n0 + nn, :], in_=xf[r0 : r0 + P * nn, :].rearrange("(n p) c -> p n c", p=P)
+                out=x_in[j][:, n0 : n0 + count, :],
+                in_=tokens[r0 : r0 + P * count, :].rearrange("(n p) c -> p n c", p=P),
             )
 
-        def t_ldw(c, n0, nn):
-            src = Wk if c < 2 else Wv
-            r0 = 512 * (c % 2) + P * n0
+        def load_weights(c, n0, count):
+            w = Wk if c < 2 else Wv
+            r0 = CHUNK * (c % 2) + P * n0
             nc.sync.dma_start(
-                out=wts[c][:, n0 : n0 + nn, :], in_=src[r0 : r0 + P * nn, :].rearrange("(n p) c -> p n c", p=P)
+                out=w_in[c][:, n0 : n0 + count, :], in_=w[r0 : r0 + P * count, :].rearrange("(n p) c -> p n c", p=P)
             )
 
-        def t_vb():
-            bank = pst.tile([P, 512], F32, tag="tp", name="vb")
-            live[("vb",)] = bank
-            nc.tensor.transpose(bank[:, 0:P], vecs[:].bitcast(F32), ident[:])
+        def transpose_gain_shift():
+            bank = transposes_psum.tile([P, CHUNK], F32, tag="bank", name="vector_bank")
+            live["vector_bank"] = bank
+            nc.tensor.transpose(bank[:, 0:P], vector_rows[:].bitcast(F32), identity[:])
 
-        def t_wbc():
-            nc.vector.tensor_copy(out=wb[:], in_=live[("vb",)][:, 0:8].bitcast(BF16))
+        def keep_gain_shift():
+            nc.vector.tensor_copy(out=gain_shift[:], in_=live["vector_bank"][:, 0:8].bitcast(BF16))
 
-        def t_bb(h):
-            bank = pst.tile([P, 1024], BF16, tag="tp", name="bb")
-            live[("bb", h)] = bank
+        def spread_bias(h):
+            bank = transposes_psum.tile([P, 1024], BF16, tag="bank", name="bias_bank")
+            live[("bias_bank", h)] = bank
             for c in range(2):
-                o = 1024 * h + 512 * c
+                o = 1024 * h + CHUNK * c
                 nc.tensor.matmul(
-                    out=bank[:, 512 * c : 512 * c + 512], lhsT=ones[:], rhs=brow[:, o : o + 512], start=True, stop=True
+                    out=bank[:, CHUNK * c : CHUNK * c + CHUNK], lhsT=ones[:], rhs=bias_rows[:, o : o + CHUNK],
+                    start=True, stop=True,
                 )
 
-        def t_bc(h):
-            dst = bias_bc[:, 1024 * h : 1024 * h + 1024]
-            if ("BC", h) in ON_V:
-                nc.vector.tensor_copy(out=dst, in_=live[("bb", h)][:])
-            else:
-                nc.scalar.copy(out=dst, in_=live[("bb", h)][:])
+        def keep_bias(h):
+            nc.scalar.copy(out=bias[:, 1024 * h : 1024 * h + 1024], in_=live[("bias_bank", h)][:])
 
-        def t_wt(c, n):
-            bank = pst.tile([P, 512], F32, tag="tp", name="wbank")
-            live[("wt", c, n)] = bank
-            w32 = wts[c][:, n, :].bitcast(F32)
+        def transpose_weights(c, n):
+            bank = transposes_psum.tile([P, CHUNK], F32, tag="bank", name="weight_bank")
+            live[("weight_bank", c, n)] = bank
+            words = w_in[c][:, n, :].bitcast(F32)
             for v in range(4):
-                nc.tensor.transpose(bank[:, P * v : P * v + P], w32[:, P * v : P * v + P], ident[:])
+                nc.tensor.transpose(bank[:, P * v : P * v + P], words[:, P * v : P * v + P], identity[:])
 
-        def t_we(c, n):
-            if ("gw", c) not in live:
-                live[("gw", c)] = work.tile([P, 2, 2048], BF16, tag="gw", name="gw", align_bytes=64)
-            gw32 = live[("gw", c)][:].bitcast(F32).rearrange("p g (d u) -> p g d u", u=2)
-            dst = gw32[:, :, P * n : P * n + P, :]
-            src = live[("wt", c, n)][:].rearrange("p (g u d) -> p g d u", g=2, u=2)
-            if ("WE", c, n) in ON_V:
-                nc.vector.tensor_copy(out=dst, in_=src)
-            else:
-                nc.scalar.copy(out=dst, in_=src)
+        def regroup_weights(c, n):
+            if ("weight_pairs", c) not in live:
+                live[("weight_pairs", c)] = alternating.tile(
+                    [P, 2, 2048], BF16, tag="weight_pairs", name="weight_pairs", align_bytes=64
+                )
+            words = live[("weight_pairs", c)][:].bitcast(F32).rearrange("p g (d u) -> p g d u", u=2)
+            nc.scalar.copy(
+                out=words[:, :, P * n : P * n + P, :],
+                in_=live[("weight_bank", c, n)][:].rearrange("p (g u d) -> p g d u", g=2, u=2),
+            )
 
-        def t_wq(c, g):
+        def quantise_weights(c, g):
             nc.vector.quantize_mx(
-                out=wq[:, g, 512 * c : 512 * c + 512].bitcast(FP8X4),
-                scales=ws[:, g, 512 * c : 512 * c + 512],
-                in_=live[("gw", c)][:, g, :],
+                out=w_codes[:, g, CHUNK * c : CHUNK * c + CHUNK].bitcast(FP8X4),
+                scales=w_scales[:, g, CHUNK * c : CHUNK * c + CHUNK],
+                in_=live[("weight_pairs", c)][:, g, :],
             )
 
-        def t_su(i):
+        def stats_vector(i):
             for h in range(2):
-                nc.vector.bn_stats(out=st6[i][:, h, :], in_=xts[i // 2][:, i % 2, 512 * h : 512 * h + 512])
+                nc.vector.bn_stats(out=chunk_stats[i][:, h, :], in_=x_tile(i)[:, 512 * h : 512 * h + 512])
 
-        def t_sv(i):
-            nc.vector.bn_aggr(out=mv[i][:], in_=st6[i][:].rearrange("p a b -> p (a b)"))
+        def mean_var_vector(i):
+            nc.vector.bn_aggr(out=mean_var[i][:], in_=chunk_stats[i][:].rearrange("p a b -> p (a b)"))
 
-        def t_sa(i):
-            junk = work.tile([P, C], BF16, tag="junk", name="junk")
-            nc.scalar.activation(out=junk[:], in_=xts[i // 2][:, i % 2, :], func=ACT.Identity, accum_out=sm[i][:])
-
-        def t_sn(i):
-            nc.scalar.mul(out=nm[i][:], in_=sm[i][:], mul=-1.0 / C)
-
-        def t_sb(i):
-            junk = work.tile([P, C], BF16, tag="junk", name="junk")
-            nc.scalar.activation(
-                out=junk[:], in_=xts[i // 2][:, i % 2, :], func=ACT.Square, bias=nm[i][:], scale=1.0,
-                accum_out=sq[i][:],
+        def negate_mean(i):
+            eng = nc.vector if i in NORMALISE_ON_VECTOR else nc.gpsimd
+            eng.tensor_scalar(
+                out=minus_mean[i][:], in0=mean_var[i][:, 0:1], scalar1=-1.0, scalar2=0.0, op0=ALU.mult, op1=ALU.add
             )
 
-        def t_ra(i):
-            dst = std[i // 2][:, i % 2 : i % 2 + 1]
-            if i in STAT_V:
-                nc.scalar.activation(out=dst, in_=mv[i][:, 1:2], func=ACT.Sqrt, bias=eps_t[:], scale=1.0)
-            else:
-                nc.scalar.activation(out=dst, in_=sq[i][:], func=ACT.Sqrt, bias=eps_t[:], scale=1.0 / C)
+        def sum_scalar(i):
+            unused = alternating.tile([P, FEATURES], BF16, tag="unused", name="unused")
+            nc.scalar.activation(out=unused[:], in_=x_tile(i), func=ACT.Identity, accum_out=x_sum[i][:])
 
-        def t_rb(j):
+        def negate_mean_scalar(i):
+            nc.scalar.mul(out=minus_mean[i][:], in_=x_sum[i][:], mul=-1.0 / FEATURES)
+
+        def squares_scalar(i):
+            unused = alternating.tile([P, FEATURES], BF16, tag="unused", name="unused")
+            nc.scalar.activation(
+                out=unused[:], in_=x_tile(i), func=ACT.Square, bias=minus_mean[i][:], scale=1.0,
+                accum_out=sq_sum[i][:],
+            )
+
+        def root(i):
+            dst = std[i // 2][:, i % 2 : i % 2 + 1]
+            if i in STATS_ON_VECTOR:
+                nc.scalar.activation(out=dst, in_=mean_var[i][:, 1:2], func=ACT.Sqrt, bias=eps[:], scale=1.0)
+            else:
+                nc.scalar.activation(out=dst, in_=sq_sum[i][:], func=ACT.Sqrt, bias=eps[:], scale=1.0 / FEATURES)
+
+        def reciprocal(j):
             nc.vector.reciprocal(out=rstd[j][:], in_=std[j][:])
 
-        def t_nm(i):
-            eng = nc.vector if ("P1", i) in ON_V else nc.gpsimd
-            eng.tensor_scalar(out=nm[i][:], in0=mv[i][:, 0:1], scalar1=-1.0, scalar2=0.0, op0=ALU.mult, op1=ALU.add)
-
-        def t_p1(i):
-            xh = xhp.tile([P, 8, P], F32, tag="xh", name="xh")
-            live[("xh", i)] = xh
-            eng = nc.vector if ("P1", i) in ON_V else nc.gpsimd
+        def normalise(i):
+            normalised = normalised_pool.tile([P, 8, P], F32, tag="normalised", name="normalised")
+            live[("normalised", i)] = normalised
+            eng = nc.vector if i in NORMALISE_ON_VECTOR else nc.gpsimd
             eng.tensor_scalar(
-                out=xh[:].rearrange("p (v e) q -> p v e q", e=2),
-                in0=xts[i // 2][:, i % 2, :].rearrange("p (v q e) -> p v e q", v=4, e=2),
-                scalar1=nm[i][:],
+                out=normalised[:].rearrange("p (v e) q -> p v e q", e=2),
+                in0=x_tile(i).rearrange("p (v q e) -> p v e q", v=4, e=2),
+                scalar1=minus_mean[i][:],
                 scalar2=rstd[i // 2][:, i % 2 : i % 2 + 1],
                 op0=ALU.add,
                 op1=ALU.mult,
             )
 
-        def t_t(j, g, b):
-            bank = pst.tile([P, 512], F32, tag="tp", name="xbank")
-            live[("xb", j, g, b)] = bank
+        def transpose_planes(j, g, b):
+            bank = transposes_psum.tile([P, CHUNK], F32, tag="bank", name="plane_bank")
+            live[("plane_bank", j, g, b)] = bank
             for a in range(2):
-                pl = 4 * g + 2 * b + a
                 for n in range(2):
                     o = 256 * a + P * n
-                    nc.tensor.transpose(bank[:, o : o + P], live[("xh", 2 * j + n)][:, pl, :], ident[:])
+                    nc.tensor.transpose(
+                        bank[:, o : o + P], live[("normalised", 2 * j + n)][:, 4 * g + 2 * b + a, :], identity[:]
+                    )
 
-        def t_c(j, g, b):
-            if ("plan", j) not in live:
-                live[("plan", j)] = planp.tile([P, 8, 256], BF16, tag="plan", name="plan")
-            bank = live[("xb", j, g, b)]
+        def gain_and_shift(j, g, b):
+            if ("planes", j) not in live:
+                live[("planes", j)] = planes_pool.tile([P, 8, 256], BF16, tag="planes", name="planes")
             for a in range(2):
                 pl = 4 * g + 2 * b + a
-                dst = live[("plan", j)][:, pl, :]
-                src = bank[:, 256 * a : 256 * a + 256]
-                if ("C", j, g, b) in ON_V:
-                    nc.vector.tensor_scalar(
-                        out=dst, in0=src, scalar1=wb[:, pl : pl + 1], scalar2=wb[:, 8 + pl : 9 + pl],
-                        op0=ALU.mult, op1=ALU.add,
-                    )
-                else:
-                    nc.scalar.activation(
-                        out=dst, in_=src, func=ACT.Identity, scale=wb[:, pl : pl + 1], bias=wb[:, 8 + pl : 9 + pl]
-                    )
-
-        def t_rg(j, g):
-            grp = grpp.tile([P, 256, 4], BF16, tag="grp", name="grp", align_bytes=64)
-            live[("grp", j, g)] = grp
-            if ("RG", j, g) in ON_G:
-                nc.gpsimd.tensor_scalar(
-                    out=grp[:],
-                    in0=live[("plan", j)][:, 4 * g : 4 * g + 4, :].rearrange("p t r -> p r t"),
-                    scalar1=1.0, scalar2=0.0, op0=ALU.mult, op1=ALU.add,
+                nc.scalar.activation(
+                    out=live[("planes", j)][:, pl, :], in_=live[("plane_bank", j, g, b)][:, 256 * a : 256 * a + 256],
+                    func=ACT.Identity, scale=gain_shift[:, pl : pl + 1], bias=gain_shift[:, 8 + pl : 9 + pl],
                 )
-            elif ("RG", j, g) in ON_S:
-                nc.scalar.copy(
-                    out=grp[:].rearrange("p (c i) t -> p c t i", i=4),
-                    in_=live[("plan", j)][:, 4 * g : 4 * g + 4, :].rearrange("p t (c i) -> p c t i", i=4),
+
+        def regroup_planes(j, g):
+            grouped = grouped_pool.tile([P, 256, 4], BF16, tag="grouped", name="grouped", align_bytes=64)
+            live[("grouped", j, g)] = grouped
+            four = live[("planes", j)][:, 4 * g : 4 * g + 4, :]
+            where = regroup_engine(j, g)
+            if where == "G":
+                nc.gpsimd.tensor_scalar(
+                    out=grouped[:], in0=four.rearrange("p t r -> p r t"), scalar1=1.0, scalar2=0.0,
+                    op0=ALU.mult, op1=ALU.add,
                 )
             else:
-                nc.vector.tensor_copy(
-                    out=grp[:].rearrange("p (c i) t -> p c t i", i=4),
-                    in_=live[("plan", j)][:, 4 * g : 4 * g + 4, :].rearrange("p t (c i) -> p c t i", i=4),
-                )
+                dst = grouped[:].rearrange("p (c i) t -> p c t i", i=4)
+                src = four.rearrange("p t (c i) -> p c t i", i=4)
+                if where == "S":
+                    nc.scalar.copy(out=dst, in_=src)
+                else:
+                    nc.vector.tensor_copy(out=dst, in_=src)
 
-        def t_qz(j, g):
+        def quantise_planes(j, g):
             nc.vector.quantize_mx(
-                out=xq[j][:, g, :].bitcast(FP8X4),
-                scales=xs[j][:, g, :],
-                in_=live[("grp", j, g)][:].rearrange("p r t -> p (r t)"),
+                out=x_codes[j][:, g, :].bitcast(FP8X4),
+                scales=x_scales[j][:, g, :],
+                in_=live[("grouped", j, g)][:].rearrange("p r t -> p (r t)"),
             )
 
-        def t_m(i, ch):
-            acc = pso.tile([P, 512], F32, tag="acc", name="acc")
-            live[("acc", i, ch)] = acc
+        def multiply(i, c):
+            sums = sums_psum.tile([P, CHUNK], F32, tag="sums", name="sums")
+            live[("sums", i, c)] = sums
             j, n = i // 2, i % 2
             for g in range(2):
                 nc.tensor.matmul_mx(
-                    out=acc[:],
-                    lhsT=xq[j][:, g, P * n : P * n + P].bitcast(FP8X4),
-                    lhsT_scale=xs[j][:, g, P * n : P * n + P],
-                    rhs=wq[:, g, 512 * ch : 512 * ch + 512].bitcast(FP8X4),
-                    rhs_scale=ws[:, g, 512 * ch : 512 * ch + 512],
+                    out=sums[:],
+                    lhsT=x_codes[j][:, g, P * n : P * n + P].bitcast(FP8X4),
+                    lhsT_scale=x_scales[j][:, g, P * n : P * n + P],
+                    rhs=w_codes[:, g, CHUNK * c : CHUNK * c + CHUNK].bitcast(FP8X4),
+                    rhs_scale=w_scales[:, g, CHUNK * c : CHUNK * c + CHUNK],
                     start=(g == 0),
                     stop=(g == 1),
                 )
 
-        def t_f(i, ch):
-            half = ch // 2
-            on_s = (i, half) in F_ON_S
-            if ("ost", i, half) not in live:
-                pool = osts if on_s else ostv
-                live[("ost", i, half)] = pool.tile([P, 1024], F32, tag="ost", name="ost")
-            o = live[("ost", i, half)][:, 512 * (ch % 2) : 512 * (ch % 2) + 512]
-            if on_s:
-                nc.scalar.copy(out=o, in_=live[("acc", i, ch)][:])
-            else:
-                nc.vector.tensor_tensor(
-                    out=o, in0=live[("acc", i, ch)][:], in1=bias_bc[:, 512 * ch : 512 * ch + 512], op=ALU.add
-                )
+        def add_bias(i, c):
+            if ("result", i, c // 2) not in live:
+                live[("result", i, c // 2)] = result_pool.tile([P, 1024], F32, tag="result", name="result")
+            o = CHUNK * (c % 2)
+            nc.vector.tensor_tensor(
+                out=live[("result", i, c // 2)][:, o : o + CHUNK], in0=live[("sums", i, c)][:],
+                in1=bias[:, CHUNK * c : CHUNK * c + CHUNK], op=ALU.add,
+            )
 
-        def t_a(i, half):
-            o = live[("ost", i, half)]
-            nc.gpsimd.tensor_tensor(out=o[:], in0=o[:], in1=bias_bc[:, 1024 * half : 1024 * half + 1024], op=ALU.add)
+        def store(i, h):
+            nc.sync.dma_start(out=outs[h][P * i : P * i + P, :], in_=live[("result", i, h)][:])
 
-        def t_st(i, half):
-            nc.sync.dma_start(out=outs[half][P * i : P * i + P, :], in_=live[("ost", i, half)][:])
+        def store_chunk(i, c):
+            o = CHUNK * (c % 2)
+            nc.sync.dma_start(
+                out=outs[c // 2][P * i : P * i + P, o : o + CHUNK], in_=live[("result", i, c // 2)][:, o : o + CHUNK]
+            )
 
-        fn = {"IV": t_init_v, "IS": t_init_s, "IG": t_init_g, "LDV": t_ldv, "LDB": t_ldb, "LDX": t_ldx, "LDW": t_ldw,
-              "VB": t_vb, "WBC": t_wbc, "BB": t_bb, "BC": t_bc, "WT": t_wt, "WE": t_we, "WQ": t_wq, "SU": t_su, "SV": t_sv,
-              "SA": t_sa, "SN": t_sn, "SB": t_sb, "RA": t_ra, "RB": t_rb, "NM": t_nm, "P1": t_p1, "T": t_t, "C": t_c, "RG": t_rg,
-              "QZ": t_qz, "M": t_m, "F": t_f, "A": t_a, "ST": t_st}
-
-        queues = build_queues()
-
-        need = {}
-
-        def after(key, *others):
-            need[key] = need.get(key, []) + [o for o in others]
-
-        ldx_of = {}
-        ldw_of = {}
-        for k in queues["SP"]:
-            if k[0] == "LDX":
-                for n in range(k[2], k[2] + k[3]):
-                    ldx_of[2 * k[1] + n] = k
-            if k[0] == "LDW":
-                for n in range(k[2], k[2] + k[3]):
-                    ldw_of[(k[1], n)] = k
-        after(("IS",), ("IV",))
-        after(("LDV",), ("IV",))
-        after(("LDB",), ("IV",))
-        after(("VB",), ("LDV",), ("IG",))
-        after(("WBC",), ("VB",))
-        for h in range(2):
-            after(("BB", h), ("LDB",))
-            after(("BC", h), ("BB", h))
-        for c in range(4):
-            for n in range(4):
-                after(("WT", c, n), ldw_of[(c, n)], ("IG",))
-                after(("WE", c, n), ("WT", c, n))
-                if c >= 2:
-                    after(("WE", c, n), ("WQ", c - 2, 0), ("WQ", c - 2, 1))
-                if c >= 1:
-                    after(("WE", c, n), ("WE", c - 1, 0))
-            for g in range(2):
-                after(("WQ", c, g), *[("WE", c, n) for n in range(4)])
-        for i in range(16):
-            j = i // 2
-            after(("SU", i), ldx_of[i])
-            after(("SV", i), ("SU", i))
-            after(("SA", i), ldx_of[i], ("IS",))
-            after(("SN", i), ("SA", i))
-            after(("SB", i), ("SN", i))
-            after(("RA", i), ("SV", i) if i in STAT_V else ("SB", i), ("IS",))
-            after(("RB", j), ("RA", i))
-            after(("P1", i), ("RB", j))
-            if i in STAT_V:
-                after(("NM", i), ("SV", i))
-                after(("P1", i), ("NM", i))
-            if i >= 1:
-                after(("P1", i), ("P1", i - 1))
-            if i >= XH_BUFS:
-                after(("P1", i), *[("T", (i - XH_BUFS) // 2, g, b) for g in range(2) for b in range(2)])
-            for ch in range(4):
-                after(("M", i, ch), ("QZ", j, 0), ("QZ", j, 1), ("WQ", ch, 0), ("WQ", ch, 1))
-                after(("F", i, ch), ("M", i, ch), ("BC", ch // 2))
-            for half in range(2):
-                fs = [("F", i, 2 * half), ("F", i, 2 * half + 1)]
-                if (i, half) in F_ON_S:
-                    after(("A", i, half), ("BC", half), *fs)
-                    after(("ST", i, half), ("A", i, half))
-                else:
-                    after(("ST", i, half), *fs)
-        for j in range(NG):
-            for g in range(2):
-                for b in range(2):
-                    after(("T", j, g, b), ("P1", 2 * j), ("P1", 2 * j + 1))
-                    after(("C", j, g, b), ("T", j, g, b), ("WBC",))
-                    if j >= 1:
-                        after(("C", j, g, b), ("C", j - 1, 0, 0))
-                    if j >= PLAN_BUFS:
-                        after(("C", j, g, b), ("RG", j - PLAN_BUFS, 0), ("RG", j - PLAN_BUFS, 1))
-                    after(("RG", j, g), ("C", j, g, b))
-                after(("QZ", j, g), ("RG", j, g))
-                prev = (j, 0) if g == 1 else (j - 1, 1)
-                if prev[0] >= 0:
-                    after(("RG", j, g), ("RG", prev[0], prev[1]))
-                if j >= 2:
-                    after(("RG", j, g), ("QZ", j - 2, g))
-        evac = {"VB": "WBC", "BB": "BC", "WT": "WE", "T": "C", "M": "F"}
-        ring = {"tp": [], "acc": []}
-        for k in queues["PE"]:
-            r = ring["acc" if k[0] == "M" else "tp"]
-            if len(r) >= 4:
-                after(k, r[len(r) - 4])
-            r.append((evac[k[0]],) + k[1:])
-        for eng, bufs in (("V", OSTV_BUFS), ("S", OSTS_BUFS)):
-            r = []
-            for k in queues[eng]:
-                if k[0] == "F" and ("ST", k[1], k[2] // 2) not in r:
-                    if len(r) >= bufs:
-                        after(k, r[len(r) - bufs])
-                    r.append(("ST", k[1], k[2] // 2))
-
-        order = ("SP", "PE", "S", "V", "G")
-        pos = {e: 0 for e in order}
-        done = set()
-        total = sum(len(queues[e]) for e in order)
-        while len(done) < total:
-            moved = False
-            for e in order:
-                while pos[e] < len(queues[e]):
-                    k = queues[e][pos[e]]
-                    if not all(o in done for o in need.get(k, [])):
-                        break
-                    fn[k[0]](*k[1:])
-                    done.add(k)
-                    pos[e] += 1
-                    moved = True
-            if not moved:
-                raise ValueError("queues wait for each other: %s" % str([queues[e][pos[e]] for e in order if pos[e] < len(queues[e])]))
+        units = {
+            "IV": constants_vector, "IS": constants_scalar, "IG": constants_gpsimd, "LDV": load_gain_shift,
+            "LDB": load_bias, "LDX": load_tokens, "LDW": load_weights, "VB": transpose_gain_shift,
+            "WBC": keep_gain_shift, "BB": spread_bias, "BC": keep_bias, "WT": transpose_weights,
+            "WE": regroup_weights, "WQ": quantise_weights, "SU": stats_vector, "SV": mean_var_vector,
+            "NM": negate_mean, "SA": sum_scalar, "SN": negate_mean_scalar, "SB": squares_scalar, "RA": root,
+            "RB": reciprocal, "P1": normalise, "T": transpose_planes, "C": gain_and_shift, "RG": regroup_planes,
+            "QZ": quantise_planes, "M": multiply, "F": add_bias, "ST": store, "SH": store_chunk,
+        }
+        queues = engine_queues()
+        merge_queues(queues, text_rules(queues), lambda u: units[u[0]](*u[1:]))

@@ -28,182 +28,14 @@ RESULT_BUFS = 5
 STATS_ON_VECTOR = tuple(range(10))
 NORMALISE_ON_VECTOR = tuple(range(4))
 REGROUP_1_ON_SCALAR = (0, 2, 6, 7)
+SECOND_PASS = {1: (11,), 2: (12,), 3: (13,), 4: (14, 15)}
+FIRST_PASS = {1: (12,), 2: (13,), 3: (14, 15)}
 
 
 def regroup_engine(j, g):
     if g == 0:
         return "V" if j == 0 else "G"
     return "S" if j in REGROUP_1_ON_SCALAR else "V"
-
-
-def engine_queues():
-    def banks(name, j):
-        return [(name, j, g, b) for g in range(2) for b in range(2)] if j < GROUPS else []
-
-    def pair(name, j):
-        return [(name, 2 * j), (name, 2 * j + 1)] if j < GROUPS else []
-
-    def rows(name, c):
-        return [(name, c, n) for n in range(4)]
-
-    def both(name, j):
-        return [(name, j, 0), (name, j, 1)] if j < GROUPS else []
-
-    def recip(j):
-        return [("RB", j)] if j < GROUPS else []
-
-    def regroup(j, g, engine):
-        return [("RG", j, g)] if j < GROUPS and regroup_engine(j, g) == engine else []
-
-    def results(name, i, chunks):
-        return [(name, i, c) for c in chunks]
-
-    sync = [("LDX", 0, 0, 1), ("LDX", 0, 1, 1), ("LDW", 0, 0, 2), ("LDW", 0, 2, 2), ("LDX", 1, 0, 2), ("LDW", 1, 0, 4)]
-    sync += [("LDX", 2, 0, 2), ("LDW", 2, 0, 4), ("LDW", 3, 0, 4)] + [("LDX", j, 0, 2) for j in range(3, GROUPS)]
-    sync += [("ST", 0, 0), ("ST", 1, 0), ("ST", 0, 1), ("ST", 1, 1)]
-    tensor = [("WT", 0, 0), ("WT", 0, 1), ("VB",), ("WT", 0, 2), ("WT", 0, 3), ("BB", 0)] + banks("T", 0) + rows("WT", 1)
-    tensor += [("M", 0, 0), ("M", 1, 0)] + rows("WT", 2) + [("M", 0, 1), ("M", 1, 1)] + banks("T", 1) + rows("WT", 3)
-    tensor += [("BB", 1), ("M", 0, 2), ("M", 1, 2), ("M", 0, 3), ("M", 1, 3)]
-    scalar = [("LDV",), ("IS",), ("LDB",)] + pair("RA", 0) + rows("WE", 0) + [("BC", 0)] + banks("C", 0) + pair("RA", 1)
-    scalar += regroup(0, 1, "S") + rows("WE", 1) + rows("WE", 2) + pair("RA", 2) + banks("C", 1) + rows("WE", 3)
-    scalar += [("BC", 1)] + pair("RA", 3) + [("SA", 10), ("SA", 11), ("SN", 10), ("SB", 10)]
-    vector = [("IV",)] + pair("SU", 0) + pair("SV", 0) + pair("NM", 0) + recip(0) + [("P1", 0), ("WBC",), ("P1", 1)]
-    vector += pair("SU", 1) + both("WQ", 0) + regroup(0, 0, "V") + pair("SV", 1)
-    vector += [("NM", 2), ("QZ", 0, 0), ("SU", 5), ("QZ", 0, 1), ("SU", 4)] + recip(1)
-    vector += [("P1", 2), ("WQ", 1, 0), ("NM", 3), ("WQ", 1, 1), ("P1", 3)] + pair("SV", 2)
-    vector += [("F", 0, 0), ("F", 1, 0), ("WQ", 2, 0)] + recip(2) + [("WQ", 2, 1)] + pair("SU", 3)
-    vector += [("F", 0, 1), ("F", 1, 1), ("SV", 6), ("SU", 9), ("SV", 7)] + both("WQ", 3) + regroup(1, 1, "V")
-    vector += [("F", 0, 2)] + both("QZ", 1) + recip(3) + [("F", 1, 2), ("F", 0, 3), ("F", 1, 3), ("SU", 8)]
-    gpsimd = [("IG",)] + pair("NM", 2) + pair("P1", 2) + regroup(1, 0, "G") + pair("NM", 3)
-
-    for j in range(1, GROUPS):
-        a, b = 2 * j, 2 * j + 1
-        tensor += banks("T", j + 1) + results("M", a, range(4)) + results("M", b, range(4))
-        second = {1: (11,), 2: (12,), 3: (13,), 4: (14, 15)}.get(j, ())
-        first = {1: (12,), 2: (13,), 3: (14, 15)}.get(j, ())
-        roots = (pair("RA", 4) + [("RA", 10)] if j == 1 else []) + [("RA", i) for i in second]
-        emptied = banks("C", j + 1)
-        scalar += emptied[0:1] + [("SN", i) for i in second] + emptied[1:] + [("SB", i) for i in second]
-        if regroup(j + 1, 1, "S"):
-            scalar += regroup(j + 1, 1, "S") + roots + [("SA", i) for i in first]
-        else:
-            scalar += [("SA", i) for i in first] + roots
-        vector += results("F", a, range(4)) + (pair("SV", 4) if j == 1 else []) + results("F", b, (0, 1))
-        vector += regroup(j + 1, 1, "V") + both("QZ", j + 1) + recip(j + 3) + results("F", b, (2, 3))
-        gpsimd += pair("P1", j + 2) + regroup(j + 1, 0, "G") + (pair("NM", 4) if j == 1 else [])
-        if b < TILES - 1:
-            sync += [("ST", a, 0), ("ST", a, 1), ("ST", b, 0), ("ST", b, 1)]
-        else:
-            sync += [("ST", a, 0), ("ST", a, 1), ("ST", b, 0), ("SH", b, 2), ("SH", b, 3)]
-    return {"SP": sync, "PE": tensor, "S": scalar, "V": vector, "G": gpsimd}
-
-
-def text_rules(queues):
-    earlier = {}
-
-    def after(unit, *others):
-        earlier[unit] = earlier.get(unit, []) + [o for o in others]
-
-    load_of_tile = {}
-    load_of_rows = {}
-    for u in queues["SP"]:
-        for n in range(u[2], u[2] + u[3]) if u[0] in ("LDX", "LDW") else ():
-            if u[0] == "LDX":
-                load_of_tile[2 * u[1] + n] = u
-            else:
-                load_of_rows[(u[1], n)] = u
-    after(("IS",), ("IV",))
-    after(("LDV",), ("IV",))
-    after(("LDB",), ("IV",))
-    after(("VB",), ("LDV",), ("IG",))
-    after(("WBC",), ("VB",))
-    for h in range(2):
-        after(("BB", h), ("LDB",))
-        after(("BC", h), ("BB", h))
-    for c in range(4):
-        for n in range(4):
-            after(("WT", c, n), load_of_rows[(c, n)], ("IG",))
-            after(("WE", c, n), ("WT", c, n))
-            if c >= 1:
-                after(("WE", c, n), ("WE", c - 1, 0))
-            if c >= 2:
-                after(("WE", c, n), ("WQ", c - 2, 0), ("WQ", c - 2, 1))
-        for g in range(2):
-            after(("WQ", c, g), *[("WE", c, n) for n in range(4)])
-    for i in range(TILES):
-        j = i // 2
-        if i in STATS_ON_VECTOR:
-            after(("SU", i), load_of_tile[i])
-            after(("SV", i), ("SU", i))
-            after(("NM", i), ("SV", i))
-            after(("RA", i), ("SV", i), ("IS",))
-            after(("P1", i), ("NM", i))
-        else:
-            after(("SA", i), load_of_tile[i], ("IS",))
-            after(("SN", i), ("SA", i))
-            after(("SB", i), ("SN", i))
-            after(("RA", i), ("SB", i))
-        after(("RB", j), ("RA", i))
-        after(("P1", i), ("RB", j))
-        if i >= 1:
-            after(("P1", i), ("P1", i - 1))
-        if i >= NORMALISED_BUFS:
-            after(("P1", i), *[("T", (i - NORMALISED_BUFS) // 2, g, b) for g in range(2) for b in range(2)])
-        for c in range(4):
-            after(("M", i, c), ("QZ", j, 0), ("QZ", j, 1), ("WQ", c, 0), ("WQ", c, 1))
-            after(("F", i, c), ("M", i, c), ("BC", c // 2))
-            after(("SH", i, c), ("F", i, c))
-        for h in range(2):
-            after(("ST", i, h), ("F", i, 2 * h), ("F", i, 2 * h + 1))
-    for j in range(GROUPS):
-        for g in range(2):
-            for b in range(2):
-                after(("T", j, g, b), ("P1", 2 * j), ("P1", 2 * j + 1))
-                after(("C", j, g, b), ("T", j, g, b), ("WBC",))
-                if j >= 1:
-                    after(("C", j, g, b), ("C", j - 1, 0, 0))
-                if j >= PLANES_BUFS:
-                    after(("C", j, g, b), ("RG", j - PLANES_BUFS, 0), ("RG", j - PLANES_BUFS, 1))
-                after(("RG", j, g), ("C", j, g, b))
-            after(("QZ", j, g), ("RG", j, g))
-            if (j, g) != (0, 0):
-                after(("RG", j, g), ("RG", j, 0) if g == 1 else ("RG", j - 1, 1))
-            if j >= GROUPED_BUFS // 2:
-                after(("RG", j, g), ("QZ", j - GROUPED_BUFS // 2, g))
-    empties = {"VB": "WBC", "BB": "BC", "WT": "WE", "T": "C", "M": "F"}
-    rings = {"transposes": [], "sums": []}
-    for u in queues["PE"]:
-        ring = rings["sums" if u[0] == "M" else "transposes"]
-        if len(ring) >= PSUM_RING:
-            after(u, ring[len(ring) - PSUM_RING])
-        ring.append((empties[u[0]],) + u[1:])
-    stores = []
-    for u in queues["V"]:
-        if u[0] == "F" and ("ST", u[1], u[2] // 2) not in stores:
-            if len(stores) >= RESULT_BUFS:
-                after(u, stores[len(stores) - RESULT_BUFS])
-            stores.append(("ST", u[1], u[2] // 2))
-    return earlier
-
-
-def merge_queues(queues, earlier, emit):
-    names = ("SP", "PE", "S", "V", "G")
-    position = {e: 0 for e in names}
-    written = set()
-    total = sum(len(queues[e]) for e in names)
-    while len(written) < total:
-        moved = False
-        for e in names:
-            while position[e] < len(queues[e]):
-                u = queues[e][position[e]]
-                if not all(o in written for o in earlier.get(u, [])):
-                    break
-                emit(u)
-                written.add(u)
-                position[e] += 1
-                moved = True
-        if not moved:
-            raise ValueError("the queues wait for each other")
 
 
 def tile_attentionalpoolerwmasking_pa_kernel(tc, x, ln_k_w, ln_k_b, Wk, Wv, bk, bv, out_0, out_1):
@@ -457,14 +289,200 @@ def tile_attentionalpoolerwmasking_pa_kernel(tc, x, ln_k_w, ln_k_b, Wk, Wv, bk, 
                 out=outs[c // 2][P * i : P * i + P, o : o + CHUNK], in_=live[("result", i, c // 2)][:, o : o + CHUNK]
             )
 
-        units = {
-            "IV": constants_vector, "IS": constants_scalar, "IG": constants_gpsimd, "LDV": load_gain_shift,
-            "LDB": load_bias, "LDX": load_tokens, "LDW": load_weights, "VB": transpose_gain_shift,
-            "WBC": keep_gain_shift, "BB": spread_bias, "BC": keep_bias, "WT": transpose_weights,
-            "WE": regroup_weights, "WQ": quantise_weights, "SU": stats_vector, "SV": mean_var_vector,
-            "NM": negate_mean, "SA": sum_scalar, "SN": negate_mean_scalar, "SB": squares_scalar, "RA": root,
-            "RB": reciprocal, "P1": normalise, "T": transpose_planes, "C": gain_and_shift, "RG": regroup_planes,
-            "QZ": quantise_planes, "M": multiply, "F": add_bias, "ST": store, "SH": store_chunk,
-        }
-        queues = engine_queues()
-        merge_queues(queues, text_rules(queues), lambda u: units[u[0]](*u[1:]))
+        load_tokens(0, 0, 1)
+        load_tokens(0, 1, 1)
+        load_weights(0, 0, 2)
+        load_weights(0, 2, 2)
+        load_tokens(1, 0, 2)
+        load_weights(1, 0, 4)
+        load_tokens(2, 0, 2)
+        load_weights(2, 0, 4)
+        load_weights(3, 0, 4)
+        for j in range(3, GROUPS):
+            load_tokens(j, 0, 2)
+        constants_vector()
+        constants_gpsimd()
+        load_gain_shift()
+        constants_scalar()
+        load_bias()
+
+        for i in (0, 1):
+            stats_vector(i)
+        for i in (0, 1):
+            mean_var_vector(i)
+        for i in (0, 1):
+            negate_mean(i)
+        for i in (0, 1):
+            root(i)
+        reciprocal(0)
+        normalise(0)
+        for n in (0, 1):
+            transpose_weights(0, n)
+            regroup_weights(0, n)
+        transpose_gain_shift()
+        keep_gain_shift()
+        normalise(1)
+        for n in (2, 3):
+            transpose_weights(0, n)
+            regroup_weights(0, n)
+        spread_bias(0)
+        keep_bias(0)
+        for i in (2, 3):
+            stats_vector(i)
+        for g in range(2):
+            quantise_weights(0, g)
+
+        for g in range(2):
+            for b in range(2):
+                transpose_planes(0, g, b)
+                gain_and_shift(0, g, b)
+        regroup_planes(0, 0)
+        for i in (2, 3):
+            mean_var_vector(i)
+        for i in (2, 3):
+            negate_mean(i)
+            root(i)
+        quantise_planes(0, 0)
+        stats_vector(4)
+        regroup_planes(0, 1)
+        quantise_planes(0, 1)
+        stats_vector(5)
+        for n in range(4):
+            transpose_weights(1, n)
+            regroup_weights(1, n)
+        reciprocal(1)
+        normalise(2)
+        for g in range(2):
+            quantise_weights(1, g)
+        normalise(3)
+        for i in (4, 5):
+            mean_var_vector(i)
+        for i in (4, 5):
+            negate_mean(i)
+
+        for i in (0, 1):
+            multiply(i, 0)
+            add_bias(i, 0)
+        for n in range(4):
+            transpose_weights(2, n)
+            regroup_weights(2, n)
+        for i in (4, 5):
+            root(i)
+        reciprocal(2)
+        for g in range(2):
+            quantise_weights(2, g)
+        for i in (4, 5):
+            normalise(i)
+        for i in (6, 7):
+            stats_vector(i)
+        for i in (0, 1):
+            multiply(i, 1)
+            add_bias(i, 1)
+            store(i, 0)
+        for i in (6, 7):
+            mean_var_vector(i)
+        stats_vector(8)
+        for g in range(2):
+            for b in range(2):
+                transpose_planes(1, g, b)
+                gain_and_shift(1, g, b)
+        regroup_planes(1, 0)
+        for i in (6, 7):
+            negate_mean(i)
+        for n in range(4):
+            transpose_weights(3, n)
+            regroup_weights(3, n)
+        for g in range(2):
+            quantise_weights(3, g)
+        regroup_planes(1, 1)
+        spread_bias(1)
+        keep_bias(1)
+        for i in (6, 7):
+            root(i)
+        for c in (2, 3):
+            for i in (0, 1):
+                multiply(i, c)
+        add_bias(0, 2)
+        for g in range(2):
+            quantise_planes(1, g)
+        reciprocal(3)
+        add_bias(1, 2)
+        for i in (0, 1):
+            add_bias(i, 3)
+            store(i, 1)
+        stats_vector(9)
+        sum_scalar(10)
+        sum_scalar(11)
+        negate_mean_scalar(10)
+        squares_scalar(10)
+
+        for j in range(1, GROUPS):
+            even, odd = 2 * j, 2 * j + 1
+            ahead = j + 1
+            second = SECOND_PASS.get(j, ())
+            first = FIRST_PASS.get(j, ())
+            if ahead < GROUPS:
+                for g in range(2):
+                    for b in range(2):
+                        transpose_planes(ahead, g, b)
+                gain_and_shift(ahead, 0, 0)
+            for i in second:
+                negate_mean_scalar(i)
+            if ahead < GROUPS:
+                gain_and_shift(ahead, 0, 1)
+                gain_and_shift(ahead, 1, 0)
+                gain_and_shift(ahead, 1, 1)
+            for i in second:
+                squares_scalar(i)
+            if j + 2 < GROUPS:
+                normalise(2 * j + 4)
+                normalise(2 * j + 5)
+            if ahead < GROUPS:
+                regroup_planes(ahead, 0)
+                if regroup_engine(ahead, 1) == "S":
+                    regroup_planes(ahead, 1)
+
+            for c in range(4):
+                multiply(even, c)
+            for c in range(4):
+                add_bias(even, c)
+            store(even, 0)
+            store(even, 1)
+            if j == 1:
+                for i in (8, 9):
+                    mean_var_vector(i)
+                for i in (8, 9):
+                    negate_mean(i)
+                    root(i)
+                root(10)
+            if ahead < GROUPS and regroup_engine(ahead, 1) == "S":
+                for i in second:
+                    root(i)
+                for i in first:
+                    sum_scalar(i)
+            else:
+                for i in first:
+                    sum_scalar(i)
+                for i in second:
+                    root(i)
+
+            for c in range(4):
+                multiply(odd, c)
+            add_bias(odd, 0)
+            add_bias(odd, 1)
+            store(odd, 0)
+            if ahead < GROUPS:
+                if regroup_engine(ahead, 1) == "V":
+                    regroup_planes(ahead, 1)
+                quantise_planes(ahead, 0)
+                quantise_planes(ahead, 1)
+            if j + 3 < GROUPS:
+                reciprocal(j + 3)
+            if odd < TILES - 1:
+                add_bias(odd, 2)
+                add_bias(odd, 3)
+                store(odd, 1)
+            else:
+                for c in (2, 3):
+                    add_bias(odd, c)
+                    store_chunk(odd, c)

from contextlib import ExitStack

import concourse.mybir as mybir
from concourse.masks import make_identity

F32 = mybir.dt.float32
BF16 = mybir.dt.bfloat16
U32 = mybir.dt.uint32
U8 = mybir.dt.uint8
FP8X4 = mybir.dt.float8_e4m3fn_x4
ALU = mybir.AluOpType
ACT = mybir.ActivationFunctionType

P = 128
FEATURES = 1024
EPS = 1e-5
TILES = 16
GROUPS = 8
CHUNK = 512
FLOPS = 2 * 2048 * 1024 * 2048

PSUM_RING = 4
NORMALISED_BUFS = 6
PLANES_BUFS = 3
GROUPED_BUFS = 4
RESULT_BUFS = 5

STATS_ON_VECTOR = tuple(range(10))
NORMALISE_ON_VECTOR = tuple(range(4))
REGROUP_1_ON_SCALAR = (0, 2, 6, 7)
SECOND_PASS = {1: (11,), 2: (12,), 3: (13,), 4: (14, 15)}
FIRST_PASS = {1: (12,), 2: (13,), 3: (14, 15)}


def regroup_engine(j, g):
    if g == 0:
        return "V" if j == 0 else "G"
    return "S" if j in REGROUP_1_ON_SCALAR else "V"


def tile_attentionalpoolerwmasking_pa_kernel(tc, x, ln_k_w, ln_k_b, Wk, Wv, bk, bv, out_0, out_1):
    nc = tc.nc
    tokens = x.flatten_outer_dims()
    outs = (out_0.flatten_outer_dims(), out_1.flatten_outer_dims())
    with ExitStack() as ctx:
        ctx.enter_context(tc.manual_schedule())
        keep = ctx.enter_context(tc.tile_pool(name="keep", bufs=1))
        normalised_pool = ctx.enter_context(tc.tile_pool(name="normalised", bufs=NORMALISED_BUFS))
        alternating = ctx.enter_context(tc.tile_pool(name="alternating", bufs=2))
        planes_pool = ctx.enter_context(tc.tile_pool(name="planes", bufs=PLANES_BUFS))
        grouped_pool = ctx.enter_context(tc.tile_pool(name="grouped", bufs=GROUPED_BUFS))
        result_pool = ctx.enter_context(tc.tile_pool(name="result", bufs=RESULT_BUFS))
        transposes_psum = ctx.enter_context(tc.psum_pool(name="transposes", bufs=PSUM_RING))
        sums_psum = ctx.enter_context(tc.psum_pool(name="sums", bufs=PSUM_RING))

        vector_rows = keep.tile([P, 256], BF16, name="vector_rows")
        bias_rows = keep.tile([P, 2048], BF16, name="bias_rows")
        ones = keep.tile([P, P], BF16, name="ones")
        zero = keep.tile([P, 1], F32, name="zero")
        eps = keep.tile([P, 1], F32, name="eps")
        warm = keep.tile([P, 1], F32, name="warm")
        identity = keep.tile([P, P], F32, name="identity")
        gain_shift = keep.tile([P, 16], F32, name="gain_shift")
        bias = keep.tile([P, 2048], BF16, name="bias")
        x_in = [keep.tile([P, 2, FEATURES], BF16, name="x_in%d" % j) for j in range(GROUPS)]
        w_in = [keep.tile([P, 4, FEATURES], BF16, name="w_in%d" % c) for c in range(4)]
        w_codes = keep.tile([P, 2, 2048], U32, name="w_codes", align_bytes=64)
        w_scales = keep.tile([P, 2, 2048], U8, name="w_scales", align_bytes=64)
        x_codes = [keep.tile([P, 2, 256], U32, name="x_codes%d" % j, align_bytes=64) for j in range(GROUPS)]
        x_scales = [keep.tile([P, 2, 256], U8, name="x_scales%d" % j, align_bytes=64) for j in range(GROUPS)]
        chunk_stats = {i: keep.tile([P, 2, 6], F32, name="chunk_stats%d" % i) for i in STATS_ON_VECTOR}
        mean_var = {i: keep.tile([P, 2], F32, name="mean_var%d" % i) for i in STATS_ON_VECTOR}
        x_sum = {i: keep.tile([P, 1], F32, name="x_sum%d" % i) for i in range(TILES) if i not in STATS_ON_VECTOR}
        sq_sum = {i: keep.tile([P, 1], F32, name="sq_sum%d" % i) for i in range(TILES) if i not in STATS_ON_VECTOR}
        minus_mean = [keep.tile([P, 1], F32, name="minus_mean%d" % i) for i in range(TILES)]
        std = [keep.tile([P, 2], F32, name="std%d" % j) for j in range(GROUPS)]
        rstd = [keep.tile([P, 2], F32, name="rstd%d" % j) for j in range(GROUPS)]
        live = {}

        def x_tile(i):
            return x_in[i // 2][:, i % 2, :]

        def constants_vector():
            nc.vector.memset(vector_rows[:], 0.0)
            nc.vector.memset(zero[:], 0.0)
            nc.vector.tensor_scalar(out=eps[:], in0=zero[:], scalar1=EPS, scalar2=None, op0=ALU.add)
            nc.vector.memset(bias_rows[:], 0.0)
            nc.vector.memset(ones[:], 1.0)

        def constants_scalar():
            nc.scalar.activation(out=warm[:], in_=eps[:], func=ACT.Sqrt)

        def constants_gpsimd():
            make_identity(nc, identity[:])

        def load_gain_shift():
            nc.scalar.dma_start(out=vector_rows[0:4, :], in_=ln_k_w.rearrange("(v q) -> v q", v=4))
            nc.scalar.dma_start(out=vector_rows[4:8, :], in_=ln_k_b.rearrange("(v q) -> v q", v=4))

        def load_bias():
            nc.scalar.dma_start(out=bias_rows[0:1, 0:1024], in_=bk.rearrange("(o d) -> o d", o=1))
            nc.scalar.dma_start(out=bias_rows[0:1, 1024:2048], in_=bv.rearrange("(o d) -> o d", o=1))

        def load_tokens(j, n0, count):
            r0 = P * (2 * j + n0)
            nc.sync.dma_start(
                out=x_in[j][:, n0 : n0 + count, :],
                in_=tokens[r0 : r0 + P * count, :].rearrange("(n p) c -> p n c", p=P),
            )

        def load_weights(c, n0, count):
            w = Wk if c < 2 else Wv
            r0 = CHUNK * (c % 2) + P * n0
            nc.sync.dma_start(
                out=w_in[c][:, n0 : n0 + count, :], in_=w[r0 : r0 + P * count, :].rearrange("(n p) c -> p n c", p=P)
            )

        def transpose_gain_shift():
            bank = transposes_psum.tile([P, CHUNK], F32, tag="bank", name="vector_bank")
            live["vector_bank"] = bank
            nc.tensor.transpose(bank[:, 0:P], vector_rows[:].bitcast(F32), identity[:])

        def keep_gain_shift():
            nc.vector.tensor_copy(out=gain_shift[:], in_=live["vector_bank"][:, 0:8].bitcast(BF16))

        def spread_bias(h):
            bank = transposes_psum.tile([P, 1024], BF16, tag="bank", name="bias_bank")
            live[("bias_bank", h)] = bank
            for c in range(2):
                o = 1024 * h + CHUNK * c
                nc.tensor.matmul(
                    out=bank[:, CHUNK * c : CHUNK * c + CHUNK], lhsT=ones[:], rhs=bias_rows[:, o : o + CHUNK],
                    start=True, stop=True,
                )

        def keep_bias(h):
            nc.scalar.copy(out=bias[:, 1024 * h : 1024 * h + 1024], in_=live[("bias_bank", h)][:])

        def transpose_weights(c, n):
            bank = transposes_psum.tile([P, CHUNK], F32, tag="bank", name="weight_bank")
            live[("weight_bank", c, n)] = bank
            words = w_in[c][:, n, :].bitcast(F32)
            for v in range(4):
                nc.tensor.transpose(bank[:, P * v : P * v + P], words[:, P * v : P * v + P], identity[:])

        def regroup_weights(c, n):
            if ("weight_pairs", c) not in live:
                live[("weight_pairs", c)] = alternating.tile(
                    [P, 2, 2048], BF16, tag="weight_pairs", name="weight_pairs", align_bytes=64
                )
            words = live[("weight_pairs", c)][:].bitcast(F32).rearrange("p g (d u) -> p g d u", u=2)
            nc.scalar.copy(
                out=words[:, :, P * n : P * n + P, :],
                in_=live[("weight_bank", c, n)][:].rearrange("p (g u d) -> p g d u", g=2, u=2),
            )

        def quantise_weights(c, g):
            nc.vector.quantize_mx(
                out=w_codes[:, g, CHUNK * c : CHUNK * c + CHUNK].bitcast(FP8X4),
                scales=w_scales[:, g, CHUNK * c : CHUNK * c + CHUNK],
                in_=live[("weight_pairs", c)][:, g, :],
            )

        def stats_vector(i):
            for h in range(2):
                nc.vector.bn_stats(out=chunk_stats[i][:, h, :], in_=x_tile(i)[:, 512 * h : 512 * h + 512])

        def mean_var_vector(i):
            nc.vector.bn_aggr(out=mean_var[i][:], in_=chunk_stats[i][:].rearrange("p a b -> p (a b)"))

        def negate_mean(i):
            eng = nc.vector if i in NORMALISE_ON_VECTOR else nc.gpsimd
            eng.tensor_scalar(
                out=minus_mean[i][:], in0=mean_var[i][:, 0:1], scalar1=-1.0, scalar2=0.0, op0=ALU.mult, op1=ALU.add
            )

        def sum_scalar(i):
            unused = alternating.tile([P, FEATURES], BF16, tag="unused", name="unused")
            nc.scalar.activation(out=unused[:], in_=x_tile(i), func=ACT.Identity, accum_out=x_sum[i][:])

        def negate_mean_scalar(i):
            nc.scalar.mul(out=minus_mean[i][:], in_=x_sum[i][:], mul=-1.0 / FEATURES)

        def squares_scalar(i):
            unused = alternating.tile([P, FEATURES], BF16, tag="unused", name="unused")
            nc.scalar.activation(
                out=unused[:], in_=x_tile(i), func=ACT.Square, bias=minus_mean[i][:], scale=1.0,
                accum_out=sq_sum[i][:],
            )

        def root(i):
            dst = std[i // 2][:, i % 2 : i % 2 + 1]
            if i in STATS_ON_VECTOR:
                nc.scalar.activation(out=dst, in_=mean_var[i][:, 1:2], func=ACT.Sqrt, bias=eps[:], scale=1.0)
            else:
                nc.scalar.activation(out=dst, in_=sq_sum[i][:], func=ACT.Sqrt, bias=eps[:], scale=1.0 / FEATURES)

        def reciprocal(j):
            nc.vector.reciprocal(out=rstd[j][:], in_=std[j][:])

        def normalise(i):
            normalised = normalised_pool.tile([P, 8, P], F32, tag="normalised", name="normalised")
            live[("normalised", i)] = normalised
            eng = nc.vector if i in NORMALISE_ON_VECTOR else nc.gpsimd
            eng.tensor_scalar(
                out=normalised[:].rearrange("p (v e) q -> p v e q", e=2),
                in0=x_tile(i).rearrange("p (v q e) -> p v e q", v=4, e=2),
                scalar1=minus_mean[i][:],
                scalar2=rstd[i // 2][:, i % 2 : i % 2 + 1],
                op0=ALU.add,
                op1=ALU.mult,
            )

        def transpose_planes(j, g, b):
            bank = transposes_psum.tile([P, CHUNK], F32, tag="bank", name="plane_bank")
            live[("plane_bank", j, g, b)] = bank
            for a in range(2):
                for n in range(2):
                    o = 256 * a + P * n
                    nc.tensor.transpose(
                        bank[:, o : o + P], live[("normalised", 2 * j + n)][:, 4 * g + 2 * b + a, :], identity[:]
                    )

        def gain_and_shift(j, g, b):
            if ("planes", j) not in live:
                live[("planes", j)] = planes_pool.tile([P, 8, 256], BF16, tag="planes", name="planes")
            for a in range(2):
                pl = 4 * g + 2 * b + a
                nc.scalar.activation(
                    out=live[("planes", j)][:, pl, :], in_=live[("plane_bank", j, g, b)][:, 256 * a : 256 * a + 256],
                    func=ACT.Identity, scale=gain_shift[:, pl : pl + 1], bias=gain_shift[:, 8 + pl : 9 + pl],
                )

        def regroup_planes(j, g):
            grouped = grouped_pool.tile([P, 256, 4], BF16, tag="grouped", name="grouped", align_bytes=64)
            live[("grouped", j, g)] = grouped
            four = live[("planes", j)][:, 4 * g : 4 * g + 4, :]
            where = regroup_engine(j, g)
            if where == "G":
                nc.gpsimd.tensor_scalar(
                    out=grouped[:], in0=four.rearrange("p t r -> p r t"), scalar1=1.0, scalar2=0.0,
                    op0=ALU.mult, op1=ALU.add,
                )
            else:
                dst = grouped[:].rearrange("p (c i) t -> p c t i", i=4)
                src = four.rearrange("p t (c i) -> p c t i", i=4)
                if where == "S":
                    nc.scalar.copy(out=dst, in_=src)
                else:
                    nc.vector.tensor_copy(out=dst, in_=src)

        def quantise_planes(j, g):
            nc.vector.quantize_mx(
                out=x_codes[j][:, g, :].bitcast(FP8X4),
                scales=x_scales[j][:, g, :],
                in_=live[("grouped", j, g)][:].rearrange("p r t -> p (r t)"),
            )

        def multiply(i, c):
            sums = sums_psum.tile([P, CHUNK], F32, tag="sums", name="sums")
            live[("sums", i, c)] = sums
            j, n = i // 2, i % 2
            for g in range(2):
                nc.tensor.matmul_mx(
                    out=sums[:],
                    lhsT=x_codes[j][:, g, P * n : P * n + P].bitcast(FP8X4),
                    lhsT_scale=x_scales[j][:, g, P * n : P * n + P],
                    rhs=w_codes[:, g, CHUNK * c : CHUNK * c + CHUNK].bitcast(FP8X4),
                    rhs_scale=w_scales[:, g, CHUNK * c : CHUNK * c + CHUNK],
                    start=(g == 0),
                    stop=(g == 1),
                )

        def add_bias(i, c):
            if ("result", i, c // 2) not in live:
                live[("result", i, c // 2)] = result_pool.tile([P, 1024], F32, tag="result", name="result")
            o = CHUNK * (c % 2)
            nc.vector.tensor_tensor(
                out=live[("result", i, c // 2)][:, o : o + CHUNK], in0=live[("sums", i, c)][:],
                in1=bias[:, CHUNK * c : CHUNK * c + CHUNK], op=ALU.add,
            )

        def store(i, h):
            nc.sync.dma_start(out=outs[h][P * i : P * i + P, :], in_=live[("result", i, h)][:])

        def store_chunk(i, c):
            o = CHUNK * (c % 2)
            nc.sync.dma_start(
                out=outs[c // 2][P * i : P * i + P, o : o + CHUNK], in_=live[("result", i, c // 2)][:, o : o + CHUNK]
            )

        load_tokens(0, 0, 1)
        load_tokens(0, 1, 1)
        load_weights(0, 0, 2)
        load_weights(0, 2, 2)
        load_tokens(1, 0, 2)
        load_weights(1, 0, 4)
        load_tokens(2, 0, 2)
        load_weights(2, 0, 4)
        load_weights(3, 0, 4)
        for j in range(3, GROUPS):
            load_tokens(j, 0, 2)
        constants_vector()
        constants_gpsimd()
        load_gain_shift()
        constants_scalar()
        load_bias()

        for i in (0, 1):
            stats_vector(i)
        for i in (0, 1):
            mean_var_vector(i)
        for i in (0, 1):
            negate_mean(i)
        for i in (0, 1):
            root(i)
        reciprocal(0)
        normalise(0)
        for n in (0, 1):
            transpose_weights(0, n)
            regroup_weights(0, n)
        transpose_gain_shift()
        keep_gain_shift()
        normalise(1)
        for n in (2, 3):
            transpose_weights(0, n)
            regroup_weights(0, n)
        spread_bias(0)
        keep_bias(0)
        for i in (2, 3):
            stats_vector(i)
        for g in range(2):
            quantise_weights(0, g)

        for g in range(2):
            for b in range(2):
                transpose_planes(0, g, b)
                gain_and_shift(0, g, b)
        regroup_planes(0, 0)
        for i in (2, 3):
            mean_var_vector(i)
        for i in (2, 3):
            negate_mean(i)
            root(i)
        quantise_planes(0, 0)
        stats_vector(4)
        regroup_planes(0, 1)
        quantise_planes(0, 1)
        stats_vector(5)
        for n in range(4):
            transpose_weights(1, n)
            regroup_weights(1, n)
        reciprocal(1)
        normalise(2)
        for g in range(2):
            quantise_weights(1, g)
        normalise(3)
        for i in (4, 5):
            mean_var_vector(i)
        for i in (4, 5):
            negate_mean(i)

        for i in (0, 1):
            multiply(i, 0)
            add_bias(i, 0)
        for n in range(4):
            transpose_weights(2, n)
            regroup_weights(2, n)
        for i in (4, 5):
            root(i)
        reciprocal(2)
        for g in range(2):
            quantise_weights(2, g)
        for i in (4, 5):
            normalise(i)
        for i in (6, 7):
            stats_vector(i)
        for i in (0, 1):
            multiply(i, 1)
            add_bias(i, 1)
            store(i, 0)
        for i in (6, 7):
            mean_var_vector(i)
        stats_vector(8)
        for g in range(2):
            for b in range(2):
                transpose_planes(1, g, b)
                gain_and_shift(1, g, b)
        regroup_planes(1, 0)
        for i in (6, 7):
            negate_mean(i)
        for n in range(4):
            transpose_weights(3, n)
            regroup_weights(3, n)
        for g in range(2):
            quantise_weights(3, g)
        regroup_planes(1, 1)
        spread_bias(1)
        keep_bias(1)
        for i in (6, 7):
            root(i)
        for c in (2, 3):
            for i in (0, 1):
                multiply(i, c)
        add_bias(0, 2)
        for g in range(2):
            quantise_planes(1, g)
        reciprocal(3)
        add_bias(1, 2)
        for i in (0, 1):
            add_bias(i, 3)
            store(i, 1)
        stats_vector(9)
        sum_scalar(10)
        sum_scalar(11)
        negate_mean_scalar(10)
        squares_scalar(10)

        for j in range(1, GROUPS):
            even, odd = 2 * j, 2 * j + 1
            ahead = j + 1
            second = SECOND_PASS.get(j, ())
            first = FIRST_PASS.get(j, ())
            if ahead < GROUPS:
                for g in range(2):
                    for b in range(2):
                        transpose_planes(ahead, g, b)
                gain_and_shift(ahead, 0, 0)
            for i in second:
                negate_mean_scalar(i)
            if ahead < GROUPS:
                gain_and_shift(ahead, 0, 1)
                gain_and_shift(ahead, 1, 0)
                gain_and_shift(ahead, 1, 1)
            for i in second:
                squares_scalar(i)
            if j + 2 < GROUPS:
                normalise(2 * j + 4)
                normalise(2 * j + 5)
            if ahead < GROUPS:
                regroup_planes(ahead, 0)
                if regroup_engine(ahead, 1) == "S":
                    regroup_planes(ahead, 1)

            for c in range(4):
                multiply(even, c)
            for c in range(4):
                add_bias(even, c)
            store(even, 0)
            store(even, 1)
            if j == 1:
                for i in (8, 9):
                    mean_var_vector(i)
                for i in (8, 9):
                    negate_mean(i)
                    root(i)
                root(10)
            if ahead < GROUPS and regroup_engine(ahead, 1) == "S":
                for i in second:
                    root(i)
                for i in first:
                    sum_scalar(i)
            else:
                for i in first:
                    sum_scalar(i)
                for i in second:
                    root(i)

            for c in range(4):
                multiply(odd, c)
            add_bias(odd, 0)
            add_bias(odd, 1)
            store(odd, 0)
            if ahead < GROUPS:
                if regroup_engine(ahead, 1) == "V":
                    regroup_planes(ahead, 1)
                quantise_planes(ahead, 0)
                quantise_planes(ahead, 1)
            if j + 3 < GROUPS:
                reciprocal(j + 3)
            if odd < TILES - 1:
                add_bias(odd, 2)
                add_bias(odd, 3)
                store(odd, 1)
            else:
                for c in (2, 3):
                    add_bias(odd, c)
                    store_chunk(odd, c)
